import numpy as np
import ml_dtypes


def mxq(x, axis, fmt="e4m3"):
    dtype, down = {"e4m3": (ml_dtypes.float8_e4m3fn, 7), "e5m2": (ml_dtypes.float8_e5m2, 14)}[fmt]
    v = np.moveaxis(np.asarray(x, np.float32).astype(ml_dtypes.bfloat16).astype(np.float64), axis, -1)
    blocks = v.reshape(v.shape[:-1] + (-1, 32))
    amax = np.abs(blocks).max(-1, keepdims=True)
    byte = np.maximum(np.where(amax > 0, np.frexp(amax)[1] - 1 + 127, 0) - down, 1)
    scale = np.exp2(byte - 127.0)
    codes = (blocks / scale).astype(np.float32).astype(dtype).astype(np.float64)
    return np.moveaxis((codes * scale).reshape(v.shape), -1, axis)


WIDE = False


def mx_kscale(k):
    if not WIDE:
        return np.ones(k)
    levels = np.array([10, -10, 5, -5, 0])
    a = np.random.permutation(np.resize(levels, k // 512 * 4)).reshape(k // 512, 4)
    idx = np.arange(k)
    return np.exp2(a[idx // 512, idx % 128 // 32])


BF16 = ml_dtypes.bfloat16


def bf(x):
    return np.asarray(x, np.float32).astype(BF16)


def f64(x):
    return np.asarray(x).astype(np.float64)


B, I, O, NUM, KO = 384, 1024, 1024, 8, 3
G = NUM + KO


def silu(v):
    e = np.exp(-np.abs(v))
    return v * np.where(v >= 0, 1.0, e) / (1.0 + e)


def extend_grid(grid, k):
    h = (grid[:, -1:] - grid[:, :1]) / (grid.shape[1] - 1)
    for _ in range(k):
        grid = np.concatenate([grid[:, :1] - h, grid, grid[:, -1:] + h], axis=1)
    return grid


def b_batch(x, grid, k):
    xg = x[:, :, None]
    g = grid[None, :, :]
    value = ((xg >= g[:, :, :-1]) & (xg < g[:, :, 1:])).astype(np.float64)
    for p in range(1, k + 1):
        value = (xg - g[:, :, :-(p + 1)]) / (g[:, :, p:-1] - g[:, :, :-(p + 1)]) * value[:, :, :-1] \
              + (g[:, :, p + 1:] - xg) / (g[:, :, p + 1:] - g[:, :, 1:-p]) * value[:, :, 1:]
        value = np.nan_to_num(value)
    return value


def setup_inputs():
    s = mx_kscale(I)
    x = np.random.uniform(-1.0, 1.0, (B, I))
    lo = -1.0 - 0.2 * np.random.random((I, 1))
    hi = 1.0 + 0.2 * np.random.random((I, 1))
    base_grid = lo + (hi - lo) * np.linspace(0.0, 1.0, NUM + 1)[None, :]
    grid = extend_grid(base_grid, KO)
    return {"x": bf(x * s),
            "grid": bf(grid * s[:, None]),
            "coef": bf(np.random.standard_normal((I, O, G))),
            "scale_base": bf(np.random.standard_normal((I, O)) * 2.0 / np.sqrt(I) / s[:, None]),
            "scale_sp": bf((1.0 + 0.1 * np.random.standard_normal((I, O))) / np.sqrt(I)),
            "mask": bf(1.0 + 0.1 * np.random.standard_normal((I, O)))}


def reference(x, grid, coef, scale_base, scale_sp, mask):
    x, grid, coef = f64(x), f64(grid), f64(coef)
    scale_base, scale_sp, mask = f64(scale_base), f64(scale_sp), f64(mask)
    base = silu(x)
    bs = b_batch(x, grid, KO)
    ws = coef * (mask * scale_sp)[:, :, None]
    out_spline = (mxq(bs.transpose(2, 0, 1), 2, "e4m3") @ mxq(ws.transpose(2, 0, 1), 1, "e4m3")).sum(0)
    out_base = mxq(base, 1, "e4m3") @ mxq(mask * scale_base, 0, "e4m3")
    return out_base + out_spline

@@ -1,0 +1,200 @@
+from contextlib import ExitStack
+
+import concourse.bass as bass
+import concourse.mybir as mybir
+import concourse.tile as tile
+from concourse.masks import make_identity
+
+F32 = mybir.dt.float32
+BF16 = mybir.dt.bfloat16
+U32 = mybir.dt.uint32
+U8 = mybir.dt.uint8
+FP8X4 = mybir.dt.float8_e4m3fn_x4
+ALU = mybir.AluOpType
+ACTF = mybir.ActivationFunctionType
+
+P = 128
+B = 384
+I = 1024
+O = 1024
+G = 11
+NK = 15
+NQ = I // P
+NM = B // P
+NPL = G + 1
+OB = 128
+NOB = O // OB
+PW = NPL * B
+
+FLOPS = 2 * B * I * O * NPL
+
+
+def tile_kan_layer_kernel(tc, x, grid, coef, scale_base, scale_sp, mask, out):
+    nc = tc.nc
+    coef_v = coef.rearrange("(q p) o g -> p q (o g)", p=P)
+    mask_v = mask.rearrange("(q p) o -> p q o", p=P)
+    sp_v = scale_sp.rearrange("(q p) o -> p q o", p=P)
+    sb_v = scale_base.rearrange("(q p) o -> p q o", p=P)
+    out_v = out.rearrange("(m p) o -> p m o", p=P)
+
+    with ExitStack() as ctx:
+        const = ctx.enter_context(tc.tile_pool(name="const", bufs=1))
+        psum = ctx.enter_context(tc.psum_pool(name="psum", bufs=2))
+
+        ident = const.tile([P, P], BF16)
+        make_identity(nc, ident[:])
+        g_bf = const.tile([P, NQ, 16], BF16)
+        nc.sync.dma_start(out=g_bf[:, :, 0:NK], in_=grid.rearrange("(q p) r -> p q r", p=P))
+        t_sb = const.tile([P, NQ, B], BF16)
+        bs_codes = const.tile([P, 2, PW], U32, align_bytes=64)
+        bs_scales = const.tile([P, 2, PW], U8, align_bytes=64)
+        accs = const.tile([P, NM, O], F32)
+
+        gf = const.tile([P, NQ, 16], F32)
+        negg = const.tile([P, NQ, 16], F32)
+        d1 = const.tile([P, NQ, 16], F32)
+        d2 = const.tile([P, NQ, 16], F32)
+        d3 = const.tile([P, NQ, 16], F32)
+        d4 = const.tile([P, NQ, 16], F32)
+        ca = const.tile([P, NQ, 16], F32)
+        cc = const.tile([P, NQ, 16], F32)
+        r1 = const.tile([P, NQ, 16], F32)
+        negk = const.tile([P, NQ, 16], F32)
+        negl = const.tile([P, NQ, 16], F32)
+        nc.vector.tensor_copy(out=gf[:, :, 0:NK], in_=g_bf[:, :, 0:NK])
+        nc.vector.tensor_scalar(out=negg[:, :, 0:NK], in0=gf[:, :, 0:NK], scalar1=-1.0, scalar2=None, op0=ALU.mult)
+        nc.vector.tensor_tensor(out=d1[:, :, 0:14], in0=gf[:, :, 1:15], in1=gf[:, :, 0:14], op=ALU.subtract)
+        nc.vector.tensor_tensor(out=d2[:, :, 0:13], in0=gf[:, :, 2:15], in1=gf[:, :, 0:13], op=ALU.subtract)
+        nc.vector.tensor_tensor(out=d3[:, :, 0:12], in0=gf[:, :, 3:15], in1=gf[:, :, 0:12], op=ALU.subtract)
+        nc.vector.tensor_tensor(out=d4[:, :, 0:11], in0=gf[:, :, 4:15], in1=gf[:, :, 0:11], op=ALU.subtract)
+        nc.vector.tensor_tensor(out=ca[:, :, 0:12], in0=d1[:, :, 0:12], in1=d2[:, :, 0:12], op=ALU.mult)
+        nc.vector.tensor_tensor(out=ca[:, :, 0:12], in0=ca[:, :, 0:12], in1=d3[:, :, 0:12], op=ALU.mult)
+        nc.vector.reciprocal(out=ca[:, :, 0:12], in_=ca[:, :, 0:12])
+        nc.vector.tensor_tensor(out=cc[:, :, 0:12], in0=d3[:, :, 0:12], in1=d2[:, :, 1:13], op=ALU.mult)
+        nc.vector.scalar_tensor_tensor(out=cc[:, :, 0:12], in0=cc[:, :, 0:12], scalar=-1.0, in1=d1[:, :, 2:14],
+                                       op0=ALU.mult, op1=ALU.mult)
+        nc.vector.reciprocal(out=cc[:, :, 0:12], in_=cc[:, :, 0:12])
+        nc.vector.reciprocal(out=r1[:, :, 0:14], in_=d1[:, :, 0:14])
+        nc.vector.scalar_tensor_tensor(out=negk[:, :, 0:11], in0=d4[:, :, 0:11], scalar=-1.0, in1=r1[:, :, 0:11],
+                                       op0=ALU.mult, op1=ALU.mult)
+        nc.vector.scalar_tensor_tensor(out=negl[:, :, 0:11], in0=d4[:, :, 0:11], scalar=-1.0, in1=r1[:, :, 3:14],
+                                       op0=ALU.mult, op1=ALU.mult)
+
+        bas = ctx.enter_context(tc.tile_pool(name="bas", bufs=3))
+        big = ctx.enter_context(tc.tile_pool(name="big", bufs=1))
+        wts = ctx.enter_context(tc.tile_pool(name="wts", bufs=2))
+
+        x_sb = big.tile([P, NM, I], BF16)
+        nc.sync.dma_start(out=x_sb[:], in_=x.rearrange("(m p) i -> p m i", p=P))
+
+        state = {}
+
+        def basis_group(q):
+            c, tt = divmod(q, 4)
+            if tt == 0:
+                mx4 = big.tile([P, 4, PW], BF16)
+                state["mx4"] = mx4
+            mx4 = state["mx4"]
+            tp = psum.tile([P, B], BF16, tag="tp")
+            for m in range(NM):
+                nc.tensor.transpose(out=tp[:, m * P:(m + 1) * P], in_=x_sb[:, m, q * P:(q + 1) * P], identity=ident[:])
+            tq = t_sb[:, q, :]
+            nc.scalar.activation(out=mx4[:, tt, G * B:NPL * B], in_=tp[:], func=ACTF.Silu)
+            nc.vector.tensor_scalar(out=tq, in0=tp[:], scalar1=gf[:, q, 0:1], scalar2=gf[:, q, 14:15],
+                                    op0=ALU.max, op1=ALU.min)
+            lt = big.tile([P, G, B], BF16, tag="lt")
+            rt = big.tile([P, G, B], BF16, tag="rt")
+            pp = {}
+            qq = {}
+            for r in range(NK):
+                sq = bas.tile([P, B], F32, tag="sq")
+                nc.scalar.activation(out=sq[:], in_=tq, func=ACTF.Square, bias=negg[:, q, r:r + 1], scale=1.0)
+                cu = bas.tile([P, B], F32, tag="cu")
+                nc.vector.scalar_tensor_tensor(out=cu[:], in0=tq, scalar=gf[:, q, r:r + 1], in1=sq[:],
+                                               op0=ALU.subtract, op1=ALU.mult)
+                if r <= 11:
+                    pt = bas.tile([P, B], F32, tag="pt", bufs=4)
+                    nc.scalar.activation(out=pt[:], in_=cu[:], func=ACTF.Relu, scale=ca[:, q, r:r + 1])
+                    pp[r] = pt
+                if r >= 3:
+                    qt = bas.tile([P, B], F32, tag="qt", bufs=4)
+                    nc.scalar.activation(out=qt[:], in_=cu[:], func=ACTF.Relu, scale=cc[:, q, r - 3:r - 2])
+                    qq[r] = qt
+                if 1 <= r <= 11:
+                    nc.vector.scalar_tensor_tensor(out=lt[:, r - 1, :], in0=pp[r][:], scalar=negk[:, q, r - 1:r],
+                                                   in1=pp[r - 1][:], op0=ALU.mult, op1=ALU.add)
+                if r >= 4:
+                    nc.vector.scalar_tensor_tensor(out=rt[:, r - 4, :], in0=qq[r - 1][:], scalar=negl[:, q, r - 4:r - 3],
+                                                   in1=qq[r][:], op0=ALU.mult, op1=ALU.add)
+            nc.vector.tensor_tensor(out=mx4[:, tt, 0:G * B], in0=lt[:].rearrange("p j b -> p (j b)"),
+                                    in1=rt[:].rearrange("p j b -> p (j b)"), op=ALU.max)
+            if tt == 3:
+                w0 = 0
+                while w0 < PW:
+                    wn = min(1024, PW - w0)
+                    gb = bas.tile([P, 1024, 4], BF16, tag="gb", bufs=2, align_bytes=64)
+                    nc.scalar.copy(out=gb[:, 0:wn, :], in_=mx4[:, :, w0:w0 + wn].rearrange("p t w -> p w t"))
+                    nc.vector.quantize_mx(out=bs_codes[:, c, w0:w0 + wn].bitcast(FP8X4),
+                                          scales=bs_scales[:, c, w0:w0 + wn],
+                                          in_=gb[:, 0:wn, :].rearrange("p w t -> p (w t)"))
+                    w0 += wn
+
+        def weight_chunk(c, ob):
+            osl = slice(ob * OB, (ob + 1) * OB)
+            qsl = slice(4 * c, 4 * c + 4)
+            ct = wts.tile([P, 4, OB * G], BF16, tag="ct", bufs=3)
+            nc.sync.dma_start(out=ct[:], in_=coef_v[:, qsl, ob * OB * G:(ob + 1) * OB * G])
+            mk = wts.tile([P, 4, OB], BF16, tag="mk")
+            nc.sync.dma_start(out=mk[:], in_=mask_v[:, qsl, osl])
+            sps = wts.tile([P, 4, OB], BF16, tag="sps")
+            nc.sync.dma_start(out=sps[:], in_=sp_v[:, qsl, osl])
+            sbs = wts.tile([P, 4, OB], BF16, tag="sbs")
+            nc.sync.dma_start(out=sbs[:], in_=sb_v[:, qsl, osl])
+            ms = wts.tile([P, 4, OB], F32, tag="ms")
+            nc.vector.tensor_tensor(out=ms[:], in0=mk[:], in1=sps[:], op=ALU.mult)
+            acc = []
+            for m in range(NM):
+                am = psum.tile([P, OB], F32, tag="acc%d" % m)
+                acc.append(am)
+            ct_v = ct[:].rearrange("p t (o g) -> p g o t", g=G)
+            ms_v = ms[:].rearrange("p t o -> p o t").unsqueeze(1)
+            for k in range(3):
+                g0 = 4 * k
+                ng = min(4, G - g0)
+                gw = wts.tile([P, 4, OB, 4], BF16, tag="gw", bufs=3, align_bytes=64)
+                nc.vector.tensor_tensor(out=gw[:, 0:ng, :, :], in0=ct_v[:, g0:g0 + ng, :, :],
+                                        in1=ms_v.to_broadcast([P, ng, OB, 4]), op=ALU.mult)
+                if ng < 4:
+                    nc.vector.tensor_tensor(out=gw[:, 3, :, :], in0=mk[:].rearrange("p t o -> p o t"),
+                                            in1=sbs[:].rearrange("p t o -> p o t"), op=ALU.mult)
+                wc = wts.tile([P, 4 * OB], U32, tag="wc", bufs=4, align_bytes=64)
+                ws = wts.tile([P, 4 * OB], U8, tag="ws", bufs=4, align_bytes=64)
+                nc.vector.quantize_mx(out=wc[:].bitcast(FP8X4), scales=ws[:],
+                                      in_=gw[:].rearrange("p g o t -> p (g o t)"))
+                for gi in range(4):
+                    pl = g0 + gi
+                    for m in range(NM):
+                        l0 = pl * B + m * P
+                        nc.tensor.matmul_mx(out=acc[m][:],
+                                            lhsT=bs_codes[:, c, l0:l0 + P].bitcast(FP8X4),
+                                            lhsT_scale=bs_scales[:, c, l0:l0 + P],
+                                            rhs=wc[:, gi * OB:(gi + 1) * OB].bitcast(FP8X4),
+                                            rhs_scale=ws[:, gi * OB:(gi + 1) * OB],
+                                            start=(pl == 0), stop=(pl == NPL - 1))
+            if c == 0:
+                for m in range(NM):
+                    nc.scalar.copy(out=accs[:, m, osl], in_=acc[m][:])
+            else:
+                ot = wts.tile([P, NM, OB], F32, tag="ot")
+                for m in range(NM):
+                    nc.vector.tensor_tensor(out=ot[:, m, :], in0=acc[m][:], in1=accs[:, m, osl], op=ALU.add)
+                nc.sync.dma_start(out=out_v[:, :, osl], in_=ot[:])
+
+        for q in range(4):
+            basis_group(q)
+        for i in range(4):
+            weight_chunk(0, 2 * i)
+            weight_chunk(0, 2 * i + 1)
+            basis_group(4 + i)
+        for ob in range(NOB):
+            weight_chunk(1, ob)

@@ -150,20 +150,22 @@ def tile_kan_layer_kernel(tc, x, grid, coef, scale_base, scale_sp, mask, out):
             nc.sync.dma_start(out=sps[:], in_=sp_v[:, qsl, osl])
             sbs = wts.tile([P, 4, OB], BF16, tag="sbs")
             nc.sync.dma_start(out=sbs[:], in_=sb_v[:, qsl, osl])
-            ms = wts.tile([P, 4, OB], F32, tag="ms")
-            nc.vector.tensor_tensor(out=ms[:], in0=mk[:], in1=sps[:], op=ALU.mult)
+            ms = wts.tile([P, OB, 4], F32, tag="ms")
+            nc.vector.tensor_tensor(out=ms[:], in0=mk[:].rearrange("p t o -> p o t"),
+                                    in1=sps[:].rearrange("p t o -> p o t"), op=ALU.mult)
             acc = []
             for m in range(NM):
                 am = psum.tile([P, OB], F32, tag="acc%d" % m)
                 acc.append(am)
-            ct_v = ct[:].rearrange("p t (o g) -> p g o t", g=G)
-            ms_v = ms[:].rearrange("p t o -> p o t").unsqueeze(1)
+            ct_v = ct[:].rearrange("p t (o g) -> p o g t", g=G)
+            ms_v = ms[:].unsqueeze(2)
             for k in range(3):
                 g0 = 4 * k
                 ng = min(4, G - g0)
                 gw = wts.tile([P, 4, OB, 4], BF16, tag="gw", bufs=3, align_bytes=64)
-                nc.vector.tensor_tensor(out=gw[:, 0:ng, :, :], in0=ct_v[:, g0:g0 + ng, :, :],
-                                        in1=ms_v.to_broadcast([P, ng, OB, 4]), op=ALU.mult)
+                nc.vector.tensor_tensor(out=gw[:, 0:ng, :, :].rearrange("p g o t -> p o g t"),
+                                        in0=ct_v[:, :, g0:g0 + ng, :],
+                                        in1=ms_v.to_broadcast([P, OB, ng, 4]), op=ALU.mult)
                 if ng < 4:
                     nc.vector.tensor_tensor(out=gw[:, 3, :, :], in0=mk[:].rearrange("p t o -> p o t"),
                                             in1=sbs[:].rearrange("p t o -> p o t"), op=ALU.mult)

@@ -150,25 +150,25 @@ def tile_kan_layer_kernel(tc, x, grid, coef, scale_base, scale_sp, mask, out):
             nc.sync.dma_start(out=sps[:], in_=sp_v[:, qsl, osl])
             sbs = wts.tile([P, 4, OB], BF16, tag="sbs")
             nc.sync.dma_start(out=sbs[:], in_=sb_v[:, qsl, osl])
-            ms = wts.tile([P, OB, 4], F32, tag="ms")
-            nc.vector.tensor_tensor(out=ms[:], in0=mk[:].rearrange("p t o -> p o t"),
-                                    in1=sps[:].rearrange("p t o -> p o t"), op=ALU.mult)
+            ms = wts.tile([P, 4, OB], F32, tag="ms")
+            nc.vector.tensor_tensor(out=ms[:], in0=mk[:], in1=sps[:], op=ALU.mult)
+            wbn = wts.tile([P, 4, OB], BF16, tag="wbn")
+            nc.vector.tensor_tensor(out=wbn[:], in0=mk[:], in1=sbs[:], op=ALU.mult)
             acc = []
             for m in range(NM):
                 am = psum.tile([P, OB], F32, tag="acc%d" % m)
                 acc.append(am)
-            ct_v = ct[:].rearrange("p t (o g) -> p o g t", g=G)
-            ms_v = ms[:].unsqueeze(2)
+            ct_v = ct[:].rearrange("p t (o g) -> p o t g", g=G)
+            ms_v = ms[:].rearrange("p t o -> p o t").unsqueeze(3)
             for k in range(3):
                 g0 = 4 * k
                 ng = min(4, G - g0)
                 gw = wts.tile([P, 4, OB, 4], BF16, tag="gw", bufs=3, align_bytes=64)
-                nc.vector.tensor_tensor(out=gw[:, 0:ng, :, :].rearrange("p g o t -> p o g t"),
-                                        in0=ct_v[:, :, g0:g0 + ng, :],
-                                        in1=ms_v.to_broadcast([P, OB, ng, 4]), op=ALU.mult)
+                nc.vector.tensor_tensor(out=gw[:, 0:ng, :, :].rearrange("p g o t -> p o t g"),
+                                        in0=ct_v[:, :, :, g0:g0 + ng],
+                                        in1=ms_v.to_broadcast([P, OB, 4, ng]), op=ALU.mult)
                 if ng < 4:
-                    nc.vector.tensor_tensor(out=gw[:, 3, :, :], in0=mk[:].rearrange("p t o -> p o t"),
-                                            in1=sbs[:].rearrange("p t o -> p o t"), op=ALU.mult)
+                    nc.scalar.copy(out=gw[:, 3, :, :], in_=wbn[:].rearrange("p t o -> p o t"))
                 wc = wts.tile([P, 4 * OB], U32, tag="wc", bufs=4, align_bytes=64)
                 ws = wts.tile([P, 4 * OB], U8, tag="ws", bufs=4, align_bytes=64)
                 nc.vector.quantize_mx(out=wc[:].bitcast(FP8X4), scales=ws[:],

@@ -24,6 +24,8 @@ NM = B // P
 NPL = G + 1
 OB = 128
 NOB = O // OB
+GW = 512
+NWC = 12
 PW = NPL * B
 
 FLOPS = 2 * B * I * O * NPL
@@ -39,16 +41,21 @@ def tile_kan_layer_kernel(tc, x, grid, coef, scale_base, scale_sp, mask, out):
 
     with ExitStack() as ctx:
         const = ctx.enter_context(tc.tile_pool(name="const", bufs=1))
-        psum = ctx.enter_context(tc.psum_pool(name="psum", bufs=2))
+        psum = ctx.enter_context(tc.psum_pool(name="psum", bufs=1))
 
         ident = const.tile([P, P], BF16)
         make_identity(nc, ident[:])
+        ident_f = const.tile([P, P], F32)
+        make_identity(nc, ident_f[:])
+        ctx.enter_context(tc.manual_schedule())
         g_bf = const.tile([P, NQ, 16], BF16)
         nc.sync.dma_start(out=g_bf[:, :, 0:NK], in_=grid.rearrange("(q p) r -> p q r", p=P))
-        t_sb = const.tile([P, NQ, B], BF16)
         bs_codes = const.tile([P, 2, PW], U32, align_bytes=64)
         bs_scales = const.tile([P, 2, PW], U8, align_bytes=64)
         accs = const.tile([P, NM, O], F32)
+
+        x_sb = const.tile([P, NM, I], BF16)
+        nc.sync.dma_start(out=x_sb[:], in_=x.rearrange("(m p) i -> p m i", p=P))
 
         gf = const.tile([P, NQ, 16], F32)
         negg = const.tile([P, NQ, 16], F32)
@@ -61,6 +68,8 @@ def tile_kan_layer_kernel(tc, x, grid, coef, scale_base, scale_sp, mask, out):
         r1 = const.tile([P, NQ, 16], F32)
         negk = const.tile([P, NQ, 16], F32)
         negl = const.tile([P, NQ, 16], F32)
+        kp = const.tile([P, NQ, 16], F32)
+        kq = const.tile([P, NQ, 16], F32)
         nc.vector.tensor_copy(out=gf[:, :, 0:NK], in_=g_bf[:, :, 0:NK])
         nc.vector.tensor_scalar(out=negg[:, :, 0:NK], in0=gf[:, :, 0:NK], scalar1=-1.0, scalar2=None, op0=ALU.mult)
         nc.vector.tensor_tensor(out=d1[:, :, 0:14], in0=gf[:, :, 1:15], in1=gf[:, :, 0:14], op=ALU.subtract)
@@ -79,124 +88,303 @@ def tile_kan_layer_kernel(tc, x, grid, coef, scale_base, scale_sp, mask, out):
                                        op0=ALU.mult, op1=ALU.mult)
         nc.vector.scalar_tensor_tensor(out=negl[:, :, 0:11], in0=d4[:, :, 0:11], scalar=-1.0, in1=r1[:, :, 3:14],
                                        op0=ALU.mult, op1=ALU.mult)
+        nc.vector.scalar_tensor_tensor(out=kp[:, :, 0:11], in0=negk[:, :, 0:11], scalar=-1.0, in1=ca[:, :, 1:12],
+                                       op0=ALU.mult, op1=ALU.mult)
+        nc.vector.scalar_tensor_tensor(out=kq[:, :, 0:11], in0=negl[:, :, 0:11], scalar=-1.0, in1=cc[:, :, 0:11],
+                                       op0=ALU.mult, op1=ALU.mult)
 
         bas = ctx.enter_context(tc.tile_pool(name="bas", bufs=3))
         big = ctx.enter_context(tc.tile_pool(name="big", bufs=1))
         wts = ctx.enter_context(tc.tile_pool(name="wts", bufs=2))
 
-        x_sb = big.tile([P, NM, I], BF16)
-        nc.sync.dma_start(out=x_sb[:], in_=x.rearrange("(m p) i -> p m i", p=P))
+        def bind(f, *args):
+            return lambda: f(*args)
 
-        state = {}
+        tps = {}
+        tqs = {}
+        mx4s = {}
+        cts = {}
+        mss = {}
+        gws = {}
+        wcs = {}
+        accd = {}
+        pending = {}
+        ready = []
 
-        def basis_group(q):
-            c, tt = divmod(q, 4)
-            if tt == 0:
-                mx4 = big.tile([P, 4, PW], BF16)
-                state["mx4"] = mx4
-            mx4 = state["mx4"]
-            tp = psum.tile([P, B], BF16, tag="tp")
+        def turn(q):
+            tp = psum.tile([P, B], BF16, tag="tp", bufs=2)
             for m in range(NM):
                 nc.tensor.transpose(out=tp[:, m * P:(m + 1) * P], in_=x_sb[:, m, q * P:(q + 1) * P], identity=ident[:])
-            tq = t_sb[:, q, :]
-            nc.scalar.activation(out=mx4[:, tt, G * B:NPL * B], in_=tp[:], func=ACTF.Silu)
-            nc.vector.tensor_scalar(out=tq, in0=tp[:], scalar1=gf[:, q, 0:1], scalar2=gf[:, q, 14:15],
+            tps[q] = tp
+
+        def clamp(q):
+            c, tt = divmod(q, 4)
+            if tt == 0:
+                mx4 = big.tile([P, 4, PW], BF16, tag="mx4")
+                mx4s[c] = mx4
+            tq = bas.tile([P, B], BF16, tag="tq", bufs=2)
+            nc.vector.tensor_scalar(out=tq[:], in0=tps[q][:], scalar1=gf[:, q, 0:1], scalar2=gf[:, q, 14:15],
                                     op0=ALU.max, op1=ALU.min)
-            lt = big.tile([P, G, B], BF16, tag="lt")
-            rt = big.tile([P, G, B], BF16, tag="rt")
+            nc.scalar.activation(out=mx4s[c][:, tt, G * B:NPL * B], in_=tps[q][:], func=ACTF.Silu)
+            tqs[q] = tq
+
+        def basis_steps(q, on_gpsimd):
+            c, tt = divmod(q, 4)
+            sqs = {}
+            cus = {}
             pp = {}
             qq = {}
-            for r in range(NK):
-                sq = bas.tile([P, B], F32, tag="sq")
-                nc.scalar.activation(out=sq[:], in_=tq, func=ACTF.Square, bias=negg[:, q, r:r + 1], scale=1.0)
-                cu = bas.tile([P, B], F32, tag="cu")
-                nc.vector.scalar_tensor_tensor(out=cu[:], in0=tq, scalar=gf[:, q, r:r + 1], in1=sq[:],
+            st = {}
+
+            def square(r):
+                sq = bas.tile([P, B], F32, tag="sq", bufs=4)
+                nc.scalar.activation(out=sq[:], in_=tqs[q][:], func=ACTF.Square, bias=negg[:, q, r:r + 1], scale=1.0)
+                sqs[r] = sq
+
+            def cube(r):
+                cu = bas.tile([P, B], F32, tag="cu", bufs=4)
+                t_in = tps[q] if on_gpsimd else tqs[q]
+                nc.vector.scalar_tensor_tensor(out=cu[:], in0=t_in[:], scalar=gf[:, q, r:r + 1], in1=sqs[r][:],
                                                op0=ALU.subtract, op1=ALU.mult)
-                if r <= 11:
-                    pt = bas.tile([P, B], F32, tag="pt", bufs=4)
-                    nc.scalar.activation(out=pt[:], in_=cu[:], func=ACTF.Relu, scale=ca[:, q, r:r + 1])
-                    pp[r] = pt
-                if r >= 3:
-                    qt = bas.tile([P, B], F32, tag="qt", bufs=4)
-                    nc.scalar.activation(out=qt[:], in_=cu[:], func=ACTF.Relu, scale=cc[:, q, r - 3:r - 2])
-                    qq[r] = qt
+                cus[r] = cu
+
+            def relu(tag, bufs, r, scale):
+                y = bas.tile([P, B], F32, tag=tag, bufs=bufs)
+                nc.scalar.activation(out=y[:], in_=cus[r][:], func=ACTF.Relu, scale=scale)
+                return y
+
+            def lt(j):
+                return mx4s[c][:, tt, j * B:(j + 1) * B]
+
+            def step(r):
+                if r == 0:
+                    rt = big.tile([P, G, B], BF16, tag="rt")
+                    st["rt"] = rt
+                    for e in range(3):
+                        square(e)
+                if on_gpsimd:
+                    cube(r)
+                    if r + 3 < NK:
+                        square(r + 3)
+                    if 1 <= r <= 11:
+                        pb = relu("pb", 2, r, kp[:, q, r - 1:r])
+                        nc.gpsimd.tensor_tensor(out=lt(r - 1), in0=pp[r - 1][:], in1=pb[:], op=ALU.subtract)
+                    if r <= 10:
+                        pp[r] = relu("pt", 4, r, ca[:, q, r:r + 1])
+                    if r >= 4:
+                        qa = relu("qb", 2, r, cc[:, q, r - 3:r - 2])
+                        nc.gpsimd.tensor_tensor(out=st["rt"][:, r - 4, :], in0=qa[:], in1=qq[r - 1][:], op=ALU.subtract)
+                    if 3 <= r <= 13:
+                        qq[r] = relu("qt", 4, r, kq[:, q, r - 3:r - 2])
+                else:
+                    cube(r)
+                    if r + 3 < NK:
+                        square(r + 3)
+                    if r <= 11:
+                        pp[r] = relu("pt", 4, r, ca[:, q, r:r + 1])
+                    if r >= 3:
+                        qq[r] = relu("qt", 4, r, cc[:, q, r - 3:r - 2])
+                    if r > 0:
+                        combine(r - 1)
+                    if r == NK - 1:
+                        combine(r)
+
+            def combine(r):
                 if 1 <= r <= 11:
-                    nc.vector.scalar_tensor_tensor(out=lt[:, r - 1, :], in0=pp[r][:], scalar=negk[:, q, r - 1:r],
+                    nc.vector.scalar_tensor_tensor(out=lt(r - 1), in0=pp[r][:], scalar=negk[:, q, r - 1:r],
                                                    in1=pp[r - 1][:], op0=ALU.mult, op1=ALU.add)
                 if r >= 4:
-                    nc.vector.scalar_tensor_tensor(out=rt[:, r - 4, :], in0=qq[r - 1][:], scalar=negl[:, q, r - 4:r - 3],
+                    nc.vector.scalar_tensor_tensor(out=st["rt"][:, r - 4, :], in0=qq[r - 1][:],
+                                                   scalar=negl[:, q, r - 4:r - 3],
                                                    in1=qq[r][:], op0=ALU.mult, op1=ALU.add)
-            nc.vector.tensor_tensor(out=mx4[:, tt, 0:G * B], in0=lt[:].rearrange("p j b -> p (j b)"),
-                                    in1=rt[:].rearrange("p j b -> p (j b)"), op=ALU.max)
-            if tt == 3:
-                w0 = 0
-                while w0 < PW:
-                    wn = min(1024, PW - w0)
-                    gb = bas.tile([P, 1024, 4], BF16, tag="gb", bufs=2, align_bytes=64)
-                    nc.scalar.copy(out=gb[:, 0:wn, :], in_=mx4[:, :, w0:w0 + wn].rearrange("p t w -> p w t"))
-                    nc.vector.quantize_mx(out=bs_codes[:, c, w0:w0 + wn].bitcast(FP8X4),
-                                          scales=bs_scales[:, c, w0:w0 + wn],
-                                          in_=gb[:, 0:wn, :].rearrange("p w t -> p (w t)"))
-                    w0 += wn
 
-        def weight_chunk(c, ob):
-            osl = slice(ob * OB, (ob + 1) * OB)
+            def finish():
+                both = mx4s[c][:, tt, 0:G * B]
+                nc.vector.tensor_tensor(out=both, in0=both, in1=st["rt"][:].rearrange("p j b -> p (j b)"), op=ALU.max)
+
+            return [bind(step, r) for r in range(NK)], finish
+
+        def group_steps(c):
+            gbs = {}
+            nw = PW // GW
+
+            def group(w):
+                gb = bas.tile([P, GW, 4], BF16, tag="gb", bufs=2, align_bytes=64)
+                nc.scalar.copy(out=gb[:], in_=mx4s[c][:, :, w * GW:(w + 1) * GW].rearrange("p t w -> p w t"))
+                gbs[w] = gb
+
+            def quantise(w):
+                nc.vector.quantize_mx(out=bs_codes[:, c, w * GW:(w + 1) * GW].bitcast(FP8X4),
+                                      scales=bs_scales[:, c, w * GW:(w + 1) * GW],
+                                      in_=gbs[w][:].rearrange("p w t -> p (w t)"))
+
+            def step(w):
+                if w < nw:
+                    group(w)
+                if w > 0:
+                    quantise(w - 1)
+
+            return [bind(step, w) for w in range(nw + 1)]
+
+        def load(n):
+            c, ob = divmod(n, NOB)
             qsl = slice(4 * c, 4 * c + 4)
-            ct = wts.tile([P, 4, OB * G], BF16, tag="ct", bufs=3)
-            nc.sync.dma_start(out=ct[:], in_=coef_v[:, qsl, ob * OB * G:(ob + 1) * OB * G])
+            osl = slice(ob * OB, (ob + 1) * OB)
             mk = wts.tile([P, 4, OB], BF16, tag="mk")
             nc.sync.dma_start(out=mk[:], in_=mask_v[:, qsl, osl])
             sps = wts.tile([P, 4, OB], BF16, tag="sps")
             nc.sync.dma_start(out=sps[:], in_=sp_v[:, qsl, osl])
             sbs = wts.tile([P, 4, OB], BF16, tag="sbs")
             nc.sync.dma_start(out=sbs[:], in_=sb_v[:, qsl, osl])
+            ct = wts.tile([P, 4, OB * G], BF16, tag="ct", bufs=2)
+            nc.sync.dma_start(out=ct[:], in_=coef_v[:, qsl, ob * OB * G:(ob + 1) * OB * G])
+            cts[n] = (ct, mk, sps, sbs)
+
+        def prep(n):
+            ct, mk, sps, sbs = cts[n]
             ms = wts.tile([P, 4, OB], F32, tag="ms")
             nc.vector.tensor_tensor(out=ms[:], in0=mk[:], in1=sps[:], op=ALU.mult)
+            ms_ps = psum.tile([P, OB, 4], F32, tag="ms_ps", bufs=2)
+            nc.tensor.matmul(out=ms_ps[:].rearrange("p o t -> p (o t)"), lhsT=ident_f[:],
+                             rhs=ms[:].rearrange("p t o -> p o t"), start=True, stop=True)
             wbn = wts.tile([P, 4, OB], BF16, tag="wbn")
             nc.vector.tensor_tensor(out=wbn[:], in0=mk[:], in1=sbs[:], op=ALU.mult)
-            acc = []
-            for m in range(NM):
-                am = psum.tile([P, OB], F32, tag="acc%d" % m)
-                acc.append(am)
-            ct_v = ct[:].rearrange("p t (o g) -> p o t g", g=G)
-            ms_v = ms[:].rearrange("p t o -> p o t").unsqueeze(3)
-            for k in range(3):
-                g0 = 4 * k
-                ng = min(4, G - g0)
-                gw = wts.tile([P, 4, OB, 4], BF16, tag="gw", bufs=3, align_bytes=64)
-                nc.vector.tensor_tensor(out=gw[:, 0:ng, :, :].rearrange("p g o t -> p o t g"),
-                                        in0=ct_v[:, :, :, g0:g0 + ng],
-                                        in1=ms_v.to_broadcast([P, OB, 4, ng]), op=ALU.mult)
-                if ng < 4:
-                    nc.scalar.copy(out=gw[:, 3, :, :], in_=wbn[:].rearrange("p t o -> p o t"))
-                wc = wts.tile([P, 4 * OB], U32, tag="wc", bufs=4, align_bytes=64)
-                ws = wts.tile([P, 4 * OB], U8, tag="ws", bufs=4, align_bytes=64)
-                nc.vector.quantize_mx(out=wc[:].bitcast(FP8X4), scales=ws[:],
-                                      in_=gw[:].rearrange("p g o t -> p (g o t)"))
-                for gi in range(4):
-                    pl = g0 + gi
-                    for m in range(NM):
-                        l0 = pl * B + m * P
-                        nc.tensor.matmul_mx(out=acc[m][:],
-                                            lhsT=bs_codes[:, c, l0:l0 + P].bitcast(FP8X4),
-                                            lhsT_scale=bs_scales[:, c, l0:l0 + P],
-                                            rhs=wc[:, gi * OB:(gi + 1) * OB].bitcast(FP8X4),
-                                            rhs_scale=ws[:, gi * OB:(gi + 1) * OB],
-                                            start=(pl == 0), stop=(pl == NPL - 1))
+            mss[n] = (ms_ps, wbn)
+
+        def new_gw(n, k):
+            gw = wts.tile([P, 4, OB, 4], BF16, tag="gw", bufs=3, align_bytes=64)
+            gws[n, k] = gw
+            return gw
+
+        def mult(n, k):
+            ng = min(4, G - 4 * k)
+            gw = gws[n, k] if (n, k) in gws else new_gw(n, k)
+            ct_v = cts[n][0][:].rearrange("p t (o g) -> p o t g", g=G)
+            nc.vector.tensor_tensor(out=gw[:, 0:ng, :, :].rearrange("p g o t -> p o t g"),
+                                    in0=ct_v[:, :, :, 4 * k:4 * k + ng],
+                                    in1=mss[n][0][:].unsqueeze(3).to_broadcast([P, OB, 4, ng]), op=ALU.mult)
+            if k == 1:
+                gw2 = new_gw(n, 2)
+                nc.scalar.copy(out=gw2[:, 3, :, :], in_=mss[n][1][:].rearrange("p t o -> p o t"))
+
+        def quant(n, k):
+            wc = wts.tile([P, 4 * OB], U32, tag="wc", bufs=NWC, align_bytes=64)
+            ws = wts.tile([P, 4 * OB], U8, tag="ws", bufs=NWC, align_bytes=64)
+            nc.vector.quantize_mx(out=wc[:].bitcast(FP8X4), scales=ws[:],
+                                  in_=gws[n, k][:].rearrange("p g o t -> p (g o t)"))
+            wcs[n, k] = (wc, ws)
+            pending[n, k] = True
+            flush()
+
+        def flush():
+            for n, k in list(pending):
+                if pending[n, k] and n // NOB in ready:
+                    pending[n, k] = False
+                    multiply(n, k)
+
+        def multiply(n, k):
+            c = n // NOB
+            if k == 0:
+                if n > 0:
+                    empty(n - 1)
+                accd[n] = []
+                for m in range(NM):
+                    am = psum.tile([P, OB], F32, tag="acc%d" % m)
+                    accd[n].append(am)
+            wc, ws = wcs[n, k]
+            for gi in range(4):
+                pl = 4 * k + gi
+                for m in range(NM):
+                    l0 = pl * B + m * P
+                    nc.tensor.matmul_mx(out=accd[n][m][:],
+                                        lhsT=bs_codes[:, c, l0:l0 + P].bitcast(FP8X4),
+                                        lhsT_scale=bs_scales[:, c, l0:l0 + P],
+                                        rhs=wc[:, gi * OB:(gi + 1) * OB].bitcast(FP8X4),
+                                        rhs_scale=ws[:, gi * OB:(gi + 1) * OB],
+                                        start=(pl == 0), stop=(pl == NPL - 1))
+
+        def empty(n):
+            c, ob = divmod(n, NOB)
+            osl = slice(ob * OB, (ob + 1) * OB)
             if c == 0:
                 for m in range(NM):
-                    nc.scalar.copy(out=accs[:, m, osl], in_=acc[m][:])
+                    nc.scalar.copy(out=accs[:, m, osl], in_=accd[n][m][:])
             else:
                 ot = wts.tile([P, NM, OB], F32, tag="ot")
                 for m in range(NM):
-                    nc.vector.tensor_tensor(out=ot[:, m, :], in0=acc[m][:], in1=accs[:, m, osl], op=ALU.add)
+                    nc.vector.tensor_tensor(out=ot[:, m, :], in0=accd[n][m][:], in1=accs[:, m, osl], op=ALU.add)
                 nc.sync.dma_start(out=out_v[:, :, osl], in_=ot[:])
 
+        units = [(n, k) for n in range(2 * NOB) for k in range(3)]
+        weight_steps = []
+
+        def add_unit(i):
+            n, k = units[i]
+
+            def first():
+                mult(n, k)
+                if k == 2 and n + 2 < 2 * NOB:
+                    load(n + 2)
+
+            def second():
+                if i > 0:
+                    quant(*units[i - 1])
+
+            def third():
+                prep(n + 1)
+
+            weight_steps.extend([first, second])
+            if k == 1 and n + 1 < 2 * NOB:
+                weight_steps.append(third)
+
+        for i in range(len(units)):
+            add_unit(i)
+        weight_steps.append(bind(quant, *units[-1]))
+
+        woven = [0]
+
+        def weave(chunks, others):
+            start = woven[0]
+            stop = start + 7 * chunks if chunks else len(weight_steps)
+            woven[0] = stop
+            mine = weight_steps[start:stop]
+            done = 0
+            for i, s in enumerate(mine):
+                s()
+                upto = (i + 1) * len(others) // len(mine)
+                while done < upto:
+                    others[done]()
+                    done += 1
+
+        load(0)
+        load(1)
+        for q in range(2):
+            turn(q)
+            clamp(q)
         for q in range(4):
-            basis_group(q)
-        for i in range(4):
-            weight_chunk(0, 2 * i)
-            weight_chunk(0, 2 * i + 1)
-            basis_group(4 + i)
-        for ob in range(NOB):
-            weight_chunk(1, ob)
+            steps, finish = basis_steps(q, False)
+            for s in steps:
+                s()
+            finish()
+            turn(q + 2)
+            if q < 2:
+                clamp(q + 2)
+        prep(0)
+        weave(2, group_steps(0))
+        ready.append(0)
+        flush()
+        clamp(4)
+        clamp(5)
+        waiting = []
+        for q in range(4, 8):
+            steps, finish = basis_steps(q, True)
+            weave(2, waiting + steps)
+            waiting = [finish]
+            if q + 2 < 8:
+                turn(q + 2)
+                clamp(q + 2)
+        weave(2, waiting + group_steps(1))
+        ready.append(1)
+        flush()
+        weave(0, [])
+        empty(2 * NOB - 1)

@@ -24,8 +24,9 @@ NM = B // P
 NPL = G + 1
 OB = 128
 NOB = O // OB
-GW = 512
-NWC = 12
+NWC = 18
+ON_VECTOR = (0, 2, 4, 6)
+STEPS = (7, 10)
 PW = NPL * B
 
 FLOPS = 2 * B * I * O * NPL
@@ -68,8 +69,12 @@ def tile_kan_layer_kernel(tc, x, grid, coef, scale_base, scale_sp, mask, out):
         r1 = const.tile([P, NQ, 16], F32)
         negk = const.tile([P, NQ, 16], F32)
         negl = const.tile([P, NQ, 16], F32)
+        root = const.tile([P, NQ, 16], F32)
+        nroot = const.tile([P, NQ, 16], F32)
+        rsig = const.tile([P, NQ, 16], F32)
         kp = const.tile([P, NQ, 16], F32)
-        kq = const.tile([P, NQ, 16], F32)
+        ka = const.tile([P, NQ, 16], F32)
+        kb = const.tile([P, NQ, 16], F32)
         nc.vector.tensor_copy(out=gf[:, :, 0:NK], in_=g_bf[:, :, 0:NK])
         nc.vector.tensor_scalar(out=negg[:, :, 0:NK], in0=gf[:, :, 0:NK], scalar1=-1.0, scalar2=None, op0=ALU.mult)
         nc.vector.tensor_tensor(out=d1[:, :, 0:14], in0=gf[:, :, 1:15], in1=gf[:, :, 0:14], op=ALU.subtract)
@@ -88,9 +93,19 @@ def tile_kan_layer_kernel(tc, x, grid, coef, scale_base, scale_sp, mask, out):
                                        op0=ALU.mult, op1=ALU.mult)
         nc.vector.scalar_tensor_tensor(out=negl[:, :, 0:11], in0=d4[:, :, 0:11], scalar=-1.0, in1=r1[:, :, 3:14],
                                        op0=ALU.mult, op1=ALU.mult)
-        nc.vector.scalar_tensor_tensor(out=kp[:, :, 0:11], in0=negk[:, :, 0:11], scalar=-1.0, in1=ca[:, :, 1:12],
-                                       op0=ALU.mult, op1=ALU.mult)
-        nc.vector.scalar_tensor_tensor(out=kq[:, :, 0:11], in0=negl[:, :, 0:11], scalar=-1.0, in1=cc[:, :, 0:11],
+        nc.vector.memset(root[:], 1.0)
+        nc.scalar.activation(out=rsig[:, :, 0:12], in_=ca[:, :, 0:12], func=ACTF.Sqrt)
+        nc.vector.reciprocal(out=kp[:, :, 0:12], in_=rsig[:, :, 0:12])
+        nc.vector.tensor_tensor(out=kp[:, :, 0:12], in0=kp[:, :, 0:12], in1=ca[:, :, 0:12], op=ALU.mult)
+        nc.vector.tensor_tensor(out=kp[:, :, 0:12], in0=kp[:, :, 0:12], in1=rsig[:, :, 0:12], op=ALU.add)
+        nc.vector.tensor_scalar(out=root[:, :, 0:12], in0=kp[:, :, 0:12], scalar1=0.5, scalar2=None, op0=ALU.mult)
+        nc.vector.tensor_tensor(out=nroot[:, :, 0:15], in0=root[:, :, 0:15], in1=negg[:, :, 0:15], op=ALU.mult)
+        nc.vector.tensor_tensor(out=rsig[:, :, 0:15], in0=root[:, :, 0:15], in1=root[:, :, 0:15], op=ALU.mult)
+        nc.vector.reciprocal(out=rsig[:, :, 0:15], in_=rsig[:, :, 0:15])
+        nc.vector.tensor_scalar(out=kp[:, :, 0:11], in0=negk[:, :, 0:11], scalar1=-1.0, scalar2=None, op0=ALU.mult)
+        nc.vector.tensor_tensor(out=ka[:, :, 0:11], in0=cc[:, :, 1:12], in1=rsig[:, :, 4:15], op=ALU.mult)
+        nc.vector.tensor_tensor(out=kb[:, :, 0:11], in0=cc[:, :, 0:11], in1=rsig[:, :, 3:14], op=ALU.mult)
+        nc.vector.scalar_tensor_tensor(out=kb[:, :, 0:11], in0=kb[:, :, 0:11], scalar=-1.0, in1=negl[:, :, 0:11],
                                        op0=ALU.mult, op1=ALU.mult)
 
         bas = ctx.enter_context(tc.tile_pool(name="bas", bufs=3))
@@ -128,29 +143,22 @@ def tile_kan_layer_kernel(tc, x, grid, coef, scale_base, scale_sp, mask, out):
             nc.scalar.activation(out=mx4s[c][:, tt, G * B:NPL * B], in_=tps[q][:], func=ACTF.Silu)
             tqs[q] = tq
 
-        def basis_steps(q, on_gpsimd):
+        def basis_steps(q):
             c, tt = divmod(q, 4)
             sqs = {}
-            cus = {}
-            pp = {}
-            qq = {}
+            ws = {}
+            rbs = {}
             st = {}
 
             def square(r):
                 sq = bas.tile([P, B], F32, tag="sq", bufs=4)
-                nc.scalar.activation(out=sq[:], in_=tqs[q][:], func=ACTF.Square, bias=negg[:, q, r:r + 1], scale=1.0)
+                nc.scalar.activation(out=sq[:], in_=tqs[q][:], func=ACTF.Square, bias=nroot[:, q, r:r + 1],
+                                     scale=root[:, q, r:r + 1])
                 sqs[r] = sq
-
-            def cube(r):
-                cu = bas.tile([P, B], F32, tag="cu", bufs=4)
-                t_in = tps[q] if on_gpsimd else tqs[q]
-                nc.vector.scalar_tensor_tensor(out=cu[:], in0=t_in[:], scalar=gf[:, q, r:r + 1], in1=sqs[r][:],
-                                               op0=ALU.subtract, op1=ALU.mult)
-                cus[r] = cu
 
             def relu(tag, bufs, r, scale):
                 y = bas.tile([P, B], F32, tag=tag, bufs=bufs)
-                nc.scalar.activation(out=y[:], in_=cus[r][:], func=ACTF.Relu, scale=scale)
+                nc.scalar.activation(out=y[:], in_=ws[r][:], func=ACTF.Relu, scale=scale)
                 return y
 
             def lt(j):
@@ -162,41 +170,24 @@ def tile_kan_layer_kernel(tc, x, grid, coef, scale_base, scale_sp, mask, out):
                     st["rt"] = rt
                     for e in range(3):
                         square(e)
-                if on_gpsimd:
-                    cube(r)
-                    if r + 3 < NK:
-                        square(r + 3)
-                    if 1 <= r <= 11:
-                        pb = relu("pb", 2, r, kp[:, q, r - 1:r])
-                        nc.gpsimd.tensor_tensor(out=lt(r - 1), in0=pp[r - 1][:], in1=pb[:], op=ALU.subtract)
-                    if r <= 10:
-                        pp[r] = relu("pt", 4, r, ca[:, q, r:r + 1])
-                    if r >= 4:
-                        qa = relu("qb", 2, r, cc[:, q, r - 3:r - 2])
-                        nc.gpsimd.tensor_tensor(out=st["rt"][:, r - 4, :], in0=qa[:], in1=qq[r - 1][:], op=ALU.subtract)
-                    if 3 <= r <= 13:
-                        qq[r] = relu("qt", 4, r, kq[:, q, r - 3:r - 2])
-                else:
-                    cube(r)
-                    if r + 3 < NK:
-                        square(r + 3)
-                    if r <= 11:
-                        pp[r] = relu("pt", 4, r, ca[:, q, r:r + 1])
-                    if r >= 3:
-                        qq[r] = relu("qt", 4, r, cc[:, q, r - 3:r - 2])
-                    if r > 0:
-                        combine(r - 1)
-                    if r == NK - 1:
-                        combine(r)
-
-            def combine(r):
+                w = bas.tile([P, B], F32, tag="w", bufs=5)
+                nc.vector.scalar_tensor_tensor(out=w[:], in0=tps[q][:], scalar=gf[:, q, r:r + 1], in1=sqs[r][:],
+                                               op0=ALU.subtract, op1=ALU.mult)
+                ws[r] = w
+                if r + 3 < NK:
+                    square(r + 3)
                 if 1 <= r <= 11:
-                    nc.vector.scalar_tensor_tensor(out=lt(r - 1), in0=pp[r][:], scalar=negk[:, q, r - 1:r],
-                                                   in1=pp[r - 1][:], op0=ALU.mult, op1=ALU.add)
-                if r >= 4:
-                    nc.vector.scalar_tensor_tensor(out=st["rt"][:, r - 4, :], in0=qq[r - 1][:],
-                                                   scalar=negl[:, q, r - 4:r - 3],
-                                                   in1=qq[r][:], op0=ALU.mult, op1=ALU.add)
+                    ra = relu("ra", 2, r, kp[:, q, r - 1:r])
+                    nc.gpsimd.tensor_tensor(out=lt(r - 1), in0=ws[r - 1][:], in1=ra[:], op=ALU.subtract)
+                if r >= 4 and r - 4 not in ON_VECTOR:
+                    qa = relu("qa", 2, r, ka[:, q, r - 4:r - 3])
+                    nc.gpsimd.tensor_tensor(out=st["rt"][:, r - 4, :], in0=qa[:], in1=rbs[r - 1][:], op=ALU.subtract)
+                if r >= 5 and r - 5 in ON_VECTOR:
+                    nc.vector.scalar_tensor_tensor(out=st["rt"][:, r - 5, :], in0=ws[r - 1][:],
+                                                   scalar=ka[:, q, r - 5:r - 4], in1=rbs[r - 2][:],
+                                                   op0=ALU.mult, op1=ALU.subtract)
+                if 3 <= r <= 13:
+                    rbs[r] = relu("rb", 4, r, kb[:, q, r - 3:r - 2])
 
             def finish():
                 both = mx4s[c][:, tt, 0:G * B]
@@ -206,25 +197,31 @@ def tile_kan_layer_kernel(tc, x, grid, coef, scale_base, scale_sp, mask, out):
 
         def group_steps(c):
             gbs = {}
-            nw = PW // GW
+            pieces = [(w, 256) for w in range(0, 4096, 256)] + [(4096, 128), (4224, 256), (4480, 128)]
 
-            def group(w):
-                gb = bas.tile([P, GW, 4], BF16, tag="gb", bufs=2, align_bytes=64)
-                nc.scalar.copy(out=gb[:], in_=mx4s[c][:, :, w * GW:(w + 1) * GW].rearrange("p t w -> p w t"))
-                gbs[w] = gb
+            def group(i):
+                w0, wn = pieces[i]
+                gb = bas.tile([P, 256, 4], BF16, tag="gb", bufs=2, align_bytes=64)
+                source = mx4s[c][:, :, w0:w0 + wn].rearrange("p t w -> p w t")
+                if w0 < G * B:
+                    nc.scalar.activation(out=gb[:, 0:wn, :], in_=source, func=ACTF.Relu)
+                else:
+                    nc.scalar.copy(out=gb[:, 0:wn, :], in_=source)
+                gbs[i] = gb
 
-            def quantise(w):
-                nc.vector.quantize_mx(out=bs_codes[:, c, w * GW:(w + 1) * GW].bitcast(FP8X4),
-                                      scales=bs_scales[:, c, w * GW:(w + 1) * GW],
-                                      in_=gbs[w][:].rearrange("p w t -> p (w t)"))
+            def quantise(i):
+                w0, wn = pieces[i]
+                nc.vector.quantize_mx(out=bs_codes[:, c, w0:w0 + wn].bitcast(FP8X4),
+                                      scales=bs_scales[:, c, w0:w0 + wn],
+                                      in_=gbs[i][:, 0:wn, :].rearrange("p w t -> p (w t)"))
 
-            def step(w):
-                if w < nw:
-                    group(w)
-                if w > 0:
-                    quantise(w - 1)
+            def step(i):
+                if i < len(pieces):
+                    group(i)
+                if i > 0:
+                    quantise(i - 1)
 
-            return [bind(step, w) for w in range(nw + 1)]
+            return [bind(step, i) for i in range(len(pieces) + 1)]
 
         def load(n):
             c, ob = divmod(n, NOB)
@@ -242,7 +239,7 @@ def tile_kan_layer_kernel(tc, x, grid, coef, scale_base, scale_sp, mask, out):
 
         def prep(n):
             ct, mk, sps, sbs = cts[n]
-            ms = wts.tile([P, 4, OB], F32, tag="ms")
+            ms = wts.tile([P, 4, OB], F32, tag="ms", bufs=1)
             nc.vector.tensor_tensor(out=ms[:], in0=mk[:], in1=sps[:], op=ALU.mult)
             ms_ps = psum.tile([P, OB, 4], F32, tag="ms_ps", bufs=2)
             nc.tensor.matmul(out=ms_ps[:].rearrange("p o t -> p (o t)"), lhsT=ident_f[:],
@@ -274,13 +271,13 @@ def tile_kan_layer_kernel(tc, x, grid, coef, scale_base, scale_sp, mask, out):
                                   in_=gws[n, k][:].rearrange("p g o t -> p (g o t)"))
             wcs[n, k] = (wc, ws)
             pending[n, k] = True
-            flush()
 
-        def flush():
+        def flush(most):
             for n, k in list(pending):
-                if pending[n, k] and n // NOB in ready:
+                if most and pending[n, k] and n // NOB in ready:
                     pending[n, k] = False
                     multiply(n, k)
+                    most -= 1
 
         def multiply(n, k):
             c = n // NOB
@@ -310,7 +307,7 @@ def tile_kan_layer_kernel(tc, x, grid, coef, scale_base, scale_sp, mask, out):
                 for m in range(NM):
                     nc.scalar.copy(out=accs[:, m, osl], in_=accd[n][m][:])
             else:
-                ot = wts.tile([P, NM, OB], F32, tag="ot")
+                ot = wts.tile([P, NM, OB], F32, tag="ot", bufs=1)
                 for m in range(NM):
                     nc.vector.tensor_tensor(out=ot[:, m, :], in0=accd[n][m][:], in1=accs[:, m, osl], op=ALU.add)
                 nc.sync.dma_start(out=out_v[:, :, osl], in_=ot[:])
@@ -343,15 +340,15 @@ def tile_kan_layer_kernel(tc, x, grid, coef, scale_base, scale_sp, mask, out):
 
         woven = [0]
 
-        def weave(chunks, others):
+        def weave(count, others):
             start = woven[0]
-            stop = start + 7 * chunks if chunks else len(weight_steps)
+            stop = min(start + count, len(weight_steps))
             woven[0] = stop
-            mine = weight_steps[start:stop]
             done = 0
-            for i, s in enumerate(mine):
-                s()
-                upto = (i + 1) * len(others) // len(mine)
+            for i in range(start, stop):
+                weight_steps[i]()
+                flush(2)
+                upto = (i + 1 - start) * len(others) // (stop - start)
                 while done < upto:
                     others[done]()
                     done += 1
@@ -361,30 +358,23 @@ def tile_kan_layer_kernel(tc, x, grid, coef, scale_base, scale_sp, mask, out):
         for q in range(2):
             turn(q)
             clamp(q)
-        for q in range(4):
-            steps, finish = basis_steps(q, False)
-            for s in steps:
-                s()
-            finish()
-            turn(q + 2)
-            if q < 2:
-                clamp(q + 2)
         prep(0)
-        weave(2, group_steps(0))
-        ready.append(0)
-        flush()
-        clamp(4)
-        clamp(5)
         waiting = []
-        for q in range(4, 8):
-            steps, finish = basis_steps(q, True)
-            weave(2, waiting + steps)
-            waiting = [finish]
-            if q + 2 < 8:
-                turn(q + 2)
-                clamp(q + 2)
-        weave(2, waiting + group_steps(1))
-        ready.append(1)
-        flush()
-        weave(0, [])
+        for c in range(2):
+            for q in range(4 * c, 4 * c + 4):
+                steps, finish = basis_steps(q)
+                weave(STEPS[c], waiting + steps)
+                waiting = [finish]
+                if q + 2 < 8:
+                    turn(q + 2)
+                    if q + 2 != 4 and q + 2 != 5:
+                        clamp(q + 2)
+            weave(14, waiting + group_steps(c))
+            waiting = []
+            ready.append(c)
+            if c == 0:
+                clamp(4)
+                clamp(5)
+        weave(len(weight_steps), [])
+        flush(len(pending))
         empty(2 * NOB - 1)

@@ -24,9 +24,8 @@ NM = B // P
 NPL = G + 1
 OB = 128
 NOB = O // OB
-NWC = 18
-ON_VECTOR = (0, 2, 4, 6)
-STEPS = (7, 10)
+NWC = 22
+STEPS = (51, 48)
 PW = NPL * B
 
 FLOPS = 2 * B * I * O * NPL
@@ -34,10 +33,10 @@ FLOPS = 2 * B * I * O * NPL
 
 def tile_kan_layer_kernel(tc, x, grid, coef, scale_base, scale_sp, mask, out):
     nc = tc.nc
-    coef_v = coef.rearrange("(q p) o g -> p q (o g)", p=P)
-    mask_v = mask.rearrange("(q p) o -> p q o", p=P)
-    sp_v = scale_sp.rearrange("(q p) o -> p q o", p=P)
-    sb_v = scale_base.rearrange("(q p) o -> p q o", p=P)
+    coef_v = coef.rearrange("(h p e) o g -> p h e (o g)", p=P, e=2)
+    mask_v = mask.rearrange("(h p e) o -> p h e o", p=P, e=2)
+    sp_v = scale_sp.rearrange("(h p e) o -> p h e o", p=P, e=2)
+    sb_v = scale_base.rearrange("(h p e) o -> p h e o", p=P, e=2)
     out_v = out.rearrange("(m p) o -> p m o", p=P)
 
     with ExitStack() as ctx:
@@ -51,8 +50,8 @@ def tile_kan_layer_kernel(tc, x, grid, coef, scale_base, scale_sp, mask, out):
         ctx.enter_context(tc.manual_schedule())
         g_bf = const.tile([P, NQ, 16], BF16)
         nc.sync.dma_start(out=g_bf[:, :, 0:NK], in_=grid.rearrange("(q p) r -> p q r", p=P))
-        bs_codes = const.tile([P, 2, PW], U32, align_bytes=64)
-        bs_scales = const.tile([P, 2, PW], U8, align_bytes=64)
+        bs_codes = const.tile([P, PW], U32, align_bytes=64)
+        bs_scales = const.tile([P, PW], U8, align_bytes=64)
         accs = const.tile([P, NM, O], F32)
 
         x_sb = const.tile([P, NM, I], BF16)
@@ -70,11 +69,12 @@ def tile_kan_layer_kernel(tc, x, grid, coef, scale_base, scale_sp, mask, out):
         negk = const.tile([P, NQ, 16], F32)
         negl = const.tile([P, NQ, 16], F32)
         root = const.tile([P, NQ, 16], F32)
-        nroot = const.tile([P, NQ, 16], F32)
+        groot = const.tile([P, NQ, 16], F32)
+        sig = const.tile([P, NQ, 16], F32)
         rsig = const.tile([P, NQ, 16], F32)
-        kp = const.tile([P, NQ, 16], F32)
+        sa = const.tile([P, NQ, 16], F32)
         ka = const.tile([P, NQ, 16], F32)
-        kb = const.tile([P, NQ, 16], F32)
+        sb = const.tile([P, NQ, 16], F32)
         nc.vector.tensor_copy(out=gf[:, :, 0:NK], in_=g_bf[:, :, 0:NK])
         nc.vector.tensor_scalar(out=negg[:, :, 0:NK], in0=gf[:, :, 0:NK], scalar1=-1.0, scalar2=None, op0=ALU.mult)
         nc.vector.tensor_tensor(out=d1[:, :, 0:14], in0=gf[:, :, 1:15], in1=gf[:, :, 0:14], op=ALU.subtract)
@@ -93,20 +93,25 @@ def tile_kan_layer_kernel(tc, x, grid, coef, scale_base, scale_sp, mask, out):
                                        op0=ALU.mult, op1=ALU.mult)
         nc.vector.scalar_tensor_tensor(out=negl[:, :, 0:11], in0=d4[:, :, 0:11], scalar=-1.0, in1=r1[:, :, 3:14],
                                        op0=ALU.mult, op1=ALU.mult)
-        nc.vector.memset(root[:], 1.0)
-        nc.scalar.activation(out=rsig[:, :, 0:12], in_=ca[:, :, 0:12], func=ACTF.Sqrt)
-        nc.vector.reciprocal(out=kp[:, :, 0:12], in_=rsig[:, :, 0:12])
-        nc.vector.tensor_tensor(out=kp[:, :, 0:12], in0=kp[:, :, 0:12], in1=ca[:, :, 0:12], op=ALU.mult)
-        nc.vector.tensor_tensor(out=kp[:, :, 0:12], in0=kp[:, :, 0:12], in1=rsig[:, :, 0:12], op=ALU.add)
-        nc.vector.tensor_scalar(out=root[:, :, 0:12], in0=kp[:, :, 0:12], scalar1=0.5, scalar2=None, op0=ALU.mult)
-        nc.vector.tensor_tensor(out=nroot[:, :, 0:15], in0=root[:, :, 0:15], in1=negg[:, :, 0:15], op=ALU.mult)
+        nc.vector.tensor_copy(out=sig[:, :, 0:11], in_=ca[:, :, 0:11])
+        nc.vector.tensor_scalar(out=sig[:, :, 11:15], in0=cc[:, :, 8:12], scalar1=-1.0, scalar2=None, op0=ALU.mult)
+        nc.scalar.activation(out=rsig[:, :, 0:15], in_=sig[:, :, 0:15], func=ACTF.Sqrt)
+        nc.vector.reciprocal(out=root[:, :, 0:15], in_=rsig[:, :, 0:15])
+        nc.vector.tensor_tensor(out=root[:, :, 0:15], in0=root[:, :, 0:15], in1=sig[:, :, 0:15], op=ALU.mult)
+        nc.vector.tensor_tensor(out=root[:, :, 0:15], in0=root[:, :, 0:15], in1=rsig[:, :, 0:15], op=ALU.add)
+        nc.vector.tensor_scalar(out=root[:, :, 0:15], in0=root[:, :, 0:15], scalar1=0.5, scalar2=None, op0=ALU.mult)
+        nc.vector.tensor_tensor(out=groot[:, :, 0:15], in0=root[:, :, 0:15], in1=gf[:, :, 0:15], op=ALU.mult)
         nc.vector.tensor_tensor(out=rsig[:, :, 0:15], in0=root[:, :, 0:15], in1=root[:, :, 0:15], op=ALU.mult)
         nc.vector.reciprocal(out=rsig[:, :, 0:15], in_=rsig[:, :, 0:15])
-        nc.vector.tensor_scalar(out=kp[:, :, 0:11], in0=negk[:, :, 0:11], scalar1=-1.0, scalar2=None, op0=ALU.mult)
-        nc.vector.tensor_tensor(out=ka[:, :, 0:11], in0=cc[:, :, 1:12], in1=rsig[:, :, 4:15], op=ALU.mult)
-        nc.vector.tensor_tensor(out=kb[:, :, 0:11], in0=cc[:, :, 0:11], in1=rsig[:, :, 3:14], op=ALU.mult)
-        nc.vector.scalar_tensor_tensor(out=kb[:, :, 0:11], in0=kb[:, :, 0:11], scalar=-1.0, in1=negl[:, :, 0:11],
+        nc.vector.tensor_copy(out=sa[:, :, 1:11], in_=negk[:, :, 0:10])
+        nc.vector.scalar_tensor_tensor(out=sa[:, :, 11:12], in0=negk[:, :, 10:11], scalar=-1.0, in1=ca[:, :, 11:12],
                                        op0=ALU.mult, op1=ALU.mult)
+        nc.vector.tensor_tensor(out=sa[:, :, 11:12], in0=sa[:, :, 11:12], in1=rsig[:, :, 11:12], op=ALU.mult)
+        nc.vector.tensor_tensor(out=ka[:, :, 0:7], in0=cc[:, :, 1:8], in1=rsig[:, :, 4:11], op=ALU.mult)
+        nc.vector.tensor_tensor(out=sb[:, :, 3:14], in0=cc[:, :, 0:11], in1=rsig[:, :, 3:14], op=ALU.mult)
+        nc.vector.tensor_tensor(out=sb[:, :, 3:14], in0=sb[:, :, 3:14], in1=negl[:, :, 0:11], op=ALU.mult)
+        nc.vector.tensor_scalar(out=sb[:, :, 11:14], in0=sb[:, :, 11:14], scalar1=-1.0, scalar2=None, op0=ALU.mult)
+        nc.vector.tensor_scalar(out=x_sb[:], in0=x_sb[:], scalar1=-1.0, scalar2=None, op0=ALU.mult)
 
         bas = ctx.enter_context(tc.tile_pool(name="bas", bufs=3))
         big = ctx.enter_context(tc.tile_pool(name="big", bufs=1))
@@ -115,138 +120,148 @@ def tile_kan_layer_kernel(tc, x, grid, coef, scale_base, scale_sp, mask, out):
         def bind(f, *args):
             return lambda: f(*args)
 
-        tps = {}
+        tns = {}
         tqs = {}
-        mx4s = {}
+        planes = {}
+        sqs = {}
+        vs = {}
+        ras = {}
+        qas = {}
+        rbs = {}
+        lefts = {}
+        rights = {}
+        turned = {}
+        gbs = {}
         cts = {}
         mss = {}
         gws = {}
         wcs = {}
         accd = {}
-        pending = {}
         ready = []
 
-        def turn(q):
-            tp = psum.tile([P, B], BF16, tag="tp", bufs=2)
+        def begin(q):
+            tp = psum.tile([P, B], BF16, tag="tp")
             for m in range(NM):
                 nc.tensor.transpose(out=tp[:, m * P:(m + 1) * P], in_=x_sb[:, m, q * P:(q + 1) * P], identity=ident[:])
-            tps[q] = tp
-
-        def clamp(q):
-            c, tt = divmod(q, 4)
-            if tt == 0:
-                mx4 = big.tile([P, 4, PW], BF16, tag="mx4")
-                mx4s[c] = mx4
-            tq = bas.tile([P, B], BF16, tag="tq", bufs=2)
-            nc.vector.tensor_scalar(out=tq[:], in0=tps[q][:], scalar1=gf[:, q, 0:1], scalar2=gf[:, q, 14:15],
+            tn = bas.tile([P, B], BF16, tag="tn", bufs=2)
+            nc.vector.tensor_scalar(out=tn[:], in0=tp[:], scalar1=negg[:, q, 14:15], scalar2=negg[:, q, 0:1],
                                     op0=ALU.max, op1=ALU.min)
-            nc.scalar.activation(out=mx4s[c][:, tt, G * B:NPL * B], in_=tps[q][:], func=ACTF.Silu)
+            tq = bas.tile([P, B], BF16, tag="tq", bufs=2)
+            nc.vector.tensor_scalar(out=tq[:], in0=tn[:], scalar1=-1.0, scalar2=None, op0=ALU.mult)
+            tns[q] = tn
             tqs[q] = tq
 
-        def basis_steps(q):
+        def square(q, r):
+            sq = bas.tile([P, B], F32, tag="sq", bufs=5)
+            nc.scalar.activation(out=sq[:], in_=tns[q][:], func=ACTF.Square, bias=groot[:, q, r:r + 1],
+                                 scale=root[:, q, r:r + 1])
+            sqs[q, r] = sq
+
+        def cube(q, r):
+            v = bas.tile([P, B], F32, tag="v", bufs=7)
+            t, g = (tns[q], negg) if r <= 10 else (tqs[q], gf)
+            nc.vector.scalar_tensor_tensor(out=v[:], in0=t[:], scalar=g[:, q, r:r + 1], in1=sqs[q, r][:],
+                                           op0=ALU.subtract, op1=ALU.mult)
+            vs[q, r] = v
+
+        def terms(q, r):
+            if 1 <= r <= 11:
+                ra = bas.tile([P, B], F32, tag="ra", bufs=6)
+                nc.scalar.activation(out=ra[:], in_=vs[q, r][:], func=ACTF.Relu, scale=sa[:, q, r:r + 1])
+                ras[q, r] = ra
+            if 4 <= r <= 10:
+                qa = bas.tile([P, B], F32, tag="qa", bufs=3)
+                nc.scalar.activation(out=qa[:], in_=vs[q, r][:], func=ACTF.Copy, scale=ka[:, q, r - 4:r - 3])
+                qas[q, r] = qa
+            if 3 <= r <= 13:
+                rb = bas.tile([P, B], F32, tag="rb", bufs=4)
+                nc.scalar.activation(out=rb[:], in_=vs[q, r][:], func=ACTF.Relu, scale=sb[:, q, r:r + 1])
+                rbs[q, r] = rb
+
+        def add_turned(out, first, second):
+            for m in range(NM):
+                for i, term in enumerate((first, second)):
+                    nc.tensor.matmul(out=out[:, m, :], lhsT=term[:, m * P:(m + 1) * P], rhs=ident_f[:],
+                                     is_transpose=True, start=(i == 0), stop=(i == 1))
+
+        def sums(q, j):
+            right = psum.tile([P, NM, P], F32, tag="right", bufs=2)
+            add_turned(right, qas[q, j + 4] if j <= 6 else vs[q, j + 4], rbs[q, j + 3])
+            left = psum.tile([P, NM, P], F32, tag="left", bufs=2)
+            add_turned(left, vs[q, j], ras[q, j + 1])
+            lefts[q, j] = left
+            rights[q, j] = right
+
+        def unload(q, j):
+            rt = bas.tile([P, NM, P], BF16, tag="rt", bufs=2)
+            nc.scalar.activation(out=rt[:], in_=rights[q, j][:], func=ACTF.Relu, scale=-1.0)
+            rights[q, j] = rt
+
+        def join(q, j):
             c, tt = divmod(q, 4)
-            sqs = {}
-            ws = {}
-            rbs = {}
-            st = {}
+            if tt == 0 and j == 0:
+                plane = big.tile([P, G, NM, 4 * P], BF16, tag="plane")
+                planes[c] = plane
+            nc.vector.scalar_tensor_tensor(out=planes[c][:, j, :, tt * P:(tt + 1) * P], in0=lefts[q, j][:], scalar=-1.0,
+                                           in1=rights[q, j][:], op0=ALU.mult, op1=ALU.max)
 
-            def square(r):
-                sq = bas.tile([P, B], F32, tag="sq", bufs=4)
-                nc.scalar.activation(out=sq[:], in_=tqs[q][:], func=ACTF.Square, bias=nroot[:, q, r:r + 1],
-                                     scale=root[:, q, r:r + 1])
-                sqs[r] = sq
+        def turn_words(source, blocks):
+            back = psum.tile([P, 2, 2, P], F32, tag="back")
+            for k, m in enumerate(blocks):
+                words = source(m).bitcast(F32)
+                for u in range(2):
+                    nc.tensor.transpose(out=back[:, k, u, :], in_=words[:, u * P:(u + 1) * P], identity=ident_f[:])
+            return back
 
-            def relu(tag, bufs, r, scale):
-                y = bas.tile([P, B], F32, tag=tag, bufs=bufs)
-                nc.scalar.activation(out=y[:], in_=ws[r][:], func=ACTF.Relu, scale=scale)
-                return y
+        def new_gb(c, j):
+            gb = bas.tile([P, B, 2], F32, tag="gb", bufs=3, align_bytes=64)
+            gbs[c, j] = gb
 
-            def lt(j):
-                return mx4s[c][:, tt, j * B:(j + 1) * B]
+        def turn_back(c, j, blocks):
+            turned[c, j, blocks] = turn_words(lambda m: planes[c][:, j, m, :], blocks)
 
-            def step(r):
-                if r == 0:
-                    rt = big.tile([P, G, B], BF16, tag="rt")
-                    st["rt"] = rt
-                    for e in range(3):
-                        square(e)
-                w = bas.tile([P, B], F32, tag="w", bufs=5)
-                nc.vector.scalar_tensor_tensor(out=w[:], in0=tps[q][:], scalar=gf[:, q, r:r + 1], in1=sqs[r][:],
-                                               op0=ALU.subtract, op1=ALU.mult)
-                ws[r] = w
-                if r + 3 < NK:
-                    square(r + 3)
-                if 1 <= r <= 11:
-                    ra = relu("ra", 2, r, kp[:, q, r - 1:r])
-                    nc.gpsimd.tensor_tensor(out=lt(r - 1), in0=ws[r - 1][:], in1=ra[:], op=ALU.subtract)
-                if r >= 4 and r - 4 not in ON_VECTOR:
-                    qa = relu("qa", 2, r, ka[:, q, r - 4:r - 3])
-                    nc.gpsimd.tensor_tensor(out=st["rt"][:, r - 4, :], in0=qa[:], in1=rbs[r - 1][:], op=ALU.subtract)
-                if r >= 5 and r - 5 in ON_VECTOR:
-                    nc.vector.scalar_tensor_tensor(out=st["rt"][:, r - 5, :], in0=ws[r - 1][:],
-                                                   scalar=ka[:, q, r - 5:r - 4], in1=rbs[r - 2][:],
-                                                   op0=ALU.mult, op1=ALU.subtract)
-                if 3 <= r <= 13:
-                    rbs[r] = relu("rb", 4, r, kb[:, q, r - 3:r - 2])
+        def group(c, j, blocks):
+            if blocks[0] == 0:
+                new_gb(c, j)
+            n = len(blocks)
+            out = gbs[c, j][:, blocks[0] * P:(blocks[0] + n) * P, :].rearrange("p (k b) u -> p k b u", k=n)
+            nc.scalar.copy(out=out, in_=turned[c, j, blocks][:, 0:n, :, :].rearrange("p k u b -> p k b u"))
 
-            def finish():
-                both = mx4s[c][:, tt, 0:G * B]
-                nc.vector.tensor_tensor(out=both, in0=both, in1=st["rt"][:].rearrange("p j b -> p (j b)"), op=ALU.max)
+        def base_block(c, m):
+            if m == 0:
+                new_gb(c, G)
+            back = turn_words(lambda k: x_sb[:, k, 4 * P * c:4 * P * (c + 1)], (m,))
+            pairs = back[:, 0, :, :].rearrange("p u b -> p (u b)").bitcast(BF16)
+            out = gbs[c, G][:, m * P:(m + 1) * P, :].rearrange("p b u -> p (b u)").bitcast(BF16)
+            nc.scalar.activation(out=out.rearrange("p (b u e) -> p b u e", u=2, e=2),
+                                 in_=pairs.rearrange("p (u b e) -> p b u e", u=2, e=2), func=ACTF.Silu, scale=-1.0)
 
-            return [bind(step, r) for r in range(NK)], finish
-
-        def group_steps(c):
-            gbs = {}
-            pieces = [(w, 256) for w in range(0, 4096, 256)] + [(4096, 128), (4224, 256), (4480, 128)]
-
-            def group(i):
-                w0, wn = pieces[i]
-                gb = bas.tile([P, 256, 4], BF16, tag="gb", bufs=2, align_bytes=64)
-                source = mx4s[c][:, :, w0:w0 + wn].rearrange("p t w -> p w t")
-                if w0 < G * B:
-                    nc.scalar.activation(out=gb[:, 0:wn, :], in_=source, func=ACTF.Relu)
-                else:
-                    nc.scalar.copy(out=gb[:, 0:wn, :], in_=source)
-                gbs[i] = gb
-
-            def quantise(i):
-                w0, wn = pieces[i]
-                nc.vector.quantize_mx(out=bs_codes[:, c, w0:w0 + wn].bitcast(FP8X4),
-                                      scales=bs_scales[:, c, w0:w0 + wn],
-                                      in_=gbs[i][:, 0:wn, :].rearrange("p w t -> p (w t)"))
-
-            def step(i):
-                if i < len(pieces):
-                    group(i)
-                if i > 0:
-                    quantise(i - 1)
-
-            return [bind(step, i) for i in range(len(pieces) + 1)]
+        def quantise_basis(c, j):
+            for b0, bn in ((0, 256), (256, 128)):
+                w0 = j * B + b0
+                nc.vector.quantize_mx(out=bs_codes[:, w0:w0 + bn].bitcast(FP8X4), scales=bs_scales[:, w0:w0 + bn],
+                                      in_=gbs[c, j][:, b0:b0 + bn, :].rearrange("p b u -> p (b u)").bitcast(BF16))
 
         def load(n):
             c, ob = divmod(n, NOB)
-            qsl = slice(4 * c, 4 * c + 4)
             osl = slice(ob * OB, (ob + 1) * OB)
             mk = wts.tile([P, 4, OB], BF16, tag="mk")
-            nc.sync.dma_start(out=mk[:], in_=mask_v[:, qsl, osl])
             sps = wts.tile([P, 4, OB], BF16, tag="sps")
-            nc.sync.dma_start(out=sps[:], in_=sp_v[:, qsl, osl])
             sbs = wts.tile([P, 4, OB], BF16, tag="sbs")
-            nc.sync.dma_start(out=sbs[:], in_=sb_v[:, qsl, osl])
             ct = wts.tile([P, 4, OB * G], BF16, tag="ct", bufs=2)
-            nc.sync.dma_start(out=ct[:], in_=coef_v[:, qsl, ob * OB * G:(ob + 1) * OB * G])
+            for dst, view, cols in ((mk, mask_v, osl), (sps, sp_v, osl), (sbs, sb_v, osl),
+                                     (ct, coef_v, slice(ob * OB * G, (ob + 1) * OB * G))):
+                for u in range(2):
+                    nc.sync.dma_start(out=dst[:, 2 * u:2 * u + 2, :], in_=view[:, 2 * c + u, :, cols])
             cts[n] = (ct, mk, sps, sbs)
 
         def prep(n):
             ct, mk, sps, sbs = cts[n]
-            ms = wts.tile([P, 4, OB], F32, tag="ms", bufs=1)
+            ms = wts.tile([P, 4, OB], F32, tag="ms")
             nc.vector.tensor_tensor(out=ms[:], in0=mk[:], in1=sps[:], op=ALU.mult)
-            ms_ps = psum.tile([P, OB, 4], F32, tag="ms_ps", bufs=2)
-            nc.tensor.matmul(out=ms_ps[:].rearrange("p o t -> p (o t)"), lhsT=ident_f[:],
-                             rhs=ms[:].rearrange("p t o -> p o t"), start=True, stop=True)
             wbn = wts.tile([P, 4, OB], BF16, tag="wbn")
             nc.vector.tensor_tensor(out=wbn[:], in0=mk[:], in1=sbs[:], op=ALU.mult)
-            mss[n] = (ms_ps, wbn)
+            mss[n] = (ms, wbn)
 
         def new_gw(n, k):
             gw = wts.tile([P, 4, OB, 4], BF16, tag="gw", bufs=3, align_bytes=64)
@@ -257,9 +272,10 @@ def tile_kan_layer_kernel(tc, x, grid, coef, scale_base, scale_sp, mask, out):
             ng = min(4, G - 4 * k)
             gw = gws[n, k] if (n, k) in gws else new_gw(n, k)
             ct_v = cts[n][0][:].rearrange("p t (o g) -> p o t g", g=G)
+            ms_v = mss[n][0][:].rearrange("p t o -> p o t").unsqueeze(3)
             nc.vector.tensor_tensor(out=gw[:, 0:ng, :, :].rearrange("p g o t -> p o t g"),
                                     in0=ct_v[:, :, :, 4 * k:4 * k + ng],
-                                    in1=mss[n][0][:].unsqueeze(3).to_broadcast([P, OB, 4, ng]), op=ALU.mult)
+                                    in1=ms_v.to_broadcast([P, OB, 4, ng]), op=ALU.mult)
             if k == 1:
                 gw2 = new_gw(n, 2)
                 nc.scalar.copy(out=gw2[:, 3, :, :], in_=mss[n][1][:].rearrange("p t o -> p o t"))
@@ -270,46 +286,30 @@ def tile_kan_layer_kernel(tc, x, grid, coef, scale_base, scale_sp, mask, out):
             nc.vector.quantize_mx(out=wc[:].bitcast(FP8X4), scales=ws[:],
                                   in_=gws[n, k][:].rearrange("p g o t -> p (g o t)"))
             wcs[n, k] = (wc, ws)
-            pending[n, k] = True
 
-        def flush(most):
-            for n, k in list(pending):
-                if most and pending[n, k] and n // NOB in ready:
-                    pending[n, k] = False
-                    multiply(n, k)
-                    most -= 1
-
-        def multiply(n, k):
-            c = n // NOB
-            if k == 0:
-                if n > 0:
-                    empty(n - 1)
-                accd[n] = []
-                for m in range(NM):
-                    am = psum.tile([P, OB], F32, tag="acc%d" % m)
-                    accd[n].append(am)
-            wc, ws = wcs[n, k]
-            for gi in range(4):
-                pl = 4 * k + gi
-                for m in range(NM):
+        def multiply(n):
+            acc = psum.tile([P, NM, OB], F32, tag="acc", bufs=2)
+            for m in range(NM):
+                for pl in range(NPL):
+                    wc, ws = wcs[n, pl // 4]
                     l0 = pl * B + m * P
-                    nc.tensor.matmul_mx(out=accd[n][m][:],
-                                        lhsT=bs_codes[:, c, l0:l0 + P].bitcast(FP8X4),
-                                        lhsT_scale=bs_scales[:, c, l0:l0 + P],
-                                        rhs=wc[:, gi * OB:(gi + 1) * OB].bitcast(FP8X4),
-                                        rhs_scale=ws[:, gi * OB:(gi + 1) * OB],
+                    r0 = pl % 4 * OB
+                    nc.tensor.matmul_mx(out=acc[:, m, :],
+                                        lhsT=bs_codes[:, l0:l0 + P].bitcast(FP8X4),
+                                        lhsT_scale=bs_scales[:, l0:l0 + P],
+                                        rhs=wc[:, r0:r0 + OB].bitcast(FP8X4),
+                                        rhs_scale=ws[:, r0:r0 + OB],
                                         start=(pl == 0), stop=(pl == NPL - 1))
+            accd[n] = acc
 
         def empty(n):
             c, ob = divmod(n, NOB)
             osl = slice(ob * OB, (ob + 1) * OB)
             if c == 0:
-                for m in range(NM):
-                    nc.scalar.copy(out=accs[:, m, osl], in_=accd[n][m][:])
+                nc.scalar.copy(out=accs[:, :, osl], in_=accd[n][:])
             else:
                 ot = wts.tile([P, NM, OB], F32, tag="ot", bufs=1)
-                for m in range(NM):
-                    nc.vector.tensor_tensor(out=ot[:, m, :], in0=accd[n][m][:], in1=accs[:, m, osl], op=ALU.add)
+                nc.vector.tensor_tensor(out=ot[:], in0=accd[n][:], in1=accs[:, :, osl], op=ALU.add)
                 nc.sync.dma_start(out=out_v[:, :, osl], in_=ot[:])
 
         units = [(n, k) for n in range(2 * NOB) for k in range(3)]
@@ -327,54 +327,87 @@ def tile_kan_layer_kernel(tc, x, grid, coef, scale_base, scale_sp, mask, out):
                 if i > 0:
                     quant(*units[i - 1])
 
-            def third():
-                prep(n + 1)
-
             weight_steps.extend([first, second])
             if k == 1 and n + 1 < 2 * NOB:
-                weight_steps.append(third)
+                weight_steps.append(bind(prep, n + 1))
 
         for i in range(len(units)):
             add_unit(i)
         weight_steps.append(bind(quant, *units[-1]))
 
-        woven = [0]
+        done = {"steps": 0, "multiplied": 0, "emptied": 0}
 
-        def weave(count, others):
-            start = woven[0]
-            stop = min(start + count, len(weight_steps))
-            woven[0] = stop
-            done = 0
-            for i in range(start, stop):
-                weight_steps[i]()
-                flush(2)
-                upto = (i + 1 - start) * len(others) // (stop - start)
-                while done < upto:
-                    others[done]()
-                    done += 1
+        def flush():
+            n = done["multiplied"]
+            if done["emptied"] < n - (done["steps"] % 2):
+                empty(done["emptied"])
+                done["emptied"] += 1
+            if done["steps"] % 2 == 0 and (n, 2) in wcs and n // NOB in ready:
+                multiply(n)
+                done["multiplied"] = n + 1
 
+        def run_weights(upto):
+            while done["steps"] < min(upto, len(weight_steps)):
+                weight_steps[done["steps"]]()
+                done["steps"] += 1
+                flush()
+
+        events = [[] for i in range(15 * NQ + 8)]
+        cost = [0 for i in range(15 * NQ + 8)]
+
+        def at(i, passes, f, *args):
+            i = max(i, 0)
+            events[i].append(bind(f, *args))
+            cost[i] += passes
+
+        for q in range(NQ):
+            c, tt = divmod(q, 4)
+            at(15 * q - 7, 0, begin, q)
+        for q in range(NQ):
+            c, tt = divmod(q, 4)
+            for r in range(NK):
+                i = 15 * q + r
+                at(i - 3, 1, square, q, r)
+        for q in range(NQ):
+            c, tt = divmod(q, 4)
+            for r in range(NK):
+                i = 15 * q + r
+                if r >= 4:
+                    j = r - 4
+                    at(i + 1, 0, sums, q, j)
+                    at(i + 2, 1, unload, q, j)
+                    at(i + 3, 0, join, q, j)
+                    if tt == 3:
+                        for k, blocks in enumerate(((0, 1), (2,))):
+                            at(i + 4 + k, 0, turn_back, c, j, blocks)
+                            at(i + 4 + k, 0.7 * len(blocks), group, c, j, blocks)
+                        at(i + 6, 0, quantise_basis, c, j)
+                at(i, 0, cube, q, r)
+                at(i, (1 <= r <= 11) + (4 <= r <= 10) + (3 <= r <= 13), terms, q, r)
+            if tt == 3:
+                for m in range(NM):
+                    at(15 * q - 5 + 2 * m, 1.4, base_block, c, m)
+                at(15 * q + 1, 0, quantise_basis, c, G)
+                at(15 * q + 22, 0, ready.append, c)
+
+        half = sum(cost[0:15 * 4 + 8])
+        total = sum(cost)
         load(0)
         load(1)
-        for q in range(2):
-            turn(q)
-            clamp(q)
         prep(0)
-        waiting = []
-        for c in range(2):
-            for q in range(4 * c, 4 * c + 4):
-                steps, finish = basis_steps(q)
-                weave(STEPS[c], waiting + steps)
-                waiting = [finish]
-                if q + 2 < 8:
-                    turn(q + 2)
-                    if q + 2 != 4 and q + 2 != 5:
-                        clamp(q + 2)
-            weave(14, waiting + group_steps(c))
-            waiting = []
-            ready.append(c)
-            if c == 0:
-                clamp(4)
-                clamp(5)
-        weave(len(weight_steps), [])
-        flush(len(pending))
-        empty(2 * NOB - 1)
+        spent = 0
+        for i in range(len(events)):
+            for f in events[i]:
+                f()
+            spent += cost[i]
+            if spent <= half:
+                run_weights(STEPS[0] * spent // half)
+            else:
+                run_weights(STEPS[0] + STEPS[1] * (spent - half) // (total - half))
+        run_weights(len(weight_steps))
+        while done["emptied"] < 2 * NOB:
+            if done["multiplied"] < 2 * NOB:
+                multiply(done["multiplied"])
+                done["multiplied"] += 1
+            empty(done["emptied"])
+            done["emptied"] += 1

@@ -24,8 +24,10 @@ NM = B // P
 NPL = G + 1
 OB = 128
 NOB = O // OB
-NWC = 22
-STEPS = (51, 48)
+ON_TENSOR = (1, 3, 5, 7, 8, 9, 10)
+ON_VECTOR = (0, 2, 4, 6)
+NWC = 19
+STEPS = ((69, 44), (120, 36), (129, 14))
 PW = NPL * B
 
 FLOPS = 2 * B * I * O * NPL
@@ -33,10 +35,10 @@ FLOPS = 2 * B * I * O * NPL
 
 def tile_kan_layer_kernel(tc, x, grid, coef, scale_base, scale_sp, mask, out):
     nc = tc.nc
-    coef_v = coef.rearrange("(h p e) o g -> p h e (o g)", p=P, e=2)
-    mask_v = mask.rearrange("(h p e) o -> p h e o", p=P, e=2)
-    sp_v = scale_sp.rearrange("(h p e) o -> p h e o", p=P, e=2)
-    sb_v = scale_base.rearrange("(h p e) o -> p h e o", p=P, e=2)
+    coef_v = coef.rearrange("(q p) o g -> p q (o g)", p=P)
+    mask_v = mask.rearrange("(q p) o -> p q o", p=P)
+    sp_v = scale_sp.rearrange("(q p) o -> p q o", p=P)
+    sb_v = scale_base.rearrange("(q p) o -> p q o", p=P)
     out_v = out.rearrange("(m p) o -> p m o", p=P)
 
     with ExitStack() as ctx:
@@ -120,7 +122,11 @@ def tile_kan_layer_kernel(tc, x, grid, coef, scale_base, scale_sp, mask, out):
         def bind(f, *args):
             return lambda: f(*args)
 
+        tps = {}
         tns = {}
+        bases = {}
+        nears = {}
+        others = {}
         tqs = {}
         planes = {}
         sqs = {}
@@ -139,15 +145,24 @@ def tile_kan_layer_kernel(tc, x, grid, coef, scale_base, scale_sp, mask, out):
         accd = {}
         ready = []
 
-        def begin(q):
+        def turn(q):
             tp = psum.tile([P, B], BF16, tag="tp")
             for m in range(NM):
                 nc.tensor.transpose(out=tp[:, m * P:(m + 1) * P], in_=x_sb[:, m, q * P:(q + 1) * P], identity=ident[:])
+            tps[q] = tp
+
+        def begin(q):
+            c, tt = divmod(q, 4)
+            tp = tps[q]
+            if tt == 0:
+                base = bas.tile([P, 4, B], BF16, tag="base", bufs=1)
+                bases[c] = base
             tn = bas.tile([P, B], BF16, tag="tn", bufs=2)
             nc.vector.tensor_scalar(out=tn[:], in0=tp[:], scalar1=negg[:, q, 14:15], scalar2=negg[:, q, 0:1],
                                     op0=ALU.max, op1=ALU.min)
             tq = bas.tile([P, B], BF16, tag="tq", bufs=2)
             nc.vector.tensor_scalar(out=tq[:], in0=tn[:], scalar1=-1.0, scalar2=None, op0=ALU.mult)
+            nc.scalar.activation(out=bases[c][:, tt, :], in_=tp[:], func=ACTF.Silu, scale=-1.0)
             tns[q] = tn
             tqs[q] = tq
 
@@ -169,26 +184,25 @@ def tile_kan_layer_kernel(tc, x, grid, coef, scale_base, scale_sp, mask, out):
                 ra = bas.tile([P, B], F32, tag="ra", bufs=6)
                 nc.scalar.activation(out=ra[:], in_=vs[q, r][:], func=ACTF.Relu, scale=sa[:, q, r:r + 1])
                 ras[q, r] = ra
-            if 4 <= r <= 10:
+            if 4 <= r <= 10 and r - 4 in ON_TENSOR:
                 qa = bas.tile([P, B], F32, tag="qa", bufs=3)
                 nc.scalar.activation(out=qa[:], in_=vs[q, r][:], func=ACTF.Copy, scale=ka[:, q, r - 4:r - 3])
                 qas[q, r] = qa
             if 3 <= r <= 13:
-                rb = bas.tile([P, B], F32, tag="rb", bufs=4)
+                rb = bas.tile([P, B], F32, tag="rb", bufs=5)
                 nc.scalar.activation(out=rb[:], in_=vs[q, r][:], func=ACTF.Relu, scale=sb[:, q, r:r + 1])
                 rbs[q, r] = rb
 
-        def add_turned(out, first, second):
-            for m in range(NM):
-                for i, term in enumerate((first, second)):
-                    nc.tensor.matmul(out=out[:, m, :], lhsT=term[:, m * P:(m + 1) * P], rhs=ident_f[:],
-                                     is_transpose=True, start=(i == 0), stop=(i == 1))
-
         def sums(q, j):
             right = psum.tile([P, NM, P], F32, tag="right", bufs=2)
-            add_turned(right, qas[q, j + 4] if j <= 6 else vs[q, j + 4], rbs[q, j + 3])
-            left = psum.tile([P, NM, P], F32, tag="left", bufs=2)
-            add_turned(left, vs[q, j], ras[q, j + 1])
+            left = psum.tile([P, NM, P], F32, tag="left", bufs=3)
+            right_terms = (qas[q, j + 4] if j <= 6 else vs[q, j + 4], rbs[q, j + 3])
+            left_terms = (vs[q, j], ras[q, j + 1])
+            for m in range(NM):
+                for i in range(2):
+                    for out, terms in ((right, right_terms), (left, left_terms)):
+                        nc.tensor.matmul(out=out[:, m, :], lhsT=terms[i][:, m * P:(m + 1) * P], rhs=ident_f[:],
+                                         is_transpose=True, start=(i == 0), stop=(i == 1))
             lefts[q, j] = left
             rights[q, j] = right
 
@@ -199,60 +213,79 @@ def tile_kan_layer_kernel(tc, x, grid, coef, scale_base, scale_sp, mask, out):
 
         def join(q, j):
             c, tt = divmod(q, 4)
-            if tt == 0 and j == 0:
-                plane = big.tile([P, G, NM, 4 * P], BF16, tag="plane")
+            if tt == 0 and j == ON_TENSOR[0]:
+                plane = big.tile([P, len(ON_TENSOR), NM, 4 * P], BF16, tag="plane")
                 planes[c] = plane
-            nc.vector.scalar_tensor_tensor(out=planes[c][:, j, :, tt * P:(tt + 1) * P], in0=lefts[q, j][:], scalar=-1.0,
+            out = planes[c][:, ON_TENSOR.index(j), :, tt * P:(tt + 1) * P]
+            nc.vector.scalar_tensor_tensor(out=out, in0=lefts[q, j][:], scalar=-1.0,
                                            in1=rights[q, j][:], op0=ALU.mult, op1=ALU.max)
 
-        def turn_words(source, blocks):
-            back = psum.tile([P, 2, 2, P], F32, tag="back")
-            for k, m in enumerate(blocks):
-                words = source(m).bitcast(F32)
-                for u in range(2):
-                    nc.tensor.transpose(out=back[:, k, u, :], in_=words[:, u * P:(u + 1) * P], identity=ident_f[:])
-            return back
+        def left_on_vector(q, j):
+            c, tt = divmod(q, 4)
+            if j == ON_VECTOR[0]:
+                if tt == 0:
+                    near = big.tile([P, 4, len(ON_VECTOR), B], BF16, tag="near")
+                    nears[c] = near
+                other = big.tile([P, len(ON_VECTOR), B], BF16, tag="other")
+                others[q] = other
+            nc.vector.tensor_tensor(out=nears[c][:, tt, ON_VECTOR.index(j), :], in0=vs[q, j][:], in1=ras[q, j + 1][:],
+                                    op=ALU.add)
 
-        def new_gb(c, j):
-            gb = bas.tile([P, B, 2], F32, tag="gb", bufs=3, align_bytes=64)
-            gbs[c, j] = gb
+        def right_on_vector(q, j):
+            nc.vector.scalar_tensor_tensor(out=others[q][:, ON_VECTOR.index(j), :], in0=vs[q, j + 4][:],
+                                           scalar=ka[:, q, j:j + 1], in1=rbs[q, j + 3][:], op0=ALU.mult, op1=ALU.add)
+
+        def join_on_vector(q):
+            c, tt = divmod(q, 4)
+            both = nears[c][:, tt, :, :]
+            nc.vector.tensor_tensor(out=both, in0=both, in1=others[q][:], op=ALU.min)
 
         def turn_back(c, j, blocks):
-            turned[c, j, blocks] = turn_words(lambda m: planes[c][:, j, m, :], blocks)
+            back = psum.tile([P, 2, 4, P], BF16, tag="back")
+            for k, m in enumerate(blocks):
+                for tt in range(4):
+                    nc.tensor.transpose(out=back[:, k, tt, :],
+                                        in_=planes[c][:, ON_TENSOR.index(j), m, tt * P:(tt + 1) * P], identity=ident[:])
+            turned[c, j, blocks] = back
+
+        def new_gb(c, j):
+            gb = bas.tile([P, B, 4], BF16, tag="gb", bufs=3, align_bytes=64)
+            gbs[c, j] = gb
 
         def group(c, j, blocks):
             if blocks[0] == 0:
                 new_gb(c, j)
             n = len(blocks)
-            out = gbs[c, j][:, blocks[0] * P:(blocks[0] + n) * P, :].rearrange("p (k b) u -> p k b u", k=n)
-            nc.scalar.copy(out=out, in_=turned[c, j, blocks][:, 0:n, :, :].rearrange("p k u b -> p k b u"))
+            out = gbs[c, j][:, blocks[0] * P:(blocks[0] + n) * P, :].rearrange("p (k b) t -> p k b t", k=n)
+            nc.scalar.copy(out=out, in_=turned[c, j, blocks][:, 0:n, :, :].rearrange("p k t b -> p k b t"))
 
-        def base_block(c, m):
-            if m == 0:
-                new_gb(c, G)
-            back = turn_words(lambda k: x_sb[:, k, 4 * P * c:4 * P * (c + 1)], (m,))
-            pairs = back[:, 0, :, :].rearrange("p u b -> p (u b)").bitcast(BF16)
-            out = gbs[c, G][:, m * P:(m + 1) * P, :].rearrange("p b u -> p (b u)").bitcast(BF16)
-            nc.scalar.activation(out=out.rearrange("p (b u e) -> p b u e", u=2, e=2),
-                                 in_=pairs.rearrange("p (u b e) -> p b u e", u=2, e=2), func=ACTF.Silu, scale=-1.0)
+        def group_near(c, j):
+            new_gb(c, j)
+            nc.scalar.activation(out=gbs[c, j][:], in_=nears[c][:, :, ON_VECTOR.index(j), :].rearrange("p t b -> p b t"),
+                                 func=ACTF.Relu, scale=-1.0)
+
+        def group_base(c):
+            new_gb(c, G)
+            nc.scalar.copy(out=gbs[c, G][:], in_=bases[c][:].rearrange("p t b -> p b t"))
 
         def quantise_basis(c, j):
             for b0, bn in ((0, 256), (256, 128)):
                 w0 = j * B + b0
                 nc.vector.quantize_mx(out=bs_codes[:, w0:w0 + bn].bitcast(FP8X4), scales=bs_scales[:, w0:w0 + bn],
-                                      in_=gbs[c, j][:, b0:b0 + bn, :].rearrange("p b u -> p (b u)").bitcast(BF16))
+                                      in_=gbs[c, j][:, b0:b0 + bn, :].rearrange("p b t -> p (b t)"))
 
         def load(n):
             c, ob = divmod(n, NOB)
+            qsl = slice(4 * c, 4 * c + 4)
             osl = slice(ob * OB, (ob + 1) * OB)
             mk = wts.tile([P, 4, OB], BF16, tag="mk")
+            nc.sync.dma_start(out=mk[:], in_=mask_v[:, qsl, osl])
             sps = wts.tile([P, 4, OB], BF16, tag="sps")
+            nc.sync.dma_start(out=sps[:], in_=sp_v[:, qsl, osl])
             sbs = wts.tile([P, 4, OB], BF16, tag="sbs")
+            nc.sync.dma_start(out=sbs[:], in_=sb_v[:, qsl, osl])
             ct = wts.tile([P, 4, OB * G], BF16, tag="ct", bufs=2)
-            for dst, view, cols in ((mk, mask_v, osl), (sps, sp_v, osl), (sbs, sb_v, osl),
-                                     (ct, coef_v, slice(ob * OB * G, (ob + 1) * OB * G))):
-                for u in range(2):
-                    nc.sync.dma_start(out=dst[:, 2 * u:2 * u + 2, :], in_=view[:, 2 * c + u, :, cols])
+            nc.sync.dma_start(out=ct[:], in_=coef_v[:, qsl, ob * OB * G:(ob + 1) * OB * G])
             cts[n] = (ct, mk, sps, sbs)
 
         def prep(n):
@@ -288,7 +321,7 @@ def tile_kan_layer_kernel(tc, x, grid, coef, scale_base, scale_sp, mask, out):
             wcs[n, k] = (wc, ws)
 
         def multiply(n):
-            acc = psum.tile([P, NM, OB], F32, tag="acc", bufs=2)
+            acc = psum.tile([P, NM, OB], F32, tag="acc", bufs=1)
             for m in range(NM):
                 for pl in range(NPL):
                     wc, ws = wcs[n, pl // 4]
@@ -308,8 +341,9 @@ def tile_kan_layer_kernel(tc, x, grid, coef, scale_base, scale_sp, mask, out):
             if c == 0:
                 nc.scalar.copy(out=accs[:, :, osl], in_=accd[n][:])
             else:
-                ot = wts.tile([P, NM, OB], F32, tag="ot", bufs=1)
-                nc.vector.tensor_tensor(out=ot[:], in0=accd[n][:], in1=accs[:, :, osl], op=ALU.add)
+                ot = wts.tile([P, NM, OB], F32, tag="ot", bufs=2)
+                nc.scalar.copy(out=ot[:], in_=accd[n][:])
+                nc.gpsimd.tensor_tensor(out=ot[:], in0=ot[:], in1=accs[:, :, osl], op=ALU.add)
                 nc.sync.dma_start(out=out_v[:, :, osl], in_=ot[:])
 
         units = [(n, k) for n in range(2 * NOB) for k in range(3)]
@@ -339,10 +373,12 @@ def tile_kan_layer_kernel(tc, x, grid, coef, scale_base, scale_sp, mask, out):
 
         def flush():
             n = done["multiplied"]
-            if done["emptied"] < n - (done["steps"] % 2):
-                empty(done["emptied"])
-                done["emptied"] += 1
-            if done["steps"] % 2 == 0 and (n, 2) in wcs and n // NOB in ready:
+            e = done["emptied"]
+            if done["steps"] % 2:
+                if e < n:
+                    empty(e)
+                    done["emptied"] = e + 1
+            elif (n, 2) in wcs and n // NOB in ready:
                 multiply(n)
                 done["multiplied"] = n + 1
 
@@ -352,8 +388,8 @@ def tile_kan_layer_kernel(tc, x, grid, coef, scale_base, scale_sp, mask, out):
                 done["steps"] += 1
                 flush()
 
-        events = [[] for i in range(15 * NQ + 8)]
-        cost = [0 for i in range(15 * NQ + 8)]
+        events = [[] for i in range(15 * NQ + 9)]
+        cost = [0 for i in range(15 * NQ + 9)]
 
         def at(i, passes, f, *args):
             i = max(i, 0)
@@ -362,7 +398,8 @@ def tile_kan_layer_kernel(tc, x, grid, coef, scale_base, scale_sp, mask, out):
 
         for q in range(NQ):
             c, tt = divmod(q, 4)
-            at(15 * q - 7, 0, begin, q)
+            at(15 * q - 9, 0, turn, q)
+            at(15 * q - 6, 0, begin, q)
         for q in range(NQ):
             c, tt = divmod(q, 4)
             for r in range(NK):
@@ -372,42 +409,49 @@ def tile_kan_layer_kernel(tc, x, grid, coef, scale_base, scale_sp, mask, out):
             c, tt = divmod(q, 4)
             for r in range(NK):
                 i = 15 * q + r
-                if r >= 4:
+                if 1 <= r <= 11 and r - 1 in ON_VECTOR:
+                    at(i + 3, 0, left_on_vector, q, r - 1)
+                if r >= 4 and r - 4 in ON_VECTOR:
+                    at(i + 2, 0, right_on_vector, q, r - 4)
+                    if r - 4 == ON_VECTOR[-1]:
+                        at(i + 4, 0, join_on_vector, q)
+                        if tt == 3:
+                            for k, j in enumerate(ON_VECTOR):
+                                at(i + 5 + k, 4.5, group_near, c, j)
+                                at(i + 6 + k, 0, quantise_basis, c, j)
+                if r >= 4 and r - 4 in ON_TENSOR:
                     j = r - 4
                     at(i + 1, 0, sums, q, j)
                     at(i + 2, 1, unload, q, j)
-                    at(i + 3, 0, join, q, j)
+                    at(i + 4, 0, join, q, j)
                     if tt == 3:
                         for k, blocks in enumerate(((0, 1), (2,))):
-                            at(i + 4 + k, 0, turn_back, c, j, blocks)
-                            at(i + 4 + k, 0.7 * len(blocks), group, c, j, blocks)
-                        at(i + 6, 0, quantise_basis, c, j)
+                            at(i + 5 + k, 0, turn_back, c, j, blocks)
+                            at(i + 5 + k, 1.4 * len(blocks), group, c, j, blocks)
+                        at(i + 7, 0, quantise_basis, c, j)
                 at(i, 0, cube, q, r)
-                at(i, (1 <= r <= 11) + (4 <= r <= 10) + (3 <= r <= 13), terms, q, r)
+                at(i, (1 <= r <= 11) + (4 <= r <= 10 and r - 4 in ON_TENSOR) + (3 <= r <= 13), terms, q, r)
             if tt == 3:
-                for m in range(NM):
-                    at(15 * q - 5 + 2 * m, 1.4, base_block, c, m)
-                at(15 * q + 1, 0, quantise_basis, c, G)
-                at(15 * q + 22, 0, ready.append, c)
+                at(15 * q - 5, 4.5, group_base, c)
+                at(15 * q - 3, 0, quantise_basis, c, G)
+                at(15 * q + 23, 0, ready.append, c)
 
-        half = sum(cost[0:15 * 4 + 8])
-        total = sum(cost)
         load(0)
         load(1)
         prep(0)
-        spent = 0
-        for i in range(len(events)):
-            for f in events[i]:
-                f()
-            spent += cost[i]
-            if spent <= half:
-                run_weights(STEPS[0] * spent // half)
-            else:
-                run_weights(STEPS[0] + STEPS[1] * (spent - half) // (total - half))
+        first = 0
+        before = 0
+        for last_event, count in STEPS:
+            whole = sum(cost[first:last_event])
+            spent = 0
+            for i in range(first, last_event):
+                for f in events[i]:
+                    f()
+                spent += cost[i]
+                run_weights(before + count * spent // whole)
+            first = last_event
+            before += count
         run_weights(len(weight_steps))
         while done["emptied"] < 2 * NOB:
-            if done["multiplied"] < 2 * NOB:
-                multiply(done["multiplied"])
-                done["multiplied"] += 1
-            empty(done["emptied"])
-            done["emptied"] += 1
+            done["steps"] += 1
+            flush()

@@ -26,8 +26,8 @@ OB = 128
 NOB = O // OB
 ON_TENSOR = (1, 3, 5, 7, 8, 9, 10)
 ON_VECTOR = (0, 2, 4, 6)
-NWC = 19
-STEPS = ((69, 44), (120, 36), (129, 14))
+NWC = 18
+STEPS = ((69, 42), (120, 37), (129, 14))
 PW = NPL * B
 
 FLOPS = 2 * B * I * O * NPL
@@ -67,7 +67,9 @@ def tile_kan_layer_kernel(tc, x, grid, coef, scale_base, scale_sp, mask, out):
         d4 = const.tile([P, NQ, 16], F32)
         ca = const.tile([P, NQ, 16], F32)
         cc = const.tile([P, NQ, 16], F32)
-        r1 = const.tile([P, NQ, 16], F32)
+        e23 = const.tile([P, NQ, 16], F32)
+        f32 = const.tile([P, NQ, 16], F32)
+        sroot = const.tile([P, NQ, 16], F32)
         negk = const.tile([P, NQ, 16], F32)
         negl = const.tile([P, NQ, 16], F32)
         root = const.tile([P, NQ, 16], F32)
@@ -83,28 +85,30 @@ def tile_kan_layer_kernel(tc, x, grid, coef, scale_base, scale_sp, mask, out):
         nc.vector.tensor_tensor(out=d2[:, :, 0:13], in0=gf[:, :, 2:15], in1=gf[:, :, 0:13], op=ALU.subtract)
         nc.vector.tensor_tensor(out=d3[:, :, 0:12], in0=gf[:, :, 3:15], in1=gf[:, :, 0:12], op=ALU.subtract)
         nc.vector.tensor_tensor(out=d4[:, :, 0:11], in0=gf[:, :, 4:15], in1=gf[:, :, 0:11], op=ALU.subtract)
-        nc.vector.tensor_tensor(out=ca[:, :, 0:12], in0=d1[:, :, 0:12], in1=d2[:, :, 0:12], op=ALU.mult)
-        nc.vector.tensor_tensor(out=ca[:, :, 0:12], in0=ca[:, :, 0:12], in1=d3[:, :, 0:12], op=ALU.mult)
-        nc.vector.reciprocal(out=ca[:, :, 0:12], in_=ca[:, :, 0:12])
-        nc.vector.tensor_tensor(out=cc[:, :, 0:12], in0=d3[:, :, 0:12], in1=d2[:, :, 1:13], op=ALU.mult)
-        nc.vector.scalar_tensor_tensor(out=cc[:, :, 0:12], in0=cc[:, :, 0:12], scalar=-1.0, in1=d1[:, :, 2:14],
+        nc.vector.tensor_tensor(out=e23[:, :, 0:12], in0=d2[:, :, 0:12], in1=d3[:, :, 0:12], op=ALU.mult)
+        nc.vector.tensor_tensor(out=f32[:, :, 0:12], in0=d3[:, :, 0:12], in1=d2[:, :, 1:13], op=ALU.mult)
+        nc.vector.tensor_tensor(out=rsig[:, :, 0:12], in0=e23[:, :, 0:12], in1=d1[:, :, 0:12], op=ALU.mult)
+        nc.vector.scalar_tensor_tensor(out=cc[:, :, 0:12], in0=f32[:, :, 0:12], scalar=-1.0, in1=d1[:, :, 2:14],
                                        op0=ALU.mult, op1=ALU.mult)
+        nc.vector.reciprocal(out=ca[:, :, 0:12], in_=rsig[:, :, 0:12])
+        nc.vector.tensor_scalar(out=rsig[:, :, 11:15], in0=cc[:, :, 8:12], scalar1=-1.0, scalar2=None, op0=ALU.mult)
         nc.vector.reciprocal(out=cc[:, :, 0:12], in_=cc[:, :, 0:12])
-        nc.vector.reciprocal(out=r1[:, :, 0:14], in_=d1[:, :, 0:14])
-        nc.vector.scalar_tensor_tensor(out=negk[:, :, 0:11], in0=d4[:, :, 0:11], scalar=-1.0, in1=r1[:, :, 0:11],
-                                       op0=ALU.mult, op1=ALU.mult)
-        nc.vector.scalar_tensor_tensor(out=negl[:, :, 0:11], in0=d4[:, :, 0:11], scalar=-1.0, in1=r1[:, :, 3:14],
-                                       op0=ALU.mult, op1=ALU.mult)
         nc.vector.tensor_copy(out=sig[:, :, 0:11], in_=ca[:, :, 0:11])
         nc.vector.tensor_scalar(out=sig[:, :, 11:15], in0=cc[:, :, 8:12], scalar1=-1.0, scalar2=None, op0=ALU.mult)
-        nc.scalar.activation(out=rsig[:, :, 0:15], in_=sig[:, :, 0:15], func=ACTF.Sqrt)
-        nc.vector.reciprocal(out=root[:, :, 0:15], in_=rsig[:, :, 0:15])
-        nc.vector.tensor_tensor(out=root[:, :, 0:15], in0=root[:, :, 0:15], in1=sig[:, :, 0:15], op=ALU.mult)
-        nc.vector.tensor_tensor(out=root[:, :, 0:15], in0=root[:, :, 0:15], in1=rsig[:, :, 0:15], op=ALU.add)
-        nc.vector.tensor_scalar(out=root[:, :, 0:15], in0=root[:, :, 0:15], scalar1=0.5, scalar2=None, op0=ALU.mult)
+        nc.scalar.activation(out=sroot[:, :, 0:15], in_=sig[:, :, 0:15], func=ACTF.Sqrt)
+        nc.vector.scalar_tensor_tensor(out=negk[:, :, 0:11], in0=d4[:, :, 0:11], scalar=-1.0, in1=ca[:, :, 0:11],
+                                       op0=ALU.mult, op1=ALU.mult)
+        nc.vector.tensor_tensor(out=negl[:, :, 0:11], in0=d4[:, :, 0:11], in1=cc[:, :, 1:12], op=ALU.mult)
+        nc.vector.tensor_tensor(out=negk[:, :, 0:11], in0=negk[:, :, 0:11], in1=e23[:, :, 0:11], op=ALU.mult)
+        nc.vector.tensor_tensor(out=negl[:, :, 0:11], in0=negl[:, :, 0:11], in1=f32[:, :, 1:12], op=ALU.mult)
+        for s, better in ((sroot, root), (root, sroot)):
+            nc.vector.tensor_tensor(out=d1[:, :, 0:15], in0=s[:, :, 0:15], in1=s[:, :, 0:15], op=ALU.mult)
+            nc.vector.tensor_tensor(out=d1[:, :, 0:15], in0=d1[:, :, 0:15], in1=rsig[:, :, 0:15], op=ALU.mult)
+            nc.vector.tensor_scalar(out=d1[:, :, 0:15], in0=d1[:, :, 0:15], scalar1=-0.5, scalar2=1.5,
+                                    op0=ALU.mult, op1=ALU.add)
+            nc.vector.tensor_tensor(out=better[:, :, 0:15], in0=s[:, :, 0:15], in1=d1[:, :, 0:15], op=ALU.mult)
+        root = sroot
         nc.vector.tensor_tensor(out=groot[:, :, 0:15], in0=root[:, :, 0:15], in1=gf[:, :, 0:15], op=ALU.mult)
-        nc.vector.tensor_tensor(out=rsig[:, :, 0:15], in0=root[:, :, 0:15], in1=root[:, :, 0:15], op=ALU.mult)
-        nc.vector.reciprocal(out=rsig[:, :, 0:15], in_=rsig[:, :, 0:15])
         nc.vector.tensor_copy(out=sa[:, :, 1:11], in_=negk[:, :, 0:10])
         nc.vector.scalar_tensor_tensor(out=sa[:, :, 11:12], in0=negk[:, :, 10:11], scalar=-1.0, in1=ca[:, :, 11:12],
                                        op0=ALU.mult, op1=ALU.mult)
@@ -113,7 +117,6 @@ def tile_kan_layer_kernel(tc, x, grid, coef, scale_base, scale_sp, mask, out):
         nc.vector.tensor_tensor(out=sb[:, :, 3:14], in0=cc[:, :, 0:11], in1=rsig[:, :, 3:14], op=ALU.mult)
         nc.vector.tensor_tensor(out=sb[:, :, 3:14], in0=sb[:, :, 3:14], in1=negl[:, :, 0:11], op=ALU.mult)
         nc.vector.tensor_scalar(out=sb[:, :, 11:14], in0=sb[:, :, 11:14], scalar1=-1.0, scalar2=None, op0=ALU.mult)
-        nc.vector.tensor_scalar(out=x_sb[:], in0=x_sb[:], scalar1=-1.0, scalar2=None, op0=ALU.mult)
 
         bas = ctx.enter_context(tc.tile_pool(name="bas", bufs=3))
         big = ctx.enter_context(tc.tile_pool(name="big", bufs=1))
@@ -146,7 +149,7 @@ def tile_kan_layer_kernel(tc, x, grid, coef, scale_base, scale_sp, mask, out):
         ready = []
 
         def turn(q):
-            tp = psum.tile([P, B], BF16, tag="tp")
+            tp = psum.tile([P, B], BF16, tag="back")
             for m in range(NM):
                 nc.tensor.transpose(out=tp[:, m * P:(m + 1) * P], in_=x_sb[:, m, q * P:(q + 1) * P], identity=ident[:])
             tps[q] = tp
@@ -158,16 +161,16 @@ def tile_kan_layer_kernel(tc, x, grid, coef, scale_base, scale_sp, mask, out):
                 base = bas.tile([P, 4, B], BF16, tag="base", bufs=1)
                 bases[c] = base
             tn = bas.tile([P, B], BF16, tag="tn", bufs=2)
-            nc.vector.tensor_scalar(out=tn[:], in0=tp[:], scalar1=negg[:, q, 14:15], scalar2=negg[:, q, 0:1],
-                                    op0=ALU.max, op1=ALU.min)
             tq = bas.tile([P, B], BF16, tag="tq", bufs=2)
-            nc.vector.tensor_scalar(out=tq[:], in0=tn[:], scalar1=-1.0, scalar2=None, op0=ALU.mult)
-            nc.scalar.activation(out=bases[c][:, tt, :], in_=tp[:], func=ACTF.Silu, scale=-1.0)
+            nc.vector.tensor_scalar(out=tq[:], in0=tp[:], scalar1=gf[:, q, 0:1], scalar2=gf[:, q, 14:15],
+                                    op0=ALU.max, op1=ALU.min)
+            nc.vector.tensor_scalar(out=tn[:], in0=tq[:], scalar1=-1.0, scalar2=None, op0=ALU.mult)
+            nc.scalar.activation(out=bases[c][:, tt, :], in_=tp[:], func=ACTF.Silu)
             tns[q] = tn
             tqs[q] = tq
 
         def square(q, r):
-            sq = bas.tile([P, B], F32, tag="sq", bufs=5)
+            sq = bas.tile([P, B], F32, tag="sq", bufs=6)
             nc.scalar.activation(out=sq[:], in_=tns[q][:], func=ACTF.Square, bias=groot[:, q, r:r + 1],
                                  scale=root[:, q, r:r + 1])
             sqs[q, r] = sq
@@ -320,20 +323,20 @@ def tile_kan_layer_kernel(tc, x, grid, coef, scale_base, scale_sp, mask, out):
                                   in_=gws[n, k][:].rearrange("p g o t -> p (g o t)"))
             wcs[n, k] = (wc, ws)
 
-        def multiply(n):
-            acc = psum.tile([P, NM, OB], F32, tag="acc", bufs=1)
-            for m in range(NM):
-                for pl in range(NPL):
-                    wc, ws = wcs[n, pl // 4]
-                    l0 = pl * B + m * P
-                    r0 = pl % 4 * OB
-                    nc.tensor.matmul_mx(out=acc[:, m, :],
-                                        lhsT=bs_codes[:, l0:l0 + P].bitcast(FP8X4),
-                                        lhsT_scale=bs_scales[:, l0:l0 + P],
-                                        rhs=wc[:, r0:r0 + OB].bitcast(FP8X4),
-                                        rhs_scale=ws[:, r0:r0 + OB],
-                                        start=(pl == 0), stop=(pl == NPL - 1))
-            accd[n] = acc
+        def multiply(n, m):
+            if m == 0:
+                acc = psum.tile([P, NM, OB], F32, tag="acc", bufs=2)
+                accd[n] = acc
+            for pl in range(NPL):
+                wc, ws = wcs[n, pl // 4]
+                l0 = pl * B + m * P
+                r0 = pl % 4 * OB
+                nc.tensor.matmul_mx(out=accd[n][:, m, :],
+                                    lhsT=bs_codes[:, l0:l0 + P].bitcast(FP8X4),
+                                    lhsT_scale=bs_scales[:, l0:l0 + P],
+                                    rhs=wc[:, r0:r0 + OB].bitcast(FP8X4),
+                                    rhs_scale=ws[:, r0:r0 + OB],
+                                    start=(pl == 0), stop=(pl == NPL - 1))
 
         def empty(n):
             c, ob = divmod(n, NOB)
@@ -342,9 +345,13 @@ def tile_kan_layer_kernel(tc, x, grid, coef, scale_base, scale_sp, mask, out):
                 nc.scalar.copy(out=accs[:, :, osl], in_=accd[n][:])
             else:
                 ot = wts.tile([P, NM, OB], F32, tag="ot", bufs=2)
-                nc.scalar.copy(out=ot[:], in_=accd[n][:])
-                nc.gpsimd.tensor_tensor(out=ot[:], in0=ot[:], in1=accs[:, :, osl], op=ALU.add)
-                nc.sync.dma_start(out=out_v[:, :, osl], in_=ot[:])
+                if n < 2 * NOB - 1:
+                    nc.scalar.copy(out=ot[:], in_=accd[n][:])
+                    nc.gpsimd.tensor_tensor(out=ot[:], in0=ot[:], in1=accs[:, :, osl], op=ALU.add)
+                    nc.gpsimd.dma_start(out=out_v[:, :, osl], in_=ot[:])
+                else:
+                    nc.vector.tensor_tensor(out=ot[:], in0=accd[n][:], in1=accs[:, :, osl], op=ALU.add)
+                    nc.sync.dma_start(out=out_v[:, :, osl], in_=ot[:])
 
         units = [(n, k) for n in range(2 * NOB) for k in range(3)]
         weight_steps = []
@@ -369,24 +376,23 @@ def tile_kan_layer_kernel(tc, x, grid, coef, scale_base, scale_sp, mask, out):
             add_unit(i)
         weight_steps.append(bind(quant, *units[-1]))
 
-        done = {"steps": 0, "multiplied": 0, "emptied": 0}
+        done = {"steps": 0, "blocks": 0, "emptied": 0}
 
-        def flush():
-            n = done["multiplied"]
-            e = done["emptied"]
-            if done["steps"] % 2:
-                if e < n:
-                    empty(e)
-                    done["emptied"] = e + 1
-            elif (n, 2) in wcs and n // NOB in ready:
-                multiply(n)
-                done["multiplied"] = n + 1
+        def flush(blocks):
+            for k in range(blocks):
+                n, m = divmod(done["blocks"], NM)
+                if (m == 1 or n == 2 * NOB) and done["emptied"] < n:
+                    empty(done["emptied"])
+                    done["emptied"] += 1
+                elif (n, 2) in wcs and n // NOB in ready:
+                    multiply(n, m)
+                    done["blocks"] += 1
 
         def run_weights(upto):
             while done["steps"] < min(upto, len(weight_steps)):
                 weight_steps[done["steps"]]()
                 done["steps"] += 1
-                flush()
+                flush(3 if 1 in ready else 2)
 
         events = [[] for i in range(15 * NQ + 9)]
         cost = [0 for i in range(15 * NQ + 9)]
@@ -404,7 +410,7 @@ def tile_kan_layer_kernel(tc, x, grid, coef, scale_base, scale_sp, mask, out):
             c, tt = divmod(q, 4)
             for r in range(NK):
                 i = 15 * q + r
-                at(i - 3, 1, square, q, r)
+                at(i - 4, 1, square, q, r)
         for q in range(NQ):
             c, tt = divmod(q, 4)
             for r in range(NK):
@@ -432,8 +438,8 @@ def tile_kan_layer_kernel(tc, x, grid, coef, scale_base, scale_sp, mask, out):
                 at(i, 0, cube, q, r)
                 at(i, (1 <= r <= 11) + (4 <= r <= 10 and r - 4 in ON_TENSOR) + (3 <= r <= 13), terms, q, r)
             if tt == 3:
-                at(15 * q - 5, 4.5, group_base, c)
-                at(15 * q - 3, 0, quantise_basis, c, G)
+                at(15 * q + 2, 4.5, group_base, c)
+                at(15 * q + 4, 0, quantise_basis, c, G)
                 at(15 * q + 23, 0, ready.append, c)
 
         load(0)
@@ -452,6 +458,4 @@ def tile_kan_layer_kernel(tc, x, grid, coef, scale_base, scale_sp, mask, out):
             first = last_event
             before += count
         run_weights(len(weight_steps))
-        while done["emptied"] < 2 * NOB:
-            done["steps"] += 1
-            flush()
+        flush(4 * NOB)

@@ -24,10 +24,23 @@ NM = B // P
 NPL = G + 1
 OB = 128
 NOB = O // OB
-ON_TENSOR = (1, 3, 5, 7, 8, 9, 10)
-ON_VECTOR = (0, 2, 4, 6)
-NWC = 18
-STEPS = ((69, 42), (120, 37), (129, 14))
+ON_VECTOR = ((0, 2, 4, 6), (0, 2, 4, 6))
+ON_TENSOR = tuple(tuple(j for j in range(G) if j not in on_vector) for on_vector in ON_VECTOR)
+BATCHES = ((1, 3, 5), (7, 8, 9, 10))
+BACK_TAGS = (("back", "acc", "acc"), ("back", "left"))
+TAG_BUFS = {"back": 1, "acc": 2, "left": 3}
+JL = 3
+TL = 1
+QL = 3
+NL = 5
+NS = 1
+NQL = 1
+BQ = 8
+NWC = 16
+VB = 6
+RAB = 5
+LTB = 2
+STEPS = ((69, 42), (120, 37), (134, 14))
 PW = NPL * B
 
 FLOPS = 2 * B * I * O * NPL
@@ -61,65 +74,86 @@ def tile_kan_layer_kernel(tc, x, grid, coef, scale_base, scale_sp, mask, out):
 
         gf = const.tile([P, NQ, 16], F32)
         negg = const.tile([P, NQ, 16], F32)
-        d1 = const.tile([P, NQ, 16], F32)
-        d2 = const.tile([P, NQ, 16], F32)
-        d3 = const.tile([P, NQ, 16], F32)
-        d4 = const.tile([P, NQ, 16], F32)
-        ca = const.tile([P, NQ, 16], F32)
-        cc = const.tile([P, NQ, 16], F32)
-        e23 = const.tile([P, NQ, 16], F32)
-        f32 = const.tile([P, NQ, 16], F32)
-        sroot = const.tile([P, NQ, 16], F32)
-        negk = const.tile([P, NQ, 16], F32)
-        negl = const.tile([P, NQ, 16], F32)
         root = const.tile([P, NQ, 16], F32)
         groot = const.tile([P, NQ, 16], F32)
-        sig = const.tile([P, NQ, 16], F32)
-        rsig = const.tile([P, NQ, 16], F32)
         sa = const.tile([P, NQ, 16], F32)
         ka = const.tile([P, NQ, 16], F32)
         sb = const.tile([P, NQ, 16], F32)
-        nc.vector.tensor_copy(out=gf[:, :, 0:NK], in_=g_bf[:, :, 0:NK])
-        nc.vector.tensor_scalar(out=negg[:, :, 0:NK], in0=gf[:, :, 0:NK], scalar1=-1.0, scalar2=None, op0=ALU.mult)
-        nc.vector.tensor_tensor(out=d1[:, :, 0:14], in0=gf[:, :, 1:15], in1=gf[:, :, 0:14], op=ALU.subtract)
-        nc.vector.tensor_tensor(out=d2[:, :, 0:13], in0=gf[:, :, 2:15], in1=gf[:, :, 0:13], op=ALU.subtract)
-        nc.vector.tensor_tensor(out=d3[:, :, 0:12], in0=gf[:, :, 3:15], in1=gf[:, :, 0:12], op=ALU.subtract)
-        nc.vector.tensor_tensor(out=d4[:, :, 0:11], in0=gf[:, :, 4:15], in1=gf[:, :, 0:11], op=ALU.subtract)
-        nc.vector.tensor_tensor(out=e23[:, :, 0:12], in0=d2[:, :, 0:12], in1=d3[:, :, 0:12], op=ALU.mult)
-        nc.vector.tensor_tensor(out=f32[:, :, 0:12], in0=d3[:, :, 0:12], in1=d2[:, :, 1:13], op=ALU.mult)
-        nc.vector.tensor_tensor(out=rsig[:, :, 0:12], in0=e23[:, :, 0:12], in1=d1[:, :, 0:12], op=ALU.mult)
-        nc.vector.scalar_tensor_tensor(out=cc[:, :, 0:12], in0=f32[:, :, 0:12], scalar=-1.0, in1=d1[:, :, 2:14],
-                                       op0=ALU.mult, op1=ALU.mult)
-        nc.vector.reciprocal(out=ca[:, :, 0:12], in_=rsig[:, :, 0:12])
-        nc.vector.tensor_scalar(out=rsig[:, :, 11:15], in0=cc[:, :, 8:12], scalar1=-1.0, scalar2=None, op0=ALU.mult)
-        nc.vector.reciprocal(out=cc[:, :, 0:12], in_=cc[:, :, 0:12])
-        nc.vector.tensor_copy(out=sig[:, :, 0:11], in_=ca[:, :, 0:11])
-        nc.vector.tensor_scalar(out=sig[:, :, 11:15], in0=cc[:, :, 8:12], scalar1=-1.0, scalar2=None, op0=ALU.mult)
-        nc.scalar.activation(out=sroot[:, :, 0:15], in_=sig[:, :, 0:15], func=ACTF.Sqrt)
-        nc.vector.scalar_tensor_tensor(out=negk[:, :, 0:11], in0=d4[:, :, 0:11], scalar=-1.0, in1=ca[:, :, 0:11],
-                                       op0=ALU.mult, op1=ALU.mult)
-        nc.vector.tensor_tensor(out=negl[:, :, 0:11], in0=d4[:, :, 0:11], in1=cc[:, :, 1:12], op=ALU.mult)
-        nc.vector.tensor_tensor(out=negk[:, :, 0:11], in0=negk[:, :, 0:11], in1=e23[:, :, 0:11], op=ALU.mult)
-        nc.vector.tensor_tensor(out=negl[:, :, 0:11], in0=negl[:, :, 0:11], in1=f32[:, :, 1:12], op=ALU.mult)
-        for s, better in ((sroot, root), (root, sroot)):
-            nc.vector.tensor_tensor(out=d1[:, :, 0:15], in0=s[:, :, 0:15], in1=s[:, :, 0:15], op=ALU.mult)
-            nc.vector.tensor_tensor(out=d1[:, :, 0:15], in0=d1[:, :, 0:15], in1=rsig[:, :, 0:15], op=ALU.mult)
-            nc.vector.tensor_scalar(out=d1[:, :, 0:15], in0=d1[:, :, 0:15], scalar1=-0.5, scalar2=1.5,
-                                    op0=ALU.mult, op1=ALU.add)
-            nc.vector.tensor_tensor(out=better[:, :, 0:15], in0=s[:, :, 0:15], in1=d1[:, :, 0:15], op=ALU.mult)
-        root = sroot
-        nc.vector.tensor_tensor(out=groot[:, :, 0:15], in0=root[:, :, 0:15], in1=gf[:, :, 0:15], op=ALU.mult)
-        nc.vector.tensor_copy(out=sa[:, :, 1:11], in_=negk[:, :, 0:10])
-        nc.vector.scalar_tensor_tensor(out=sa[:, :, 11:12], in0=negk[:, :, 10:11], scalar=-1.0, in1=ca[:, :, 11:12],
-                                       op0=ALU.mult, op1=ALU.mult)
-        nc.vector.tensor_tensor(out=sa[:, :, 11:12], in0=sa[:, :, 11:12], in1=rsig[:, :, 11:12], op=ALU.mult)
-        nc.vector.tensor_tensor(out=ka[:, :, 0:7], in0=cc[:, :, 1:8], in1=rsig[:, :, 4:11], op=ALU.mult)
-        nc.vector.tensor_tensor(out=sb[:, :, 3:14], in0=cc[:, :, 0:11], in1=rsig[:, :, 3:14], op=ALU.mult)
-        nc.vector.tensor_tensor(out=sb[:, :, 3:14], in0=sb[:, :, 3:14], in1=negl[:, :, 0:11], op=ALU.mult)
-        nc.vector.tensor_scalar(out=sb[:, :, 11:14], in0=sb[:, :, 11:14], scalar1=-1.0, scalar2=None, op0=ALU.mult)
+        def binary(out, in0, in1, op):
+            nc.vector.tensor_tensor(out=out, in0=in0, in1=in1, op=op)
 
-        bas = ctx.enter_context(tc.tile_pool(name="bas", bufs=3))
+        def triple(out, in0, scalar, in1):
+            nc.vector.scalar_tensor_tensor(out=out, in0=in0, scalar=scalar, in1=in1, op0=ALU.mult, op1=ALU.mult)
+
+        def scaled(out, in_, scalar):
+            nc.vector.tensor_scalar(out=out, in0=in_, scalar1=scalar, scalar2=None, op0=ALU.mult)
+
+        with tc.tile_pool(name="early", bufs=1) as early:
+            d1 = early.tile([P, NQ, 16], F32)
+            d2 = early.tile([P, NQ, 16], F32)
+            d3 = early.tile([P, NQ, 16], F32)
+            d4 = early.tile([P, NQ, 16], F32)
+            ca = early.tile([P, NQ, 16], F32)
+            cc = early.tile([P, NQ, 16], F32)
+            e23 = early.tile([P, NQ, 16], F32)
+            f32 = early.tile([P, NQ, 16], F32)
+            rcc = early.tile([P, NQ, 16], F32)
+            near = early.tile([P, NQ, 16], F32)
+            nearer = early.tile([P, NQ, 16], F32)
+            w = early.tile([P, NQ, 16], F32)
+            negl = early.tile([P, NQ, 16], F32)
+            sig = early.tile([P, NQ, 16], F32)
+            rsig = early.tile([P, NQ, 16], F32)
+            binary(d2[:, :, 0:13], g_bf[:, :, 2:15], g_bf[:, :, 0:13], ALU.subtract)
+            binary(d3[:, :, 0:12], g_bf[:, :, 3:15], g_bf[:, :, 0:12], ALU.subtract)
+            binary(d1[:, :, 0:14], g_bf[:, :, 1:15], g_bf[:, :, 0:14], ALU.subtract)
+            binary(d4[:, :, 0:11], g_bf[:, :, 4:15], g_bf[:, :, 0:11], ALU.subtract)
+            binary(f32[:, :, 0:12], d3[:, :, 0:12], d2[:, :, 1:13], ALU.mult)
+            binary(e23[:, :, 0:12], d2[:, :, 0:12], d3[:, :, 0:12], ALU.mult)
+            nc.vector.tensor_copy(out=gf[:, :, 0:NK], in_=g_bf[:, :, 0:NK])
+            triple(rcc[:, :, 0:12], f32[:, :, 0:12], -1.0, d1[:, :, 2:14])
+            binary(rsig[:, :, 0:12], e23[:, :, 0:12], d1[:, :, 0:12], ALU.mult)
+            scaled(negg[:, :, 0:NK], g_bf[:, :, 0:NK], -1.0)
+            nc.vector.reciprocal(out=cc[:, :, 0:12], in_=rcc[:, :, 0:12])
+            nc.vector.reciprocal(out=ca[:, :, 0:12], in_=rsig[:, :, 0:12])
+            scaled(rsig[:, :, 11:15], rcc[:, :, 8:12], -1.0)
+            scaled(sig[:, :, 11:15], cc[:, :, 8:12], -1.0)
+            nc.vector.tensor_copy(out=sig[:, :, 0:11], in_=ca[:, :, 0:11])
+            nc.scalar.activation(out=near[:, :, 0:15], in_=sig[:, :, 0:15], func=ACTF.Sqrt)
+            knots = slice(0, 15)
+
+            def square_of(s):
+                binary(w[:, :, knots], s[:, :, knots], s[:, :, knots], ALU.mult)
+
+            def ratio():
+                binary(w[:, :, knots], w[:, :, knots], rsig[:, :, knots], ALU.mult)
+
+            def factor():
+                nc.vector.tensor_scalar(out=w[:, :, knots], in0=w[:, :, knots], scalar1=-0.5, scalar2=1.5,
+                                        op0=ALU.mult, op1=ALU.add)
+
+            triple(sa[:, :, 1:12], d4[:, :, 0:11], -1.0, ca[:, :, 0:11])
+            binary(negl[:, :, 0:11], d4[:, :, 0:11], cc[:, :, 1:12], ALU.mult)
+            binary(ka[:, :, 0:7], cc[:, :, 1:8], rsig[:, :, 4:11], ALU.mult)
+            square_of(near)
+            binary(sb[:, :, 3:14], cc[:, :, 0:11], rsig[:, :, 3:14], ALU.mult)
+            ratio()
+            binary(sa[:, :, 1:12], sa[:, :, 1:12], e23[:, :, 0:11], ALU.mult)
+            factor()
+            binary(negl[:, :, 0:11], negl[:, :, 0:11], f32[:, :, 1:12], ALU.mult)
+            binary(nearer[:, :, knots], near[:, :, knots], w[:, :, knots], ALU.mult)
+            triple(sa[:, :, 11:12], sa[:, :, 11:12], -1.0, ca[:, :, 11:12])
+            square_of(nearer)
+            binary(sb[:, :, 3:14], sb[:, :, 3:14], negl[:, :, 0:11], ALU.mult)
+            ratio()
+            binary(sa[:, :, 11:12], sa[:, :, 11:12], rsig[:, :, 11:12], ALU.mult)
+            factor()
+            scaled(sb[:, :, 11:14], sb[:, :, 11:14], -1.0)
+            binary(root[:, :, knots], nearer[:, :, knots], w[:, :, knots], ALU.mult)
+            binary(groot[:, :, knots], root[:, :, knots], gf[:, :, knots], ALU.mult)
+
         big = ctx.enter_context(tc.tile_pool(name="big", bufs=1))
+        bas = ctx.enter_context(tc.tile_pool(name="bas", bufs=3))
         wts = ctx.enter_context(tc.tile_pool(name="wts", bufs=2))
 
         def bind(f, *args):
@@ -127,7 +161,9 @@ def tile_kan_layer_kernel(tc, x, grid, coef, scale_base, scale_sp, mask, out):
 
         tps = {}
         tns = {}
-        bases = {}
+        lts = {}
+        vvs = {}
+        ravs = {}
         nears = {}
         others = {}
         tqs = {}
@@ -147,6 +183,7 @@ def tile_kan_layer_kernel(tc, x, grid, coef, scale_base, scale_sp, mask, out):
         wcs = {}
         accd = {}
         ready = []
+        done = {"steps": 0, "blocks": 0, "emptied": 0, "turned": 0}
 
         def turn(q):
             tp = psum.tile([P, B], BF16, tag="back")
@@ -155,19 +192,16 @@ def tile_kan_layer_kernel(tc, x, grid, coef, scale_base, scale_sp, mask, out):
             tps[q] = tp
 
         def begin(q):
-            c, tt = divmod(q, 4)
             tp = tps[q]
-            if tt == 0:
-                base = bas.tile([P, 4, B], BF16, tag="base", bufs=1)
-                bases[c] = base
             tn = bas.tile([P, B], BF16, tag="tn", bufs=2)
             tq = bas.tile([P, B], BF16, tag="tq", bufs=2)
             nc.vector.tensor_scalar(out=tq[:], in0=tp[:], scalar1=gf[:, q, 0:1], scalar2=gf[:, q, 14:15],
                                     op0=ALU.max, op1=ALU.min)
-            nc.vector.tensor_scalar(out=tn[:], in0=tq[:], scalar1=-1.0, scalar2=None, op0=ALU.mult)
-            nc.scalar.activation(out=bases[c][:, tt, :], in_=tp[:], func=ACTF.Silu)
             tns[q] = tn
             tqs[q] = tq
+
+        def negate(q):
+            nc.vector.tensor_scalar(out=tns[q][:], in0=tqs[q][:], scalar1=-1.0, scalar2=None, op0=ALU.mult)
 
         def square(q, r):
             sq = bas.tile([P, B], F32, tag="sq", bufs=6)
@@ -176,24 +210,40 @@ def tile_kan_layer_kernel(tc, x, grid, coef, scale_base, scale_sp, mask, out):
             sqs[q, r] = sq
 
         def cube(q, r):
-            v = bas.tile([P, B], F32, tag="v", bufs=7)
+            on_vector = ON_VECTOR[q // 4]
+            if r in on_vector:
+                if r == on_vector[0]:
+                    vv = bas.tile([P, len(on_vector), B], F32, tag="vv", bufs=1)
+                    vvs[q] = vv
+                v = vvs[q][:, on_vector.index(r), :]
+            else:
+                single = bas.tile([P, B], F32, tag="v", bufs=VB)
+                v = single[:]
             t, g = (tns[q], negg) if r <= 10 else (tqs[q], gf)
-            nc.vector.scalar_tensor_tensor(out=v[:], in0=t[:], scalar=g[:, q, r:r + 1], in1=sqs[q, r][:],
+            nc.vector.scalar_tensor_tensor(out=v, in0=t[:], scalar=g[:, q, r:r + 1], in1=sqs[q, r][:],
                                            op0=ALU.subtract, op1=ALU.mult)
             vs[q, r] = v
 
         def terms(q, r):
             if 1 <= r <= 11:
-                ra = bas.tile([P, B], F32, tag="ra", bufs=6)
-                nc.scalar.activation(out=ra[:], in_=vs[q, r][:], func=ACTF.Relu, scale=sa[:, q, r:r + 1])
+                on_vector = ON_VECTOR[q // 4]
+                if r - 1 in on_vector:
+                    if r - 1 == on_vector[0]:
+                        rav = bas.tile([P, len(on_vector), B], F32, tag="rav", bufs=1)
+                        ravs[q] = rav
+                    ra = ravs[q][:, on_vector.index(r - 1), :]
+                else:
+                    single = bas.tile([P, B], F32, tag="ra", bufs=RAB)
+                    ra = single[:]
+                nc.scalar.activation(out=ra, in_=vs[q, r], func=ACTF.Relu, scale=sa[:, q, r:r + 1])
                 ras[q, r] = ra
-            if 4 <= r <= 10 and r - 4 in ON_TENSOR:
+            if 4 <= r <= 10 and r - 4 in ON_TENSOR[q // 4]:
                 qa = bas.tile([P, B], F32, tag="qa", bufs=3)
-                nc.scalar.activation(out=qa[:], in_=vs[q, r][:], func=ACTF.Copy, scale=ka[:, q, r - 4:r - 3])
+                nc.scalar.activation(out=qa[:], in_=vs[q, r], func=ACTF.Copy, scale=ka[:, q, r - 4:r - 3])
                 qas[q, r] = qa
             if 3 <= r <= 13:
                 rb = bas.tile([P, B], F32, tag="rb", bufs=5)
-                nc.scalar.activation(out=rb[:], in_=vs[q, r][:], func=ACTF.Relu, scale=sb[:, q, r:r + 1])
+                nc.scalar.activation(out=rb[:], in_=vs[q, r], func=ACTF.Relu, scale=sb[:, q, r:r + 1])
                 rbs[q, r] = rb
 
         def sums(q, j):
@@ -209,33 +259,48 @@ def tile_kan_layer_kernel(tc, x, grid, coef, scale_base, scale_sp, mask, out):
             lefts[q, j] = left
             rights[q, j] = right
 
+        def part_of_plane(q, j):
+            c, tt = divmod(q, 4)
+            if tt == 0 and j == ON_TENSOR[c][0]:
+                plane = big.tile([P, len(ON_TENSOR[c]), NM, 4 * P], BF16, tag="plane")
+                planes[c] = plane
+            return planes[c][:, ON_TENSOR[c].index(j), :, tt * P:(tt + 1) * P]
+
         def unload(q, j):
             rt = bas.tile([P, NM, P], BF16, tag="rt", bufs=2)
             nc.scalar.activation(out=rt[:], in_=rights[q, j][:], func=ACTF.Relu, scale=-1.0)
             rights[q, j] = rt
 
         def join(q, j):
-            c, tt = divmod(q, 4)
-            if tt == 0 and j == ON_TENSOR[0]:
-                plane = big.tile([P, len(ON_TENSOR), NM, 4 * P], BF16, tag="plane")
-                planes[c] = plane
-            out = planes[c][:, ON_TENSOR.index(j), :, tt * P:(tt + 1) * P]
-            nc.vector.scalar_tensor_tensor(out=out, in0=lefts[q, j][:], scalar=-1.0,
+            nc.vector.scalar_tensor_tensor(out=part_of_plane(q, j), in0=lefts[q, j][:], scalar=-1.0,
                                            in1=rights[q, j][:], op0=ALU.mult, op1=ALU.max)
 
-        def left_on_vector(q, j):
+        def unload_both(q, j, batch):
+            if j == batch[0]:
+                lt = bas.tile([P, len(batch), NM, P], BF16, tag="lt", bufs=LTB)
+                lts[q, batch] = lt
+            nc.scalar.activation(out=part_of_plane(q, j), in_=rights[q, j][:], func=ACTF.Relu, scale=-1.0)
+            nc.scalar.activation(out=lts[q, batch][:, batch.index(j), :, :], in_=lefts[q, j][:], func=ACTF.Relu, scale=-1.0)
+
+        def join_batch(q, batch):
             c, tt = divmod(q, 4)
-            if j == ON_VECTOR[0]:
-                if tt == 0:
-                    near = big.tile([P, 4, len(ON_VECTOR), B], BF16, tag="near")
-                    nears[c] = near
-                other = big.tile([P, len(ON_VECTOR), B], BF16, tag="other")
-                others[q] = other
-            nc.vector.tensor_tensor(out=nears[c][:, tt, ON_VECTOR.index(j), :], in0=vs[q, j][:], in1=ras[q, j + 1][:],
-                                    op=ALU.add)
+            j0 = ON_TENSOR[c].index(batch[0])
+            both = planes[c][:, j0:j0 + len(batch), :, tt * P:(tt + 1) * P].rearrange("p j m i -> p (j m) i")
+            nc.vector.tensor_tensor(out=both, in0=both, in1=lts[q, batch][:].rearrange("p j m i -> p (j m) i"), op=ALU.max)
+
+        def left_on_vector(q):
+            c, tt = divmod(q, 4)
+            if tt == 0:
+                near = big.tile([P, 4, len(ON_VECTOR[c]), B], BF16, tag="near")
+                nears[c] = near
+            nc.vector.tensor_tensor(out=nears[c][:, tt, :, :], in0=vvs[q][:], in1=ravs[q][:], op=ALU.add)
 
         def right_on_vector(q, j):
-            nc.vector.scalar_tensor_tensor(out=others[q][:, ON_VECTOR.index(j), :], in0=vs[q, j + 4][:],
+            on_vector = ON_VECTOR[q // 4]
+            if j == on_vector[0]:
+                other = big.tile([P, len(on_vector), B], BF16, tag="other")
+                others[q] = other
+            nc.vector.scalar_tensor_tensor(out=others[q][:, on_vector.index(j), :], in0=vs[q, j + 4],
                                            scalar=ka[:, q, j:j + 1], in1=rbs[q, j + 3][:], op0=ALU.mult, op1=ALU.add)
 
         def join_on_vector(q):
@@ -243,12 +308,17 @@ def tile_kan_layer_kernel(tc, x, grid, coef, scale_base, scale_sp, mask, out):
             both = nears[c][:, tt, :, :]
             nc.vector.tensor_tensor(out=both, in0=both, in1=others[q][:], op=ALU.min)
 
+        def back_tag(c):
+            done["turned"] += 1
+            return BACK_TAGS[c][done["turned"] % len(BACK_TAGS[c])]
+
         def turn_back(c, j, blocks):
-            back = psum.tile([P, 2, 4, P], BF16, tag="back")
+            tag = back_tag(c)
+            back = psum.tile([P, 2, 4, P], BF16, tag=tag, bufs=TAG_BUFS[tag])
             for k, m in enumerate(blocks):
                 for tt in range(4):
                     nc.tensor.transpose(out=back[:, k, tt, :],
-                                        in_=planes[c][:, ON_TENSOR.index(j), m, tt * P:(tt + 1) * P], identity=ident[:])
+                                        in_=planes[c][:, ON_TENSOR[c].index(j), m, tt * P:(tt + 1) * P], identity=ident[:])
             turned[c, j, blocks] = back
 
         def new_gb(c, j):
@@ -264,12 +334,25 @@ def tile_kan_layer_kernel(tc, x, grid, coef, scale_base, scale_sp, mask, out):
 
         def group_near(c, j):
             new_gb(c, j)
-            nc.scalar.activation(out=gbs[c, j][:], in_=nears[c][:, :, ON_VECTOR.index(j), :].rearrange("p t b -> p b t"),
+            nc.scalar.activation(out=gbs[c, j][:], in_=nears[c][:, :, ON_VECTOR[c].index(j), :].rearrange("p t b -> p b t"),
                                  func=ACTF.Relu, scale=-1.0)
 
-        def group_base(c):
-            new_gb(c, G)
-            nc.scalar.copy(out=gbs[c, G][:], in_=bases[c][:].rearrange("p t b -> p b t"))
+        def turn_x(c, blocks):
+            tag = back_tag(c)
+            back = psum.tile([P, 2, 4, P], BF16, tag=tag, bufs=TAG_BUFS[tag])
+            for k, m in enumerate(blocks):
+                for tt in range(4):
+                    i0 = (4 * c + tt) * P
+                    nc.tensor.transpose(out=back[:, k, tt, :], in_=x_sb[:, m, i0:i0 + P], identity=ident[:])
+            turned[c, G, blocks] = back
+
+        def group_base(c, blocks):
+            if blocks[0] == 0:
+                new_gb(c, G)
+            n = len(blocks)
+            out = gbs[c, G][:, blocks[0] * P:(blocks[0] + n) * P, :].rearrange("p (k b) t -> p k b t", k=n)
+            nc.scalar.activation(out=out, in_=turned[c, G, blocks][:, 0:n, :, :].rearrange("p k t b -> p k b t"),
+                                 func=ACTF.Silu)
 
         def quantise_basis(c, j):
             for b0, bn in ((0, 256), (256, 128)):
@@ -376,7 +459,6 @@ def tile_kan_layer_kernel(tc, x, grid, coef, scale_base, scale_sp, mask, out):
             add_unit(i)
         weight_steps.append(bind(quant, *units[-1]))
 
-        done = {"steps": 0, "blocks": 0, "emptied": 0}
 
         def flush(blocks):
             for k in range(blocks):
@@ -394,8 +476,8 @@ def tile_kan_layer_kernel(tc, x, grid, coef, scale_base, scale_sp, mask, out):
                 done["steps"] += 1
                 flush(3 if 1 in ready else 2)
 
-        events = [[] for i in range(15 * NQ + 9)]
-        cost = [0 for i in range(15 * NQ + 9)]
+        events = [[] for i in range(15 * NQ + 14)]
+        cost = [0 for i in range(15 * NQ + 14)]
 
         def at(i, passes, f, *args):
             i = max(i, 0)
@@ -406,6 +488,7 @@ def tile_kan_layer_kernel(tc, x, grid, coef, scale_base, scale_sp, mask, out):
             c, tt = divmod(q, 4)
             at(15 * q - 9, 0, turn, q)
             at(15 * q - 6, 0, begin, q)
+            at(15 * q - 5, 0, negate, q)
         for q in range(NQ):
             c, tt = divmod(q, 4)
             for r in range(NK):
@@ -415,32 +498,47 @@ def tile_kan_layer_kernel(tc, x, grid, coef, scale_base, scale_sp, mask, out):
             c, tt = divmod(q, 4)
             for r in range(NK):
                 i = 15 * q + r
-                if 1 <= r <= 11 and r - 1 in ON_VECTOR:
-                    at(i + 3, 0, left_on_vector, q, r - 1)
-                if r >= 4 and r - 4 in ON_VECTOR:
+                on_vector = ON_VECTOR[c]
+                if r - 1 == on_vector[-1]:
+                    at(i + 3, 0, left_on_vector, q)
+                if r >= 4 and r - 4 in on_vector:
                     at(i + 2, 0, right_on_vector, q, r - 4)
-                    if r - 4 == ON_VECTOR[-1]:
+                    if r - 4 == on_vector[-1]:
                         at(i + 4, 0, join_on_vector, q)
                         if tt == 3:
-                            for k, j in enumerate(ON_VECTOR):
-                                at(i + 5 + k, 4.5, group_near, c, j)
-                                at(i + 6 + k, 0, quantise_basis, c, j)
-                if r >= 4 and r - 4 in ON_TENSOR:
+                            for k, j in enumerate(on_vector):
+                                at(i + NL + NS * k, 4, group_near, c, j)
+                                at(i + NL + NQL + NS * k, 0, quantise_basis, c, j)
+                if r >= 4 and r - 4 in ON_TENSOR[c]:
                     j = r - 4
                     at(i + 1, 0, sums, q, j)
-                    at(i + 2, 1, unload, q, j)
-                    at(i + 4, 0, join, q, j)
-                    if tt == 3:
-                        for k, blocks in enumerate(((0, 1), (2,))):
-                            at(i + 5 + k, 0, turn_back, c, j, blocks)
-                            at(i + 5 + k, 1.4 * len(blocks), group, c, j, blocks)
-                        at(i + 7, 0, quantise_basis, c, j)
+                    if c == 0:
+                        at(i + 2, 1, unload, q, j)
+                        at(i + 4, 0, join, q, j)
+                        if tt == 3:
+                            for k, blocks in enumerate(((0, 1), (2,))):
+                                at(i + 5 + k, 0, turn_back, c, j, blocks)
+                                at(i + 5 + k, 1.4 * len(blocks), group, c, j, blocks)
+                            at(i + BQ, 0, quantise_basis, c, j)
+                    else:
+                        batch = [js for js in BATCHES if j in js][0]
+                        at(i + 2, 2, unload_both, q, j, batch)
+                        if j == batch[-1]:
+                            at(i + 2 + JL, 0, join_batch, q, batch)
+                            if tt == 3:
+                                for e, jj in enumerate(batch):
+                                    for k, blocks in enumerate(((0, 1), (2,))):
+                                        at(i + 2 + JL + TL + e + k, 0, turn_back, c, jj, blocks)
+                                        at(i + 2 + JL + TL + e + k, 1.4 * len(blocks), group, c, jj, blocks)
+                                    at(i + 2 + JL + TL + QL + e, 0, quantise_basis, c, jj)
                 at(i, 0, cube, q, r)
-                at(i, (1 <= r <= 11) + (4 <= r <= 10 and r - 4 in ON_TENSOR) + (3 <= r <= 13), terms, q, r)
+                at(i, (1 <= r <= 11) + (4 <= r <= 10 and r - 4 in ON_TENSOR[c]) + (3 <= r <= 13), terms, q, r)
             if tt == 3:
-                at(15 * q + 2, 4.5, group_base, c)
-                at(15 * q + 4, 0, quantise_basis, c, G)
-                at(15 * q + 23, 0, ready.append, c)
+                for k, blocks in enumerate(((0, 1), (2,))):
+                    at(15 * q + 1 + k, 0, turn_x, c, blocks)
+                    at(15 * q + 1 + k, 1.3 * len(blocks), group_base, c, blocks)
+                at(15 * q + 5, 0, quantise_basis, c, G)
+                at(15 * q + (23, 28)[c], 0, ready.append, c)
 
         load(0)
         load(1)

@@ -27,6 +27,7 @@ NOB = O // OB
 ON_VECTOR = ((0, 2, 4, 6), (0, 2, 4, 6))
 ON_TENSOR = tuple(tuple(j for j in range(G) if j not in on_vector) for on_vector in ON_VECTOR)
 BATCHES = ((1, 3, 5), (7, 8, 9, 10))
+XI = (False, True)
 BACK_TAGS = (("back", "acc", "acc"), ("back", "left"))
 TAG_BUFS = {"back": 1, "acc": 2, "left": 3}
 JL = 3
@@ -171,7 +172,7 @@ def tile_kan_layer_kernel(tc, x, grid, coef, scale_base, scale_sp, mask, out):
         sqs = {}
         vs = {}
         ras = {}
-        qas = {}
+        dgs = {}
         rbs = {}
         lefts = {}
         rights = {}
@@ -237,25 +238,31 @@ def tile_kan_layer_kernel(tc, x, grid, coef, scale_base, scale_sp, mask, out):
                     ra = single[:]
                 nc.scalar.activation(out=ra, in_=vs[q, r], func=ACTF.Relu, scale=sa[:, q, r:r + 1])
                 ras[q, r] = ra
-            if 4 <= r <= 10 and r - 4 in ON_TENSOR[q // 4]:
-                qa = bas.tile([P, B], F32, tag="qa", bufs=3)
-                nc.scalar.activation(out=qa[:], in_=vs[q, r], func=ACTF.Copy, scale=ka[:, q, r - 4:r - 3])
-                qas[q, r] = qa
             if 3 <= r <= 13:
                 rb = bas.tile([P, B], F32, tag="rb", bufs=5)
                 nc.scalar.activation(out=rb[:], in_=vs[q, r], func=ACTF.Relu, scale=sb[:, q, r:r + 1])
                 rbs[q, r] = rb
 
+        def diagonal(q, j):
+            dg = bas.tile([P, P], F32, tag="dg", bufs=4)
+            nc.gpsimd.tensor_scalar(out=dg[:], in0=ident_f[:], scalar1=ka[:, q, j:j + 1], scalar2=0.0,
+                                    op0=ALU.mult, op1=ALU.add)
+            dgs[q, j] = dg
+
         def sums(q, j):
             right = psum.tile([P, NM, P], F32, tag="right", bufs=2)
             left = psum.tile([P, NM, P], F32, tag="left", bufs=3)
-            right_terms = (qas[q, j + 4] if j <= 6 else vs[q, j + 4], rbs[q, j + 3])
+            right_terms = (vs[q, j + 4], rbs[q, j + 3])
             left_terms = (vs[q, j], ras[q, j + 1])
             for m in range(NM):
                 for i in range(2):
                     for out, terms in ((right, right_terms), (left, left_terms)):
-                        nc.tensor.matmul(out=out[:, m, :], lhsT=terms[i][:, m * P:(m + 1) * P], rhs=ident_f[:],
-                                         is_transpose=True, start=(i == 0), stop=(i == 1))
+                        term = terms[i][:, m * P:(m + 1) * P]
+                        if (q, j) in dgs and i == 0 and out is right:
+                            nc.tensor.matmul(out=out[:, m, :], lhsT=term, rhs=dgs[q, j][:], start=True, stop=False)
+                        else:
+                            nc.tensor.matmul(out=out[:, m, :], lhsT=term, rhs=ident_f[:], is_transpose=True,
+                                             start=(i == 0), stop=(i == 1))
             lefts[q, j] = left
             rights[q, j] = right
 
@@ -511,8 +518,10 @@ def tile_kan_layer_kernel(tc, x, grid, coef, scale_base, scale_sp, mask, out):
                                 at(i + NL + NQL + NS * k, 0, quantise_basis, c, j)
                 if r >= 4 and r - 4 in ON_TENSOR[c]:
                     j = r - 4
+                    if j <= 6:
+                        at(i - 3, 0, diagonal, q, j)
                     at(i + 1, 0, sums, q, j)
-                    if c == 0:
+                    if not XI[c]:
                         at(i + 2, 1, unload, q, j)
                         at(i + 4, 0, join, q, j)
                         if tt == 3:
@@ -532,7 +541,7 @@ def tile_kan_layer_kernel(tc, x, grid, coef, scale_base, scale_sp, mask, out):
                                         at(i + 2 + JL + TL + e + k, 1.4 * len(blocks), group, c, jj, blocks)
                                     at(i + 2 + JL + TL + QL + e, 0, quantise_basis, c, jj)
                 at(i, 0, cube, q, r)
-                at(i, (1 <= r <= 11) + (4 <= r <= 10 and r - 4 in ON_TENSOR[c]) + (3 <= r <= 13), terms, q, r)
+                at(i, (1 <= r <= 11) + (3 <= r <= 13), terms, q, r)
             if tt == 3:
                 for k, blocks in enumerate(((0, 1), (2,))):
                     at(15 * q + 1 + k, 0, turn_x, c, blocks)

@@ -38,7 +38,7 @@ NS = 1
 NQL = 1
 BQ = 8
 NWC = 16
-VB = 6
+VB = 7
 RAB = 5
 LTB = 2
 STEPS = ((69, 42), (120, 37), (134, 14))
@@ -163,6 +163,7 @@ def tile_kan_layer_kernel(tc, x, grid, coef, scale_base, scale_sp, mask, out):
         tps = {}
         tns = {}
         lts = {}
+        ots = {}
         vvs = {}
         ravs = {}
         nears = {}
@@ -184,7 +185,7 @@ def tile_kan_layer_kernel(tc, x, grid, coef, scale_base, scale_sp, mask, out):
         wcs = {}
         accd = {}
         ready = []
-        done = {"steps": 0, "blocks": 0, "emptied": 0, "turned": 0}
+        done = {"steps": 0, "blocks": 0, "emptied": 0, "finished": NOB, "turned": 0}
 
         def turn(q):
             tp = psum.tile([P, B], BF16, tag="back")
@@ -245,8 +246,7 @@ def tile_kan_layer_kernel(tc, x, grid, coef, scale_base, scale_sp, mask, out):
 
         def diagonal(q, j):
             dg = bas.tile([P, P], F32, tag="dg", bufs=4)
-            nc.gpsimd.tensor_scalar(out=dg[:], in0=ident_f[:], scalar1=ka[:, q, j:j + 1], scalar2=0.0,
-                                    op0=ALU.mult, op1=ALU.add)
+            nc.scalar.activation(out=dg[:], in_=ident_f[:], func=ACTF.Copy, scale=ka[:, q, j:j + 1])
             dgs[q, j] = dg
 
         def sums(q, j):
@@ -434,14 +434,18 @@ def tile_kan_layer_kernel(tc, x, grid, coef, scale_base, scale_sp, mask, out):
             if c == 0:
                 nc.scalar.copy(out=accs[:, :, osl], in_=accd[n][:])
             else:
-                ot = wts.tile([P, NM, OB], F32, tag="ot", bufs=2)
+                ot = wts.tile([P, NM, OB], F32, tag="ot", bufs=3)
                 if n < 2 * NOB - 1:
                     nc.scalar.copy(out=ot[:], in_=accd[n][:])
-                    nc.gpsimd.tensor_tensor(out=ot[:], in0=ot[:], in1=accs[:, :, osl], op=ALU.add)
-                    nc.gpsimd.dma_start(out=out_v[:, :, osl], in_=ot[:])
+                    ots[n] = ot
                 else:
                     nc.vector.tensor_tensor(out=ot[:], in0=accd[n][:], in1=accs[:, :, osl], op=ALU.add)
                     nc.sync.dma_start(out=out_v[:, :, osl], in_=ot[:])
+
+        def finish(n):
+            osl = slice(n % NOB * OB, (n % NOB + 1) * OB)
+            nc.vector.tensor_tensor(out=ots[n][:], in0=ots[n][:], in1=accs[:, :, osl], op=ALU.add)
+            nc.sync.dma_start(out=out_v[:, :, osl], in_=ots[n][:])
 
         units = [(n, k) for n in range(2 * NOB) for k in range(3)]
         weight_steps = []
@@ -470,6 +474,9 @@ def tile_kan_layer_kernel(tc, x, grid, coef, scale_base, scale_sp, mask, out):
         def flush(blocks):
             for k in range(blocks):
                 n, m = divmod(done["blocks"], NM)
+                if m == 0 and done["finished"] < min(n - 1, done["emptied"]):
+                    finish(done["finished"])
+                    done["finished"] += 1
                 if (m == 1 or n == 2 * NOB) and done["emptied"] < n:
                     empty(done["emptied"])
                     done["emptied"] += 1
@@ -519,7 +526,7 @@ def tile_kan_layer_kernel(tc, x, grid, coef, scale_base, scale_sp, mask, out):
                 if r >= 4 and r - 4 in ON_TENSOR[c]:
                     j = r - 4
                     if j <= 6:
-                        at(i - 3, 0, diagonal, q, j)
+                        at(i - 3, 0.5, diagonal, q, j)
                     at(i + 1, 0, sums, q, j)
                     if not XI[c]:
                         at(i + 2, 1, unload, q, j)

@@ -26,22 +26,25 @@ OB = 128
 NOB = O // OB
 ON_VECTOR = ((0, 2, 4, 6), (0, 2, 4, 6))
 ON_TENSOR = tuple(tuple(j for j in range(G) if j not in on_vector) for on_vector in ON_VECTOR)
-BATCHES = ((1, 3, 5), (7, 8, 9, 10))
-XI = (False, True)
+BATCHES = (((1, 3, 5), (7, 8, 9, 10)), ((1, 3, 5), (7, 8, 9, 10)))
+XTT = (2, 4)
+RDS = (23, 28)
 BACK_TAGS = (("back", "acc", "acc"), ("back", "left"))
 TAG_BUFS = {"back": 1, "acc": 2, "left": 3}
-JL = 3
+JLS = (3, 3)
 TL = 1
-QL = 3
-NL = 5
+QL = 2
+NL = 6
 NS = 1
 NQL = 1
 BQ = 8
-NWC = 16
+NWC = 20
 VB = 7
+OTB = 3
+PKB = 3
 RAB = 5
 LTB = 2
-STEPS = ((69, 42), (120, 37), (134, 14))
+STEPS = ((69, 46), (120, 38), (134, 14))
 PW = NPL * B
 
 FLOPS = 2 * B * I * O * NPL
@@ -68,13 +71,18 @@ def tile_kan_layer_kernel(tc, x, grid, coef, scale_base, scale_sp, mask, out):
         nc.sync.dma_start(out=g_bf[:, :, 0:NK], in_=grid.rearrange("(q p) r -> p q r", p=P))
         bs_codes = const.tile([P, PW], U32, align_bytes=64)
         bs_scales = const.tile([P, PW], U8, align_bytes=64)
-        accs = const.tile([P, NM, O], F32)
 
-        x_sb = const.tile([P, NM, I], BF16)
-        nc.sync.dma_start(out=x_sb[:], in_=x.rearrange("(m p) i -> p m i", p=P))
+        halves = ctx.enter_context(tc.tile_pool(name="halves", bufs=1))
+        x_v = x.rearrange("(m p) i -> p m i", p=P)
+        xs = {}
 
-        gf = const.tile([P, NQ, 16], F32)
-        negg = const.tile([P, NQ, 16], F32)
+        def load_x(c):
+            xt = halves.tile([P, NM, 4 * P], BF16, tag="x")
+            nc.sync.dma_start(out=xt[:], in_=x_v[:, :, c * 4 * P:(c + 1) * 4 * P])
+            xs[c] = xt
+
+        load_x(0)
+
         root = const.tile([P, NQ, 16], F32)
         groot = const.tile([P, NQ, 16], F32)
         sa = const.tile([P, NQ, 16], F32)
@@ -111,10 +119,8 @@ def tile_kan_layer_kernel(tc, x, grid, coef, scale_base, scale_sp, mask, out):
             binary(d4[:, :, 0:11], g_bf[:, :, 4:15], g_bf[:, :, 0:11], ALU.subtract)
             binary(f32[:, :, 0:12], d3[:, :, 0:12], d2[:, :, 1:13], ALU.mult)
             binary(e23[:, :, 0:12], d2[:, :, 0:12], d3[:, :, 0:12], ALU.mult)
-            nc.vector.tensor_copy(out=gf[:, :, 0:NK], in_=g_bf[:, :, 0:NK])
             triple(rcc[:, :, 0:12], f32[:, :, 0:12], -1.0, d1[:, :, 2:14])
             binary(rsig[:, :, 0:12], e23[:, :, 0:12], d1[:, :, 0:12], ALU.mult)
-            scaled(negg[:, :, 0:NK], g_bf[:, :, 0:NK], -1.0)
             nc.vector.reciprocal(out=cc[:, :, 0:12], in_=rcc[:, :, 0:12])
             nc.vector.reciprocal(out=ca[:, :, 0:12], in_=rsig[:, :, 0:12])
             scaled(rsig[:, :, 11:15], rcc[:, :, 8:12], -1.0)
@@ -151,7 +157,7 @@ def tile_kan_layer_kernel(tc, x, grid, coef, scale_base, scale_sp, mask, out):
             factor()
             scaled(sb[:, :, 11:14], sb[:, :, 11:14], -1.0)
             binary(root[:, :, knots], nearer[:, :, knots], w[:, :, knots], ALU.mult)
-            binary(groot[:, :, knots], root[:, :, knots], gf[:, :, knots], ALU.mult)
+            binary(groot[:, :, knots], root[:, :, knots], g_bf[:, :, knots], ALU.mult)
 
         big = ctx.enter_context(tc.tile_pool(name="big", bufs=1))
         bas = ctx.enter_context(tc.tile_pool(name="bas", bufs=3))
@@ -185,19 +191,21 @@ def tile_kan_layer_kernel(tc, x, grid, coef, scale_base, scale_sp, mask, out):
         wcs = {}
         accd = {}
         ready = []
-        done = {"steps": 0, "blocks": 0, "emptied": 0, "finished": NOB, "turned": 0}
+        done = {"steps": 0, "blocks": 0, "emptied": 0, "finished": 0, "turned": 0, "units": 0}
+        lasts = {}
+        parks = {}
 
         def turn(q):
             tp = psum.tile([P, B], BF16, tag="back")
             for m in range(NM):
-                nc.tensor.transpose(out=tp[:, m * P:(m + 1) * P], in_=x_sb[:, m, q * P:(q + 1) * P], identity=ident[:])
+                nc.tensor.transpose(out=tp[:, m * P:(m + 1) * P], in_=xs[q // 4][:, m, q % 4 * P:(q % 4 + 1) * P], identity=ident[:])
             tps[q] = tp
 
         def begin(q):
             tp = tps[q]
             tn = bas.tile([P, B], BF16, tag="tn", bufs=2)
             tq = bas.tile([P, B], BF16, tag="tq", bufs=2)
-            nc.vector.tensor_scalar(out=tq[:], in0=tp[:], scalar1=gf[:, q, 0:1], scalar2=gf[:, q, 14:15],
+            nc.vector.tensor_scalar(out=tq[:], in0=tp[:], scalar1=g_bf[:, q, 0:1], scalar2=g_bf[:, q, 14:15],
                                     op0=ALU.max, op1=ALU.min)
             tns[q] = tn
             tqs[q] = tq
@@ -221,9 +229,9 @@ def tile_kan_layer_kernel(tc, x, grid, coef, scale_base, scale_sp, mask, out):
             else:
                 single = bas.tile([P, B], F32, tag="v", bufs=VB)
                 v = single[:]
-            t, g = (tns[q], negg) if r <= 10 else (tqs[q], gf)
-            nc.vector.scalar_tensor_tensor(out=v, in0=t[:], scalar=g[:, q, r:r + 1], in1=sqs[q, r][:],
-                                           op0=ALU.subtract, op1=ALU.mult)
+            t, op = (tns[q], ALU.add) if r <= 10 else (tqs[q], ALU.subtract)
+            nc.vector.scalar_tensor_tensor(out=v, in0=t[:], scalar=g_bf[:, q, r:r + 1], in1=sqs[q, r][:],
+                                           op0=op, op1=ALU.mult)
             vs[q, r] = v
 
         def terms(q, r):
@@ -349,8 +357,7 @@ def tile_kan_layer_kernel(tc, x, grid, coef, scale_base, scale_sp, mask, out):
             back = psum.tile([P, 2, 4, P], BF16, tag=tag, bufs=TAG_BUFS[tag])
             for k, m in enumerate(blocks):
                 for tt in range(4):
-                    i0 = (4 * c + tt) * P
-                    nc.tensor.transpose(out=back[:, k, tt, :], in_=x_sb[:, m, i0:i0 + P], identity=ident[:])
+                    nc.tensor.transpose(out=back[:, k, tt, :], in_=xs[c][:, m, tt * P:(tt + 1) * P], identity=ident[:])
             turned[c, G, blocks] = back
 
         def group_base(c, blocks):
@@ -385,9 +392,7 @@ def tile_kan_layer_kernel(tc, x, grid, coef, scale_base, scale_sp, mask, out):
             ct, mk, sps, sbs = cts[n]
             ms = wts.tile([P, 4, OB], F32, tag="ms")
             nc.vector.tensor_tensor(out=ms[:], in0=mk[:], in1=sps[:], op=ALU.mult)
-            wbn = wts.tile([P, 4, OB], BF16, tag="wbn")
-            nc.vector.tensor_tensor(out=wbn[:], in0=mk[:], in1=sbs[:], op=ALU.mult)
-            mss[n] = (ms, wbn)
+            mss[n] = ms
 
         def new_gw(n, k):
             gw = wts.tile([P, 4, OB, 4], BF16, tag="gw", bufs=3, align_bytes=64)
@@ -396,15 +401,16 @@ def tile_kan_layer_kernel(tc, x, grid, coef, scale_base, scale_sp, mask, out):
 
         def mult(n, k):
             ng = min(4, G - 4 * k)
-            gw = gws[n, k] if (n, k) in gws else new_gw(n, k)
+            gw = new_gw(n, k)
             ct_v = cts[n][0][:].rearrange("p t (o g) -> p o t g", g=G)
-            ms_v = mss[n][0][:].rearrange("p t o -> p o t").unsqueeze(3)
+            ms_v = mss[n][:].rearrange("p t o -> p o t").unsqueeze(3)
             nc.vector.tensor_tensor(out=gw[:, 0:ng, :, :].rearrange("p g o t -> p o t g"),
                                     in0=ct_v[:, :, :, 4 * k:4 * k + ng],
                                     in1=ms_v.to_broadcast([P, OB, 4, ng]), op=ALU.mult)
-            if k == 1:
-                gw2 = new_gw(n, 2)
-                nc.scalar.copy(out=gw2[:, 3, :, :], in_=mss[n][1][:].rearrange("p t o -> p o t"))
+            if k == 2:
+                mk, sbs = cts[n][1], cts[n][3]
+                nc.vector.tensor_tensor(out=gw[:, 3, :, :], in0=mk[:].rearrange("p t o -> p o t"),
+                                        in1=sbs[:].rearrange("p t o -> p o t"), op=ALU.mult)
 
         def quant(n, k):
             wc = wts.tile([P, 4 * OB], U32, tag="wc", bufs=NWC, align_bytes=64)
@@ -429,23 +435,48 @@ def tile_kan_layer_kernel(tc, x, grid, coef, scale_base, scale_sp, mask, out):
                                     start=(pl == 0), stop=(pl == NPL - 1))
 
         def empty(n):
-            c, ob = divmod(n, NOB)
-            osl = slice(ob * OB, (ob + 1) * OB)
-            if c == 0:
-                nc.scalar.copy(out=accs[:, :, osl], in_=accd[n][:])
-            else:
-                ot = wts.tile([P, NM, OB], F32, tag="ot", bufs=3)
-                if n < 2 * NOB - 1:
-                    nc.scalar.copy(out=ot[:], in_=accd[n][:])
-                    ots[n] = ot
-                else:
-                    nc.vector.tensor_tensor(out=ot[:], in0=accd[n][:], in1=accs[:, :, osl], op=ALU.add)
-                    nc.sync.dma_start(out=out_v[:, :, osl], in_=ot[:])
+            ot = wts.tile([P, NM, OB], F32, tag="ot", bufs=OTB)
+            nc.scalar.copy(out=ot[:], in_=accd[n][:])
+            ots[n] = ot
+
+        def outputs(n):
+            return out_v[:, :, n % NOB * OB:(n % NOB + 1) * OB]
+
+        def park(n):
+            nc.sync.dma_start(out=outputs(n), in_=ots[n][:])
+
+        def fetch(n):
+            parked = wts.tile([P, NM, OB], F32, tag="parked", bufs=PKB)
+            nc.sync.dma_start(out=parked[:], in_=outputs(n))
+            parks[n] = parked
 
         def finish(n):
-            osl = slice(n % NOB * OB, (n % NOB + 1) * OB)
-            nc.vector.tensor_tensor(out=ots[n][:], in0=ots[n][:], in1=accs[:, :, osl], op=ALU.add)
-            nc.sync.dma_start(out=out_v[:, :, osl], in_=ots[n][:])
+            nc.vector.tensor_tensor(out=ots[n][:], in0=ots[n][:], in1=parks[n][:], op=ALU.add)
+            nc.sync.dma_start(out=outputs(n), in_=ots[n][:])
+
+        def multiply_last(k):
+            n = 2 * NOB - 1
+            wc, ws = wcs[n, k]
+            for m in range(NM):
+                if k == 0:
+                    last = psum.tile([P, OB], F32, tag="left", bufs=3)
+                    lasts[m] = last
+                for pl in range(4 * k, 4 * k + 4):
+                    l0 = pl * B + m * P
+                    r0 = pl % 4 * OB
+                    nc.tensor.matmul_mx(out=lasts[m][:],
+                                        lhsT=bs_codes[:, l0:l0 + P].bitcast(FP8X4),
+                                        lhsT_scale=bs_scales[:, l0:l0 + P],
+                                        rhs=wc[:, r0:r0 + OB].bitcast(FP8X4),
+                                        rhs_scale=ws[:, r0:r0 + OB],
+                                        start=(pl == 0), stop=(pl == NPL - 1))
+
+        def finish_last():
+            osl = slice((NOB - 1) * OB, NOB * OB)
+            for m in range(NM):
+                end = wts.tile([P, OB], F32, tag="end", bufs=3)
+                nc.vector.tensor_tensor(out=end[:], in0=lasts[m][:], in1=parks[2 * NOB - 1][:, m, :], op=ALU.add)
+                nc.sync.dma_start(out=out_v[:, m, osl], in_=end[:])
 
         units = [(n, k) for n in range(2 * NOB) for k in range(3)]
         weight_steps = []
@@ -474,15 +505,22 @@ def tile_kan_layer_kernel(tc, x, grid, coef, scale_base, scale_sp, mask, out):
         def flush(blocks):
             for k in range(blocks):
                 n, m = divmod(done["blocks"], NM)
-                if m == 0 and done["finished"] < min(n - 1, done["emptied"]):
-                    finish(done["finished"])
+                if m == 0 and done["finished"] < min(n - 1 + (done["units"] > 1), done["emptied"]):
+                    (park if done["finished"] < NOB else finish)(done["finished"])
                     done["finished"] += 1
-                if (m == 1 or n == 2 * NOB) and done["emptied"] < n:
+                if (m == 1 or done["units"] > 0) and done["emptied"] < n:
                     empty(done["emptied"])
                     done["emptied"] += 1
-                elif (n, 2) in wcs and n // NOB in ready:
+                elif n < 2 * NOB - 1 and (n, 2) in wcs and n // NOB in ready:
+                    if m == 0 and n >= NOB:
+                        fetch(n)
                     multiply(n, m)
                     done["blocks"] += 1
+                elif n == 2 * NOB - 1 and (n, done["units"]) in wcs:
+                    if done["units"] == 0:
+                        fetch(n)
+                    multiply_last(done["units"])
+                    done["units"] += 1
 
         def run_weights(upto):
             while done["steps"] < min(upto, len(weight_steps)):
@@ -528,7 +566,8 @@ def tile_kan_layer_kernel(tc, x, grid, coef, scale_base, scale_sp, mask, out):
                     if j <= 6:
                         at(i - 3, 0.5, diagonal, q, j)
                     at(i + 1, 0, sums, q, j)
-                    if not XI[c]:
+                    batches = [js for js in BATCHES[c] if j in js and tt < XTT[c]]
+                    if not batches:
                         at(i + 2, 1, unload, q, j)
                         at(i + 4, 0, join, q, j)
                         if tt == 3:
@@ -537,16 +576,16 @@ def tile_kan_layer_kernel(tc, x, grid, coef, scale_base, scale_sp, mask, out):
                                 at(i + 5 + k, 1.4 * len(blocks), group, c, j, blocks)
                             at(i + BQ, 0, quantise_basis, c, j)
                     else:
-                        batch = [js for js in BATCHES if j in js][0]
+                        batch = batches[0]
                         at(i + 2, 2, unload_both, q, j, batch)
                         if j == batch[-1]:
-                            at(i + 2 + JL, 0, join_batch, q, batch)
+                            at(i + 2 + JLS[c], 0, join_batch, q, batch)
                             if tt == 3:
                                 for e, jj in enumerate(batch):
                                     for k, blocks in enumerate(((0, 1), (2,))):
-                                        at(i + 2 + JL + TL + e + k, 0, turn_back, c, jj, blocks)
-                                        at(i + 2 + JL + TL + e + k, 1.4 * len(blocks), group, c, jj, blocks)
-                                    at(i + 2 + JL + TL + QL + e, 0, quantise_basis, c, jj)
+                                        at(i + 2 + JLS[c] + TL + e + k, 0, turn_back, c, jj, blocks)
+                                        at(i + 2 + JLS[c] + TL + e + k, 1.4 * len(blocks), group, c, jj, blocks)
+                                    at(i + 2 + JLS[c] + TL + QL + e, 0, quantise_basis, c, jj)
                 at(i, 0, cube, q, r)
                 at(i, (1 <= r <= 11) + (3 <= r <= 13), terms, q, r)
             if tt == 3:
@@ -554,7 +593,9 @@ def tile_kan_layer_kernel(tc, x, grid, coef, scale_base, scale_sp, mask, out):
                     at(15 * q + 1 + k, 0, turn_x, c, blocks)
                     at(15 * q + 1 + k, 1.3 * len(blocks), group_base, c, blocks)
                 at(15 * q + 5, 0, quantise_basis, c, G)
-                at(15 * q + (23, 28)[c], 0, ready.append, c)
+                if c == 0:
+                    at(15 * q + 2, 0, load_x, 1)
+                at(15 * q + RDS[c], 0, ready.append, c)
 
         load(0)
         load(1)
@@ -573,3 +614,4 @@ def tile_kan_layer_kernel(tc, x, grid, coef, scale_base, scale_sp, mask, out):
             before += count
         run_weights(len(weight_steps))
         flush(4 * NOB)
+        finish_last()

@@ -40,8 +40,15 @@ NQL = 1
 BQ = 8
 NWC = 20
 VB = 7
-OTB = 3
-PKB = 3
+OTB = 2
+PKB = 2
+SL = 4
+LL = 3
+RL = 2
+ML = 4
+GBB = 3
+SQB = 6
+FB = 2
 RAB = 5
 LTB = 2
 STEPS = ((69, 46), (120, 38), (134, 14))
@@ -97,6 +104,29 @@ def tile_kan_layer_kernel(tc, x, grid, coef, scale_base, scale_sp, mask, out):
         def scaled(out, in_, scalar):
             nc.vector.tensor_scalar(out=out, in0=in_, scalar1=scalar, scalar2=None, op0=ALU.mult)
 
+        bas = ctx.enter_context(tc.tile_pool(name="bas", bufs=3))
+        tps = {}
+        tns = {}
+        tqs = {}
+
+        def turn(q):
+            tp = psum.tile([P, B], BF16, tag="back")
+            for m in range(NM):
+                nc.tensor.transpose(out=tp[:, m * P:(m + 1) * P], in_=xs[q // 4][:, m, q % 4 * P:(q % 4 + 1) * P], identity=ident[:])
+            tps[q] = tp
+
+        def begin(q):
+            tp = tps[q]
+            tn = bas.tile([P, B], BF16, tag="tn", bufs=2)
+            tq = bas.tile([P, B], BF16, tag="tq", bufs=2)
+            nc.vector.tensor_scalar(out=tq[:], in0=tp[:], scalar1=g_bf[:, q, 0:1], scalar2=g_bf[:, q, 14:15],
+                                    op0=ALU.max, op1=ALU.min)
+            tns[q] = tn
+            tqs[q] = tq
+
+        def negate(q):
+            nc.vector.tensor_scalar(out=tns[q][:], in0=tqs[q][:], scalar1=-1.0, scalar2=None, op0=ALU.mult)
+
         with tc.tile_pool(name="early", bufs=1) as early:
             d1 = early.tile([P, NQ, 16], F32)
             d2 = early.tile([P, NQ, 16], F32)
@@ -104,6 +134,7 @@ def tile_kan_layer_kernel(tc, x, grid, coef, scale_base, scale_sp, mask, out):
             d4 = early.tile([P, NQ, 16], F32)
             ca = early.tile([P, NQ, 16], F32)
             cc = early.tile([P, NQ, 16], F32)
+            rca = early.tile([P, NQ, 16], F32)
             e23 = early.tile([P, NQ, 16], F32)
             f32 = early.tile([P, NQ, 16], F32)
             rcc = early.tile([P, NQ, 16], F32)
@@ -111,22 +142,21 @@ def tile_kan_layer_kernel(tc, x, grid, coef, scale_base, scale_sp, mask, out):
             nearer = early.tile([P, NQ, 16], F32)
             w = early.tile([P, NQ, 16], F32)
             negl = early.tile([P, NQ, 16], F32)
-            sig = early.tile([P, NQ, 16], F32)
             rsig = early.tile([P, NQ, 16], F32)
+            turn(0)
             binary(d2[:, :, 0:13], g_bf[:, :, 2:15], g_bf[:, :, 0:13], ALU.subtract)
             binary(d3[:, :, 0:12], g_bf[:, :, 3:15], g_bf[:, :, 0:12], ALU.subtract)
             binary(d1[:, :, 0:14], g_bf[:, :, 1:15], g_bf[:, :, 0:14], ALU.subtract)
-            binary(d4[:, :, 0:11], g_bf[:, :, 4:15], g_bf[:, :, 0:11], ALU.subtract)
             binary(f32[:, :, 0:12], d3[:, :, 0:12], d2[:, :, 1:13], ALU.mult)
             binary(e23[:, :, 0:12], d2[:, :, 0:12], d3[:, :, 0:12], ALU.mult)
+            binary(rsig[:, :, 11:15], f32[:, :, 8:12], d1[:, :, 10:14], ALU.mult)
+            binary(rsig[:, :, 0:11], e23[:, :, 0:11], d1[:, :, 0:11], ALU.mult)
+            nc.scalar.activation(out=near[:, :, 0:15], in_=rsig[:, :, 0:15], func=ACTF.Abs_reciprocal_sqrt)
             triple(rcc[:, :, 0:12], f32[:, :, 0:12], -1.0, d1[:, :, 2:14])
-            binary(rsig[:, :, 0:12], e23[:, :, 0:12], d1[:, :, 0:12], ALU.mult)
+            binary(rca[:, :, 0:12], e23[:, :, 0:12], d1[:, :, 0:12], ALU.mult)
+            binary(d4[:, :, 0:11], g_bf[:, :, 4:15], g_bf[:, :, 0:11], ALU.subtract)
             nc.vector.reciprocal(out=cc[:, :, 0:12], in_=rcc[:, :, 0:12])
-            nc.vector.reciprocal(out=ca[:, :, 0:12], in_=rsig[:, :, 0:12])
-            scaled(rsig[:, :, 11:15], rcc[:, :, 8:12], -1.0)
-            scaled(sig[:, :, 11:15], cc[:, :, 8:12], -1.0)
-            nc.vector.tensor_copy(out=sig[:, :, 0:11], in_=ca[:, :, 0:11])
-            nc.scalar.activation(out=near[:, :, 0:15], in_=sig[:, :, 0:15], func=ACTF.Sqrt)
+            nc.vector.reciprocal(out=ca[:, :, 0:12], in_=rca[:, :, 0:12])
             knots = slice(0, 15)
 
             def square_of(s):
@@ -139,42 +169,40 @@ def tile_kan_layer_kernel(tc, x, grid, coef, scale_base, scale_sp, mask, out):
                 nc.vector.tensor_scalar(out=w[:, :, knots], in0=w[:, :, knots], scalar1=-0.5, scalar2=1.5,
                                         op0=ALU.mult, op1=ALU.add)
 
-            triple(sa[:, :, 1:12], d4[:, :, 0:11], -1.0, ca[:, :, 0:11])
-            binary(negl[:, :, 0:11], d4[:, :, 0:11], cc[:, :, 1:12], ALU.mult)
-            binary(ka[:, :, 0:7], cc[:, :, 1:8], rsig[:, :, 4:11], ALU.mult)
             square_of(near)
+            triple(sa[:, :, 1:12], d4[:, :, 0:11], -1.0, ca[:, :, 0:11])
+            ratio()
+            binary(negl[:, :, 0:11], d4[:, :, 0:11], cc[:, :, 1:12], ALU.mult)
+            factor()
+            binary(ka[:, :, 0:7], cc[:, :, 1:8], rsig[:, :, 4:11], ALU.mult)
+            binary(nearer[:, :, knots], near[:, :, knots], w[:, :, knots], ALU.mult)
+            begin(0)
+            square_of(nearer)
             binary(sb[:, :, 3:14], cc[:, :, 0:11], rsig[:, :, 3:14], ALU.mult)
             ratio()
+            negate(0)
+            factor()
             binary(sa[:, :, 1:12], sa[:, :, 1:12], e23[:, :, 0:11], ALU.mult)
-            factor()
-            binary(negl[:, :, 0:11], negl[:, :, 0:11], f32[:, :, 1:12], ALU.mult)
-            binary(nearer[:, :, knots], near[:, :, knots], w[:, :, knots], ALU.mult)
-            triple(sa[:, :, 11:12], sa[:, :, 11:12], -1.0, ca[:, :, 11:12])
-            square_of(nearer)
-            binary(sb[:, :, 3:14], sb[:, :, 3:14], negl[:, :, 0:11], ALU.mult)
-            ratio()
-            binary(sa[:, :, 11:12], sa[:, :, 11:12], rsig[:, :, 11:12], ALU.mult)
-            factor()
-            scaled(sb[:, :, 11:14], sb[:, :, 11:14], -1.0)
             binary(root[:, :, knots], nearer[:, :, knots], w[:, :, knots], ALU.mult)
+            binary(negl[:, :, 0:11], negl[:, :, 0:11], f32[:, :, 1:12], ALU.mult)
             binary(groot[:, :, knots], root[:, :, knots], g_bf[:, :, knots], ALU.mult)
+            triple(sa[:, :, 11:12], sa[:, :, 11:12], -1.0, ca[:, :, 11:12])
+            binary(sb[:, :, 3:14], sb[:, :, 3:14], negl[:, :, 0:11], ALU.mult)
+            binary(sa[:, :, 11:12], sa[:, :, 11:12], rsig[:, :, 11:12], ALU.mult)
+            scaled(sb[:, :, 11:14], sb[:, :, 11:14], -1.0)
 
         big = ctx.enter_context(tc.tile_pool(name="big", bufs=1))
-        bas = ctx.enter_context(tc.tile_pool(name="bas", bufs=3))
         wts = ctx.enter_context(tc.tile_pool(name="wts", bufs=2))
 
         def bind(f, *args):
             return lambda: f(*args)
 
-        tps = {}
-        tns = {}
         lts = {}
         ots = {}
         vvs = {}
         ravs = {}
         nears = {}
         others = {}
-        tqs = {}
         planes = {}
         sqs = {}
         vs = {}
@@ -195,26 +223,8 @@ def tile_kan_layer_kernel(tc, x, grid, coef, scale_base, scale_sp, mask, out):
         lasts = {}
         parks = {}
 
-        def turn(q):
-            tp = psum.tile([P, B], BF16, tag="back")
-            for m in range(NM):
-                nc.tensor.transpose(out=tp[:, m * P:(m + 1) * P], in_=xs[q // 4][:, m, q % 4 * P:(q % 4 + 1) * P], identity=ident[:])
-            tps[q] = tp
-
-        def begin(q):
-            tp = tps[q]
-            tn = bas.tile([P, B], BF16, tag="tn", bufs=2)
-            tq = bas.tile([P, B], BF16, tag="tq", bufs=2)
-            nc.vector.tensor_scalar(out=tq[:], in0=tp[:], scalar1=g_bf[:, q, 0:1], scalar2=g_bf[:, q, 14:15],
-                                    op0=ALU.max, op1=ALU.min)
-            tns[q] = tn
-            tqs[q] = tq
-
-        def negate(q):
-            nc.vector.tensor_scalar(out=tns[q][:], in0=tqs[q][:], scalar1=-1.0, scalar2=None, op0=ALU.mult)
-
         def square(q, r):
-            sq = bas.tile([P, B], F32, tag="sq", bufs=6)
+            sq = bas.tile([P, B], F32, tag="sq", bufs=SQB)
             nc.scalar.activation(out=sq[:], in_=tns[q][:], func=ACTF.Square, bias=groot[:, q, r:r + 1],
                                  scale=root[:, q, r:r + 1])
             sqs[q, r] = sq
@@ -337,7 +347,7 @@ def tile_kan_layer_kernel(tc, x, grid, coef, scale_base, scale_sp, mask, out):
             turned[c, j, blocks] = back
 
         def new_gb(c, j):
-            gb = bas.tile([P, B, 4], BF16, tag="gb", bufs=3, align_bytes=64)
+            gb = bas.tile([P, B, 4], BF16, tag="gb", bufs=GBB, align_bytes=64)
             gbs[c, j] = gb
 
         def group(c, j, blocks):
@@ -526,7 +536,7 @@ def tile_kan_layer_kernel(tc, x, grid, coef, scale_base, scale_sp, mask, out):
             while done["steps"] < min(upto, len(weight_steps)):
                 weight_steps[done["steps"]]()
                 done["steps"] += 1
-                flush(3 if 1 in ready else 2)
+                flush(3 if 1 in ready else FB)
 
         events = [[] for i in range(15 * NQ + 14)]
         cost = [0 for i in range(15 * NQ + 14)]
@@ -538,25 +548,26 @@ def tile_kan_layer_kernel(tc, x, grid, coef, scale_base, scale_sp, mask, out):
 
         for q in range(NQ):
             c, tt = divmod(q, 4)
-            at(15 * q - 9, 0, turn, q)
-            at(15 * q - 6, 0, begin, q)
-            at(15 * q - 5, 0, negate, q)
+            if q > 0:
+                at(15 * q - 9, 0, turn, q)
+                at(15 * q - 6, 0, begin, q)
+                at(15 * q - 5, 0, negate, q)
         for q in range(NQ):
             c, tt = divmod(q, 4)
             for r in range(NK):
                 i = 15 * q + r
-                at(i - 4, 1, square, q, r)
+                at(i - SL, 1, square, q, r)
         for q in range(NQ):
             c, tt = divmod(q, 4)
             for r in range(NK):
                 i = 15 * q + r
                 on_vector = ON_VECTOR[c]
                 if r - 1 == on_vector[-1]:
-                    at(i + 3, 0, left_on_vector, q)
+                    at(i + LL, 0, left_on_vector, q)
                 if r >= 4 and r - 4 in on_vector:
-                    at(i + 2, 0, right_on_vector, q, r - 4)
+                    at(i + RL, 0, right_on_vector, q, r - 4)
                     if r - 4 == on_vector[-1]:
-                        at(i + 4, 0, join_on_vector, q)
+                        at(i + ML, 0, join_on_vector, q)
                         if tt == 3:
                             for k, j in enumerate(on_vector):
                                 at(i + NL + NS * k, 4, group_near, c, j)

@@ -24,34 +24,35 @@ NM = B // P
 NPL = G + 1
 OB = 128
 NOB = O // OB
-ON_VECTOR = ((0, 2, 4, 6), (0, 2, 4, 6))
+ON_VECTOR = ((3, 4, 5, 6), (3, 4, 5, 6))
 ON_TENSOR = tuple(tuple(j for j in range(G) if j not in on_vector) for on_vector in ON_VECTOR)
-BATCHES = (((1, 3, 5), (7, 8, 9, 10)), ((1, 3, 5), (7, 8, 9, 10)))
-XTT = (2, 4)
+BATCHES = (((0, 1, 2), (7, 8, 9, 10)), ((0, 1, 2), (7, 8, 9, 10)))
+XTT = (3, 4)
 RDS = (23, 28)
+RISING = (4, 5, 6, 11, 12, 13, 14)
 BACK_TAGS = (("back", "acc", "acc"), ("back", "left"))
 TAG_BUFS = {"back": 1, "acc": 2, "left": 3}
-JLS = (3, 3)
+JLS = (4, 3)
 TL = 1
-QL = 2
-NL = 6
+QL = 3
+NL = 5
 NS = 1
-NQL = 1
+NQL = 2
 BQ = 8
-NWC = 20
+NWC = 21
 VB = 7
 OTB = 2
 PKB = 2
 SL = 4
-LL = 3
-RL = 2
+LL = 4
+RL = 3
 ML = 4
-GBB = 3
+GBB = 4
 SQB = 6
 FB = 2
 RAB = 5
 LTB = 2
-STEPS = ((69, 46), (120, 38), (134, 14))
+STEPS = ((69, 48), (120, 37), (134, 13))
 PW = NPL * B
 
 FLOPS = 2 * B * I * O * NPL
@@ -95,6 +96,7 @@ def tile_kan_layer_kernel(tc, x, grid, coef, scale_base, scale_sp, mask, out):
         sa = const.tile([P, NQ, 16], F32)
         ka = const.tile([P, NQ, 16], F32)
         sb = const.tile([P, NQ, 16], F32)
+        kl = const.tile([P, NQ, 16], F32)
         def binary(out, in0, in1, op):
             nc.vector.tensor_tensor(out=out, in0=in0, in1=in1, op=op)
 
@@ -149,8 +151,9 @@ def tile_kan_layer_kernel(tc, x, grid, coef, scale_base, scale_sp, mask, out):
             binary(d1[:, :, 0:14], g_bf[:, :, 1:15], g_bf[:, :, 0:14], ALU.subtract)
             binary(f32[:, :, 0:12], d3[:, :, 0:12], d2[:, :, 1:13], ALU.mult)
             binary(e23[:, :, 0:12], d2[:, :, 0:12], d3[:, :, 0:12], ALU.mult)
-            binary(rsig[:, :, 11:15], f32[:, :, 8:12], d1[:, :, 10:14], ALU.mult)
             binary(rsig[:, :, 0:11], e23[:, :, 0:11], d1[:, :, 0:11], ALU.mult)
+            binary(rsig[:, :, 11:15], f32[:, :, 8:12], d1[:, :, 10:14], ALU.mult)
+            binary(rsig[:, :, 4:7], f32[:, :, 1:4], d1[:, :, 3:6], ALU.mult)
             nc.scalar.activation(out=near[:, :, 0:15], in_=rsig[:, :, 0:15], func=ACTF.Abs_reciprocal_sqrt)
             triple(rcc[:, :, 0:12], f32[:, :, 0:12], -1.0, d1[:, :, 2:14])
             binary(rca[:, :, 0:12], e23[:, :, 0:12], d1[:, :, 0:12], ALU.mult)
@@ -174,7 +177,8 @@ def tile_kan_layer_kernel(tc, x, grid, coef, scale_base, scale_sp, mask, out):
             ratio()
             binary(negl[:, :, 0:11], d4[:, :, 0:11], cc[:, :, 1:12], ALU.mult)
             factor()
-            binary(ka[:, :, 0:7], cc[:, :, 1:8], rsig[:, :, 4:11], ALU.mult)
+            binary(ka[:, :, 3:7], cc[:, :, 4:8], rsig[:, :, 7:11], ALU.mult)
+            triple(kl[:, :, 4:12], ca[:, :, 4:12], -1.0, rsig[:, :, 4:12])
             binary(nearer[:, :, knots], near[:, :, knots], w[:, :, knots], ALU.mult)
             begin(0)
             square_of(nearer)
@@ -186,9 +190,10 @@ def tile_kan_layer_kernel(tc, x, grid, coef, scale_base, scale_sp, mask, out):
             binary(root[:, :, knots], nearer[:, :, knots], w[:, :, knots], ALU.mult)
             binary(negl[:, :, 0:11], negl[:, :, 0:11], f32[:, :, 1:12], ALU.mult)
             binary(groot[:, :, knots], root[:, :, knots], g_bf[:, :, knots], ALU.mult)
-            triple(sa[:, :, 11:12], sa[:, :, 11:12], -1.0, ca[:, :, 11:12])
             binary(sb[:, :, 3:14], sb[:, :, 3:14], negl[:, :, 0:11], ALU.mult)
-            binary(sa[:, :, 11:12], sa[:, :, 11:12], rsig[:, :, 11:12], ALU.mult)
+            binary(sa[:, :, 4:7], sa[:, :, 4:7], kl[:, :, 4:7], ALU.mult)
+            binary(sa[:, :, 11:12], sa[:, :, 11:12], kl[:, :, 11:12], ALU.mult)
+            scaled(sb[:, :, 4:7], sb[:, :, 4:7], -1.0)
             scaled(sb[:, :, 11:14], sb[:, :, 11:14], -1.0)
 
         big = ctx.enter_context(tc.tile_pool(name="big", bufs=1))
@@ -207,7 +212,6 @@ def tile_kan_layer_kernel(tc, x, grid, coef, scale_base, scale_sp, mask, out):
         sqs = {}
         vs = {}
         ras = {}
-        dgs = {}
         rbs = {}
         lefts = {}
         rights = {}
@@ -239,7 +243,7 @@ def tile_kan_layer_kernel(tc, x, grid, coef, scale_base, scale_sp, mask, out):
             else:
                 single = bas.tile([P, B], F32, tag="v", bufs=VB)
                 v = single[:]
-            t, op = (tns[q], ALU.add) if r <= 10 else (tqs[q], ALU.subtract)
+            t, op = (tqs[q], ALU.subtract) if r in RISING else (tns[q], ALU.add)
             nc.vector.scalar_tensor_tensor(out=v, in0=t[:], scalar=g_bf[:, q, r:r + 1], in1=sqs[q, r][:],
                                            op0=op, op1=ALU.mult)
             vs[q, r] = v
@@ -262,11 +266,6 @@ def tile_kan_layer_kernel(tc, x, grid, coef, scale_base, scale_sp, mask, out):
                 nc.scalar.activation(out=rb[:], in_=vs[q, r], func=ACTF.Relu, scale=sb[:, q, r:r + 1])
                 rbs[q, r] = rb
 
-        def diagonal(q, j):
-            dg = bas.tile([P, P], F32, tag="dg", bufs=4)
-            nc.scalar.activation(out=dg[:], in_=ident_f[:], func=ACTF.Copy, scale=ka[:, q, j:j + 1])
-            dgs[q, j] = dg
-
         def sums(q, j):
             right = psum.tile([P, NM, P], F32, tag="right", bufs=2)
             left = psum.tile([P, NM, P], F32, tag="left", bufs=3)
@@ -275,12 +274,8 @@ def tile_kan_layer_kernel(tc, x, grid, coef, scale_base, scale_sp, mask, out):
             for m in range(NM):
                 for i in range(2):
                     for out, terms in ((right, right_terms), (left, left_terms)):
-                        term = terms[i][:, m * P:(m + 1) * P]
-                        if (q, j) in dgs and i == 0 and out is right:
-                            nc.tensor.matmul(out=out[:, m, :], lhsT=term, rhs=dgs[q, j][:], start=True, stop=False)
-                        else:
-                            nc.tensor.matmul(out=out[:, m, :], lhsT=term, rhs=ident_f[:], is_transpose=True,
-                                             start=(i == 0), stop=(i == 1))
+                        nc.tensor.matmul(out=out[:, m, :], lhsT=terms[i][:, m * P:(m + 1) * P], rhs=ident_f[:],
+                                         is_transpose=True, start=(i == 0), stop=(i == 1))
             lefts[q, j] = left
             rights[q, j] = right
 
@@ -313,12 +308,19 @@ def tile_kan_layer_kernel(tc, x, grid, coef, scale_base, scale_sp, mask, out):
             both = planes[c][:, j0:j0 + len(batch), :, tt * P:(tt + 1) * P].rearrange("p j m i -> p (j m) i")
             nc.vector.tensor_tensor(out=both, in0=both, in1=lts[q, batch][:].rearrange("p j m i -> p (j m) i"), op=ALU.max)
 
-        def left_on_vector(q):
+        def left_on_vector(q, j):
             c, tt = divmod(q, 4)
-            if tt == 0:
-                near = big.tile([P, 4, len(ON_VECTOR[c]), B], BF16, tag="near")
+            on_vector = ON_VECTOR[c]
+            if tt == 0 and j == on_vector[0]:
+                near = big.tile([P, 4, len(on_vector), B], BF16, tag="near")
                 nears[c] = near
-            nc.vector.tensor_tensor(out=nears[c][:, tt, :, :], in0=vvs[q][:], in1=ravs[q][:], op=ALU.add)
+            k = on_vector.index(j)
+            out = nears[c][:, tt, k, :]
+            if j in RISING:
+                nc.vector.scalar_tensor_tensor(out=out, in0=vvs[q][:, k, :], scalar=kl[:, q, j:j + 1], in1=ravs[q][:, k, :],
+                                               op0=ALU.mult, op1=ALU.add)
+            else:
+                nc.vector.tensor_tensor(out=out, in0=vvs[q][:, k, :], in1=ravs[q][:, k, :], op=ALU.add)
 
         def right_on_vector(q, j):
             on_vector = ON_VECTOR[q // 4]
@@ -562,8 +564,8 @@ def tile_kan_layer_kernel(tc, x, grid, coef, scale_base, scale_sp, mask, out):
             for r in range(NK):
                 i = 15 * q + r
                 on_vector = ON_VECTOR[c]
-                if r - 1 == on_vector[-1]:
-                    at(i + LL, 0, left_on_vector, q)
+                if r - 1 in on_vector:
+                    at(i + LL, 0, left_on_vector, q, r - 1)
                 if r >= 4 and r - 4 in on_vector:
                     at(i + RL, 0, right_on_vector, q, r - 4)
                     if r - 4 == on_vector[-1]:
@@ -574,8 +576,6 @@ def tile_kan_layer_kernel(tc, x, grid, coef, scale_base, scale_sp, mask, out):
                                 at(i + NL + NQL + NS * k, 0, quantise_basis, c, j)
                 if r >= 4 and r - 4 in ON_TENSOR[c]:
                     j = r - 4
-                    if j <= 6:
-                        at(i - 3, 0.5, diagonal, q, j)
                     at(i + 1, 0, sums, q, j)
                     batches = [js for js in BATCHES[c] if j in js and tt < XTT[c]]
                     if not batches:

from contextlib import ExitStack

import concourse.bass as bass
import concourse.mybir as mybir
import concourse.tile as tile
from concourse.masks import make_identity

F32 = mybir.dt.float32
BF16 = mybir.dt.bfloat16
U32 = mybir.dt.uint32
U8 = mybir.dt.uint8
FP8X4 = mybir.dt.float8_e4m3fn_x4
ALU = mybir.AluOpType
ACTF = mybir.ActivationFunctionType

P = 128
B = 384
I = 1024
O = 1024
G = 11
NK = 15
NQ = I // P
NM = B // P
NPL = G + 1
OB = 128
NOB = O // OB
ON_VECTOR = ((3, 4, 5, 6), (3, 4, 5, 6))
ON_TENSOR = tuple(tuple(j for j in range(G) if j not in on_vector) for on_vector in ON_VECTOR)
BATCHES = (((0, 1, 2), (7, 8, 9, 10)), ((0, 1, 2), (7, 8, 9, 10)))
XTT = (3, 4)
RDS = (23, 28)
RISING = (4, 5, 6, 11, 12, 13, 14)
BACK_TAGS = (("back", "acc", "acc"), ("back", "left"))
TAG_BUFS = {"back": 1, "acc": 2, "left": 3}
JLS = (4, 3)
TL = 1
QL = 3
NL = 5
NS = 1
NQL = 2
BQ = 8
NWC = 21
VB = 7
OTB = 2
PKB = 2
SL = 4
LL = 4
RL = 3
ML = 4
GBB = 4
SQB = 6
FB = 2
RAB = 5
LTB = 2
STEPS = ((69, 48), (120, 37), (134, 13))
PW = NPL * B

FLOPS = 2 * B * I * O * NPL


def tile_kan_layer_kernel(tc, x, grid, coef, scale_base, scale_sp, mask, out):
    nc = tc.nc
    coef_v = coef.rearrange("(q p) o g -> p q (o g)", p=P)
    mask_v = mask.rearrange("(q p) o -> p q o", p=P)
    sp_v = scale_sp.rearrange("(q p) o -> p q o", p=P)
    sb_v = scale_base.rearrange("(q p) o -> p q o", p=P)
    out_v = out.rearrange("(m p) o -> p m o", p=P)

    with ExitStack() as ctx:
        const = ctx.enter_context(tc.tile_pool(name="const", bufs=1))
        psum = ctx.enter_context(tc.psum_pool(name="psum", bufs=1))

        ident = const.tile([P, P], BF16)
        make_identity(nc, ident[:])
        ident_f = const.tile([P, P], F32)
        make_identity(nc, ident_f[:])
        ctx.enter_context(tc.manual_schedule())
        g_bf = const.tile([P, NQ, 16], BF16)
        nc.sync.dma_start(out=g_bf[:, :, 0:NK], in_=grid.rearrange("(q p) r -> p q r", p=P))
        bs_codes = const.tile([P, PW], U32, align_bytes=64)
        bs_scales = const.tile([P, PW], U8, align_bytes=64)

        halves = ctx.enter_context(tc.tile_pool(name="halves", bufs=1))
        x_v = x.rearrange("(m p) i -> p m i", p=P)
        xs = {}

        def load_x(c):
            xt = halves.tile([P, NM, 4 * P], BF16, tag="x")
            nc.sync.dma_start(out=xt[:], in_=x_v[:, :, c * 4 * P:(c + 1) * 4 * P])
            xs[c] = xt

        load_x(0)

        root = const.tile([P, NQ, 16], F32)
        groot = const.tile([P, NQ, 16], F32)
        sa = const.tile([P, NQ, 16], F32)
        ka = const.tile([P, NQ, 16], F32)
        sb = const.tile([P, NQ, 16], F32)
        kl = const.tile([P, NQ, 16], F32)
        def binary(out, in0, in1, op):
            nc.vector.tensor_tensor(out=out, in0=in0, in1=in1, op=op)

        def triple(out, in0, scalar, in1):
            nc.vector.scalar_tensor_tensor(out=out, in0=in0, scalar=scalar, in1=in1, op0=ALU.mult, op1=ALU.mult)

        def scaled(out, in_, scalar):
            nc.vector.tensor_scalar(out=out, in0=in_, scalar1=scalar, scalar2=None, op0=ALU.mult)

        bas = ctx.enter_context(tc.tile_pool(name="bas", bufs=3))
        tps = {}
        tns = {}
        tqs = {}

        def turn(q):
            tp = psum.tile([P, B], BF16, tag="back")
            for m in range(NM):
                nc.tensor.transpose(out=tp[:, m * P:(m + 1) * P], in_=xs[q // 4][:, m, q % 4 * P:(q % 4 + 1) * P], identity=ident[:])
            tps[q] = tp

        def begin(q):
            tp = tps[q]
            tn = bas.tile([P, B], BF16, tag="tn", bufs=2)
            tq = bas.tile([P, B], BF16, tag="tq", bufs=2)
            nc.vector.tensor_scalar(out=tq[:], in0=tp[:], scalar1=g_bf[:, q, 0:1], scalar2=g_bf[:, q, 14:15],
                                    op0=ALU.max, op1=ALU.min)
            tns[q] = tn
            tqs[q] = tq

        def negate(q):
            nc.vector.tensor_scalar(out=tns[q][:], in0=tqs[q][:], scalar1=-1.0, scalar2=None, op0=ALU.mult)

        with tc.tile_pool(name="early", bufs=1) as early:
            d1 = early.tile([P, NQ, 16], F32)
            d2 = early.tile([P, NQ, 16], F32)
            d3 = early.tile([P, NQ, 16], F32)
            d4 = early.tile([P, NQ, 16], F32)
            ca = early.tile([P, NQ, 16], F32)
            cc = early.tile([P, NQ, 16], F32)
            rca = early.tile([P, NQ, 16], F32)
            e23 = early.tile([P, NQ, 16], F32)
            f32 = early.tile([P, NQ, 16], F32)
            rcc = early.tile([P, NQ, 16], F32)
            near = early.tile([P, NQ, 16], F32)
            nearer = early.tile([P, NQ, 16], F32)
            w = early.tile([P, NQ, 16], F32)
            negl = early.tile([P, NQ, 16], F32)
            rsig = early.tile([P, NQ, 16], F32)
            turn(0)
            binary(d2[:, :, 0:13], g_bf[:, :, 2:15], g_bf[:, :, 0:13], ALU.subtract)
            binary(d3[:, :, 0:12], g_bf[:, :, 3:15], g_bf[:, :, 0:12], ALU.subtract)
            binary(d1[:, :, 0:14], g_bf[:, :, 1:15], g_bf[:, :, 0:14], ALU.subtract)
            binary(f32[:, :, 0:12], d3[:, :, 0:12], d2[:, :, 1:13], ALU.mult)
            binary(e23[:, :, 0:12], d2[:, :, 0:12], d3[:, :, 0:12], ALU.mult)
            binary(rsig[:, :, 0:11], e23[:, :, 0:11], d1[:, :, 0:11], ALU.mult)
            binary(rsig[:, :, 11:15], f32[:, :, 8:12], d1[:, :, 10:14], ALU.mult)
            binary(rsig[:, :, 4:7], f32[:, :, 1:4], d1[:, :, 3:6], ALU.mult)
            nc.scalar.activation(out=near[:, :, 0:15], in_=rsig[:, :, 0:15], func=ACTF.Abs_reciprocal_sqrt)
            triple(rcc[:, :, 0:12], f32[:, :, 0:12], -1.0, d1[:, :, 2:14])
            binary(rca[:, :, 0:12], e23[:, :, 0:12], d1[:, :, 0:12], ALU.mult)
            binary(d4[:, :, 0:11], g_bf[:, :, 4:15], g_bf[:, :, 0:11], ALU.subtract)
            nc.vector.reciprocal(out=cc[:, :, 0:12], in_=rcc[:, :, 0:12])
            nc.vector.reciprocal(out=ca[:, :, 0:12], in_=rca[:, :, 0:12])
            knots = slice(0, 15)

            def square_of(s):
                binary(w[:, :, knots], s[:, :, knots], s[:, :, knots], ALU.mult)

            def ratio():
                binary(w[:, :, knots], w[:, :, knots], rsig[:, :, knots], ALU.mult)

            def factor():
                nc.vector.tensor_scalar(out=w[:, :, knots], in0=w[:, :, knots], scalar1=-0.5, scalar2=1.5,
                                        op0=ALU.mult, op1=ALU.add)

            square_of(near)
            triple(sa[:, :, 1:12], d4[:, :, 0:11], -1.0, ca[:, :, 0:11])
            ratio()
            binary(negl[:, :, 0:11], d4[:, :, 0:11], cc[:, :, 1:12], ALU.mult)
            factor()
            binary(ka[:, :, 3:7], cc[:, :, 4:8], rsig[:, :, 7:11], ALU.mult)
            triple(kl[:, :, 4:12], ca[:, :, 4:12], -1.0, rsig[:, :, 4:12])
            binary(nearer[:, :, knots], near[:, :, knots], w[:, :, knots], ALU.mult)
            begin(0)
            square_of(nearer)
            binary(sb[:, :, 3:14], cc[:, :, 0:11], rsig[:, :, 3:14], ALU.mult)
            ratio()
            negate(0)
            factor()
            binary(sa[:, :, 1:12], sa[:, :, 1:12], e23[:, :, 0:11], ALU.mult)
            binary(root[:, :, knots], nearer[:, :, knots], w[:, :, knots], ALU.mult)
            binary(negl[:, :, 0:11], negl[:, :, 0:11], f32[:, :, 1:12], ALU.mult)
            binary(groot[:, :, knots], root[:, :, knots], g_bf[:, :, knots], ALU.mult)
            binary(sb[:, :, 3:14], sb[:, :, 3:14], negl[:, :, 0:11], ALU.mult)
            binary(sa[:, :, 4:7], sa[:, :, 4:7], kl[:, :, 4:7], ALU.mult)
            binary(sa[:, :, 11:12], sa[:, :, 11:12], kl[:, :, 11:12], ALU.mult)
            scaled(sb[:, :, 4:7], sb[:, :, 4:7], -1.0)
            scaled(sb[:, :, 11:14], sb[:, :, 11:14], -1.0)

        big = ctx.enter_context(tc.tile_pool(name="big", bufs=1))
        wts = ctx.enter_context(tc.tile_pool(name="wts", bufs=2))

        def bind(f, *args):
            return lambda: f(*args)

        lts = {}
        ots = {}
        vvs = {}
        ravs = {}
        nears = {}
        others = {}
        planes = {}
        sqs = {}
        vs = {}
        ras = {}
        rbs = {}
        lefts = {}
        rights = {}
        turned = {}
        gbs = {}
        cts = {}
        mss = {}
        gws = {}
        wcs = {}
        accd = {}
        ready = []
        done = {"steps": 0, "blocks": 0, "emptied": 0, "finished": 0, "turned": 0, "units": 0}
        lasts = {}
        parks = {}

        def square(q, r):
            sq = bas.tile([P, B], F32, tag="sq", bufs=SQB)
            nc.scalar.activation(out=sq[:], in_=tns[q][:], func=ACTF.Square, bias=groot[:, q, r:r + 1],
                                 scale=root[:, q, r:r + 1])
            sqs[q, r] = sq

        def cube(q, r):
            on_vector = ON_VECTOR[q // 4]
            if r in on_vector:
                if r == on_vector[0]:
                    vv = bas.tile([P, len(on_vector), B], F32, tag="vv", bufs=1)
                    vvs[q] = vv
                v = vvs[q][:, on_vector.index(r), :]
            else:
                single = bas.tile([P, B], F32, tag="v", bufs=VB)
                v = single[:]
            t, op = (tqs[q], ALU.subtract) if r in RISING else (tns[q], ALU.add)
            nc.vector.scalar_tensor_tensor(out=v, in0=t[:], scalar=g_bf[:, q, r:r + 1], in1=sqs[q, r][:],
                                           op0=op, op1=ALU.mult)
            vs[q, r] = v

        def terms(q, r):
            if 1 <= r <= 11:
                on_vector = ON_VECTOR[q // 4]
                if r - 1 in on_vector:
                    if r - 1 == on_vector[0]:
                        rav = bas.tile([P, len(on_vector), B], F32, tag="rav", bufs=1)
                        ravs[q] = rav
                    ra = ravs[q][:, on_vector.index(r - 1), :]
                else:
                    single = bas.tile([P, B], F32, tag="ra", bufs=RAB)
                    ra = single[:]
                nc.scalar.activation(out=ra, in_=vs[q, r], func=ACTF.Relu, scale=sa[:, q, r:r + 1])
                ras[q, r] = ra
            if 3 <= r <= 13:
                rb = bas.tile([P, B], F32, tag="rb", bufs=5)
                nc.scalar.activation(out=rb[:], in_=vs[q, r], func=ACTF.Relu, scale=sb[:, q, r:r + 1])
                rbs[q, r] = rb

        def sums(q, j):
            right = psum.tile([P, NM, P], F32, tag="right", bufs=2)
            left = psum.tile([P, NM, P], F32, tag="left", bufs=3)
            right_terms = (vs[q, j + 4], rbs[q, j + 3])
            left_terms = (vs[q, j], ras[q, j + 1])
            for m in range(NM):
                for i in range(2):
                    for out, terms in ((right, right_terms), (left, left_terms)):
                        nc.tensor.matmul(out=out[:, m, :], lhsT=terms[i][:, m * P:(m + 1) * P], rhs=ident_f[:],
                                         is_transpose=True, start=(i == 0), stop=(i == 1))
            lefts[q, j] = left
            rights[q, j] = right

        def part_of_plane(q, j):
            c, tt = divmod(q, 4)
            if tt == 0 and j == ON_TENSOR[c][0]:
                plane = big.tile([P, len(ON_TENSOR[c]), NM, 4 * P], BF16, tag="plane")
                planes[c] = plane
            return planes[c][:, ON_TENSOR[c].index(j), :, tt * P:(tt + 1) * P]

        def unload(q, j):
            rt = bas.tile([P, NM, P], BF16, tag="rt", bufs=2)
            nc.scalar.activation(out=rt[:], in_=rights[q, j][:], func=ACTF.Relu, scale=-1.0)
            rights[q, j] = rt

        def join(q, j):
            nc.vector.scalar_tensor_tensor(out=part_of_plane(q, j), in0=lefts[q, j][:], scalar=-1.0,
                                           in1=rights[q, j][:], op0=ALU.mult, op1=ALU.max)

        def unload_both(q, j, batch):
            if j == batch[0]:
                lt = bas.tile([P, len(batch), NM, P], BF16, tag="lt", bufs=LTB)
                lts[q, batch] = lt
            nc.scalar.activation(out=part_of_plane(q, j), in_=rights[q, j][:], func=ACTF.Relu, scale=-1.0)
            nc.scalar.activation(out=lts[q, batch][:, batch.index(j), :, :], in_=lefts[q, j][:], func=ACTF.Relu, scale=-1.0)

        def join_batch(q, batch):
            c, tt = divmod(q, 4)
            j0 = ON_TENSOR[c].index(batch[0])
            both = planes[c][:, j0:j0 + len(batch), :, tt * P:(tt + 1) * P].rearrange("p j m i -> p (j m) i")
            nc.vector.tensor_tensor(out=both, in0=both, in1=lts[q, batch][:].rearrange("p j m i -> p (j m) i"), op=ALU.max)

        def left_on_vector(q, j):
            c, tt = divmod(q, 4)
            on_vector = ON_VECTOR[c]
            if tt == 0 and j == on_vector[0]:
                near = big.tile([P, 4, len(on_vector), B], BF16, tag="near")
                nears[c] = near
            k = on_vector.index(j)
            out = nears[c][:, tt, k, :]
            if j in RISING:
                nc.vector.scalar_tensor_tensor(out=out, in0=vvs[q][:, k, :], scalar=kl[:, q, j:j + 1], in1=ravs[q][:, k, :],
                                               op0=ALU.mult, op1=ALU.add)
            else:
                nc.vector.tensor_tensor(out=out, in0=vvs[q][:, k, :], in1=ravs[q][:, k, :], op=ALU.add)

        def right_on_vector(q, j):
            on_vector = ON_VECTOR[q // 4]
            if j == on_vector[0]:
                other = big.tile([P, len(on_vector), B], BF16, tag="other")
                others[q] = other
            nc.vector.scalar_tensor_tensor(out=others[q][:, on_vector.index(j), :], in0=vs[q, j + 4],
                                           scalar=ka[:, q, j:j + 1], in1=rbs[q, j + 3][:], op0=ALU.mult, op1=ALU.add)

        def join_on_vector(q):
            c, tt = divmod(q, 4)
            both = nears[c][:, tt, :, :]
            nc.vector.tensor_tensor(out=both, in0=both, in1=others[q][:], op=ALU.min)

        def back_tag(c):
            done["turned"] += 1
            return BACK_TAGS[c][done["turned"] % len(BACK_TAGS[c])]

        def turn_back(c, j, blocks):
            tag = back_tag(c)
            back = psum.tile([P, 2, 4, P], BF16, tag=tag, bufs=TAG_BUFS[tag])
            for k, m in enumerate(blocks):
                for tt in range(4):
                    nc.tensor.transpose(out=back[:, k, tt, :],
                                        in_=planes[c][:, ON_TENSOR[c].index(j), m, tt * P:(tt + 1) * P], identity=ident[:])
            turned[c, j, blocks] = back

        def new_gb(c, j):
            gb = bas.tile([P, B, 4], BF16, tag="gb", bufs=GBB, align_bytes=64)
            gbs[c, j] = gb

        def group(c, j, blocks):
            if blocks[0] == 0:
                new_gb(c, j)
            n = len(blocks)
            out = gbs[c, j][:, blocks[0] * P:(blocks[0] + n) * P, :].rearrange("p (k b) t -> p k b t", k=n)
            nc.scalar.copy(out=out, in_=turned[c, j, blocks][:, 0:n, :, :].rearrange("p k t b -> p k b t"))

        def group_near(c, j):
            new_gb(c, j)
            nc.scalar.activation(out=gbs[c, j][:], in_=nears[c][:, :, ON_VECTOR[c].index(j), :].rearrange("p t b -> p b t"),
                                 func=ACTF.Relu, scale=-1.0)

        def turn_x(c, blocks):
            tag = back_tag(c)
            back = psum.tile([P, 2, 4, P], BF16, tag=tag, bufs=TAG_BUFS[tag])
            for k, m in enumerate(blocks):
                for tt in range(4):
                    nc.tensor.transpose(out=back[:, k, tt, :], in_=xs[c][:, m, tt * P:(tt + 1) * P], identity=ident[:])
            turned[c, G, blocks] = back

        def group_base(c, blocks):
            if blocks[0] == 0:
                new_gb(c, G)
            n = len(blocks)
            out = gbs[c, G][:, blocks[0] * P:(blocks[0] + n) * P, :].rearrange("p (k b) t -> p k b t", k=n)
            nc.scalar.activation(out=out, in_=turned[c, G, blocks][:, 0:n, :, :].rearrange("p k t b -> p k b t"),
                                 func=ACTF.Silu)

        def quantise_basis(c, j):
            for b0, bn in ((0, 256), (256, 128)):
                w0 = j * B + b0
                nc.vector.quantize_mx(out=bs_codes[:, w0:w0 + bn].bitcast(FP8X4), scales=bs_scales[:, w0:w0 + bn],
                                      in_=gbs[c, j][:, b0:b0 + bn, :].rearrange("p b t -> p (b t)"))

        def load(n):
            c, ob = divmod(n, NOB)
            qsl = slice(4 * c, 4 * c + 4)
            osl = slice(ob * OB, (ob + 1) * OB)
            mk = wts.tile([P, 4, OB], BF16, tag="mk")
            nc.sync.dma_start(out=mk[:], in_=mask_v[:, qsl, osl])
            sps = wts.tile([P, 4, OB], BF16, tag="sps")
            nc.sync.dma_start(out=sps[:], in_=sp_v[:, qsl, osl])
            sbs = wts.tile([P, 4, OB], BF16, tag="sbs")
            nc.sync.dma_start(out=sbs[:], in_=sb_v[:, qsl, osl])
            ct = wts.tile([P, 4, OB * G], BF16, tag="ct", bufs=2)
            nc.sync.dma_start(out=ct[:], in_=coef_v[:, qsl, ob * OB * G:(ob + 1) * OB * G])
            cts[n] = (ct, mk, sps, sbs)

        def prep(n):
            ct, mk, sps, sbs = cts[n]
            ms = wts.tile([P, 4, OB], F32, tag="ms")
            nc.vector.tensor_tensor(out=ms[:], in0=mk[:], in1=sps[:], op=ALU.mult)
            mss[n] = ms

        def new_gw(n, k):
            gw = wts.tile([P, 4, OB, 4], BF16, tag="gw", bufs=3, align_bytes=64)
            gws[n, k] = gw
            return gw

        def mult(n, k):
            ng = min(4, G - 4 * k)
            gw = new_gw(n, k)
            ct_v = cts[n][0][:].rearrange("p t (o g) -> p o t g", g=G)
            ms_v = mss[n][:].rearrange("p t o -> p o t").unsqueeze(3)
            nc.vector.tensor_tensor(out=gw[:, 0:ng, :, :].rearrange("p g o t -> p o t g"),
                                    in0=ct_v[:, :, :, 4 * k:4 * k + ng],
                                    in1=ms_v.to_broadcast([P, OB, 4, ng]), op=ALU.mult)
            if k == 2:
                mk, sbs = cts[n][1], cts[n][3]
                nc.vector.tensor_tensor(out=gw[:, 3, :, :], in0=mk[:].rearrange("p t o -> p o t"),
                                        in1=sbs[:].rearrange("p t o -> p o t"), op=ALU.mult)

        def quant(n, k):
            wc = wts.tile([P, 4 * OB], U32, tag="wc", bufs=NWC, align_bytes=64)
            ws = wts.tile([P, 4 * OB], U8, tag="ws", bufs=NWC, align_bytes=64)
            nc.vector.quantize_mx(out=wc[:].bitcast(FP8X4), scales=ws[:],
                                  in_=gws[n, k][:].rearrange("p g o t -> p (g o t)"))
            wcs[n, k] = (wc, ws)

        def multiply(n, m):
            if m == 0:
                acc = psum.tile([P, NM, OB], F32, tag="acc", bufs=2)
                accd[n] = acc
            for pl in range(NPL):
                wc, ws = wcs[n, pl // 4]
                l0 = pl * B + m * P
                r0 = pl % 4 * OB
                nc.tensor.matmul_mx(out=accd[n][:, m, :],
                                    lhsT=bs_codes[:, l0:l0 + P].bitcast(FP8X4),
                                    lhsT_scale=bs_scales[:, l0:l0 + P],
                                    rhs=wc[:, r0:r0 + OB].bitcast(FP8X4),
                                    rhs_scale=ws[:, r0:r0 + OB],
                                    start=(pl == 0), stop=(pl == NPL - 1))

        def empty(n):
            ot = wts.tile([P, NM, OB], F32, tag="ot", bufs=OTB)
            nc.scalar.copy(out=ot[:], in_=accd[n][:])
            ots[n] = ot

        def outputs(n):
            return out_v[:, :, n % NOB * OB:(n % NOB + 1) * OB]

        def park(n):
            nc.sync.dma_start(out=outputs(n), in_=ots[n][:])

        def fetch(n):
            parked = wts.tile([P, NM, OB], F32, tag="parked", bufs=PKB)
            nc.sync.dma_start(out=parked[:], in_=outputs(n))
            parks[n] = parked

        def finish(n):
            nc.vector.tensor_tensor(out=ots[n][:], in0=ots[n][:], in1=parks[n][:], op=ALU.add)
            nc.sync.dma_start(out=outputs(n), in_=ots[n][:])

        def multiply_last(k):
            n = 2 * NOB - 1
            wc, ws = wcs[n, k]
            for m in range(NM):
                if k == 0:
                    last = psum.tile([P, OB], F32, tag="left", bufs=3)
                    lasts[m] = last
                for pl in range(4 * k, 4 * k + 4):
                    l0 = pl * B + m * P
                    r0 = pl % 4 * OB
                    nc.tensor.matmul_mx(out=lasts[m][:],
                                        lhsT=bs_codes[:, l0:l0 + P].bitcast(FP8X4),
                                        lhsT_scale=bs_scales[:, l0:l0 + P],
                                        rhs=wc[:, r0:r0 + OB].bitcast(FP8X4),
                                        rhs_scale=ws[:, r0:r0 + OB],
                                        start=(pl == 0), stop=(pl == NPL - 1))

        def finish_last():
            osl = slice((NOB - 1) * OB, NOB * OB)
            for m in range(NM):
                end = wts.tile([P, OB], F32, tag="end", bufs=3)
                nc.vector.tensor_tensor(out=end[:], in0=lasts[m][:], in1=parks[2 * NOB - 1][:, m, :], op=ALU.add)
                nc.sync.dma_start(out=out_v[:, m, osl], in_=end[:])

        units = [(n, k) for n in range(2 * NOB) for k in range(3)]
        weight_steps = []

        def add_unit(i):
            n, k = units[i]

            def first():
                mult(n, k)
                if k == 2 and n + 2 < 2 * NOB:
                    load(n + 2)

            def second():
                if i > 0:
                    quant(*units[i - 1])

            weight_steps.extend([first, second])
            if k == 1 and n + 1 < 2 * NOB:
                weight_steps.append(bind(prep, n + 1))

        for i in range(len(units)):
            add_unit(i)
        weight_steps.append(bind(quant, *units[-1]))


        def flush(blocks):
            for k in range(blocks):
                n, m = divmod(done["blocks"], NM)
                if m == 0 and done["finished"] < min(n - 1 + (done["units"] > 1), done["emptied"]):
                    (park if done["finished"] < NOB else finish)(done["finished"])
                    done["finished"] += 1
                if (m == 1 or done["units"] > 0) and done["emptied"] < n:
                    empty(done["emptied"])
                    done["emptied"] += 1
                elif n < 2 * NOB - 1 and (n, 2) in wcs and n // NOB in ready:
                    if m == 0 and n >= NOB:
                        fetch(n)
                    multiply(n, m)
                    done["blocks"] += 1
                elif n == 2 * NOB - 1 and (n, done["units"]) in wcs:
                    if done["units"] == 0:
                        fetch(n)
                    multiply_last(done["units"])
                    done["units"] += 1

        def run_weights(upto):
            while done["steps"] < min(upto, len(weight_steps)):
                weight_steps[done["steps"]]()
                done["steps"] += 1
                flush(3 if 1 in ready else FB)

        events = [[] for i in range(15 * NQ + 14)]
        cost = [0 for i in range(15 * NQ + 14)]

        def at(i, passes, f, *args):
            i = max(i, 0)
            events[i].append(bind(f, *args))
            cost[i] += passes

        for q in range(NQ):
            c, tt = divmod(q, 4)
            if q > 0:
                at(15 * q - 9, 0, turn, q)
                at(15 * q - 6, 0, begin, q)
                at(15 * q - 5, 0, negate, q)
        for q in range(NQ):
            c, tt = divmod(q, 4)
            for r in range(NK):
                i = 15 * q + r
                at(i - SL, 1, square, q, r)
        for q in range(NQ):
            c, tt = divmod(q, 4)
            for r in range(NK):
                i = 15 * q + r
                on_vector = ON_VECTOR[c]
                if r - 1 in on_vector:
                    at(i + LL, 0, left_on_vector, q, r - 1)
                if r >= 4 and r - 4 in on_vector:
                    at(i + RL, 0, right_on_vector, q, r - 4)
                    if r - 4 == on_vector[-1]:
                        at(i + ML, 0, join_on_vector, q)
                        if tt == 3:
                            for k, j in enumerate(on_vector):
                                at(i + NL + NS * k, 4, group_near, c, j)
                                at(i + NL + NQL + NS * k, 0, quantise_basis, c, j)
                if r >= 4 and r - 4 in ON_TENSOR[c]:
                    j = r - 4
                    at(i + 1, 0, sums, q, j)
                    batches = [js for js in BATCHES[c] if j in js and tt < XTT[c]]
                    if not batches:
                        at(i + 2, 1, unload, q, j)
                        at(i + 4, 0, join, q, j)
                        if tt == 3:
                            for k, blocks in enumerate(((0, 1), (2,))):
                                at(i + 5 + k, 0, turn_back, c, j, blocks)
                                at(i + 5 + k, 1.4 * len(blocks), group, c, j, blocks)
                            at(i + BQ, 0, quantise_basis, c, j)
                    else:
                        batch = batches[0]
                        at(i + 2, 2, unload_both, q, j, batch)
                        if j == batch[-1]:
                            at(i + 2 + JLS[c], 0, join_batch, q, batch)
                            if tt == 3:
                                for e, jj in enumerate(batch):
                                    for k, blocks in enumerate(((0, 1), (2,))):
                                        at(i + 2 + JLS[c] + TL + e + k, 0, turn_back, c, jj, blocks)
                                        at(i + 2 + JLS[c] + TL + e + k, 1.4 * len(blocks), group, c, jj, blocks)
                                    at(i + 2 + JLS[c] + TL + QL + e, 0, quantise_basis, c, jj)
                at(i, 0, cube, q, r)
                at(i, (1 <= r <= 11) + (3 <= r <= 13), terms, q, r)
            if tt == 3:
                for k, blocks in enumerate(((0, 1), (2,))):
                    at(15 * q + 1 + k, 0, turn_x, c, blocks)
                    at(15 * q + 1 + k, 1.3 * len(blocks), group_base, c, blocks)
                at(15 * q + 5, 0, quantise_basis, c, G)
                if c == 0:
                    at(15 * q + 2, 0, load_x, 1)
                at(15 * q + RDS[c], 0, ready.append, c)

        load(0)
        load(1)
        prep(0)
        first = 0
        before = 0
        for last_event, count in STEPS:
            whole = sum(cost[first:last_event])
            spent = 0
            for i in range(first, last_event):
                for f in events[i]:
                    f()
                spent += cost[i]
                run_weights(before + count * spent // whole)
            first = last_event
            before += count
        run_weights(len(weight_steps))
        flush(4 * NOB)
        finish_last()
